import numpy as np
import ml_dtypes


def mxq(x, axis, fmt="e4m3"):
    dtype, down = {"e4m3": (ml_dtypes.float8_e4m3fn, 7), "e5m2": (ml_dtypes.float8_e5m2, 14)}[fmt]
    v = np.moveaxis(np.asarray(x, np.float32).astype(ml_dtypes.bfloat16).astype(np.float64), axis, -1)
    blocks = v.reshape(v.shape[:-1] + (-1, 32))
    amax = np.abs(blocks).max(-1, keepdims=True)
    byte = np.maximum(np.where(amax > 0, np.frexp(amax)[1] - 1 + 127, 0) - down, 1)
    scale = np.exp2(byte - 127.0)
    codes = (blocks / scale).astype(np.float32).astype(dtype).astype(np.float64)
    return np.moveaxis((codes * scale).reshape(v.shape), -1, axis)


WIDE = False


def mx_kscale(k):
    if not WIDE:
        return np.ones(k)
    levels = np.array([10, -10, 5, -5, 0])
    a = np.random.permutation(np.resize(levels, k // 512 * 4)).reshape(k // 512, 4)
    idx = np.arange(k)
    return np.exp2(a[idx // 512, idx % 128 // 32])


BF16 = ml_dtypes.bfloat16


def bf(x):
    return np.asarray(x, np.float32).astype(BF16)


def f64(x):
    return np.asarray(x).astype(np.float64)


B, L0, W0, R, DIM, OUT = 128, 16, 8, 32, 2048, 512
K1 = L0 * W0
KR = R * R
EPS = 1e-5


def setup_inputs():
    s2, s3 = mx_kscale(KR), mx_kscale(KR)
    rn = np.random.standard_normal
    return {
        "x": bf(rn((B, L0, W0))),
        "km1": bf(rn((L0, W0, DIM)) / np.sqrt(K1)),
        "b1": bf(0.5 + 0.3 * rn(DIM)),
        "t2": bf(rn((B, R, R)) * s2.reshape(R, R)),
        "core2": bf(rn((R, R, DIM)) / np.sqrt(KR) / s2.reshape(R, R, 1)),
        "t3": bf(rn((B, R, R)) * s3.reshape(R, R)),
        "core3": bf(rn((R, R, DIM)) / np.sqrt(KR) / s3.reshape(R, R, 1)),
        "ln_g": bf(1.0 + 0.1 * rn(DIM)),
        "ln_b": bf(0.1 * rn(DIM)),
        "fc_w": bf(rn((OUT, DIM)) / np.sqrt(DIM)),
        "fc_b": bf(0.3 * rn(OUT)),
    }


def reference(x, km1, b1, t2, core2, t3, core3, ln_g, ln_b, fc_w, fc_b):
    o = f64(x).reshape(B, K1) @ f64(km1).reshape(K1, DIM) + f64(b1)
    o = o + (mxq(f64(t2).reshape(B, KR), 1, "e4m3") @ mxq(f64(core2).reshape(KR, DIM), 0, "e4m3"))
    o = o + (mxq(f64(t3).reshape(B, KR), 1, "e4m3") @ mxq(f64(core3).reshape(KR, DIM), 0, "e4m3"))
    mu = o.mean(-1, keepdims=True)
    var = ((o - mu) ** 2).mean(-1, keepdims=True)
    y = (o - mu) / np.sqrt(var + EPS) * f64(ln_g) + f64(ln_b)
    out = (mxq(y, 1, "e4m3") @ mxq(f64(fc_w), 1, "e4m3").T) + f64(fc_b)
    return out[:, None, :]

@@ -1,0 +1,281 @@
+from contextlib import ExitStack
+
+import concourse.mybir as mybir
+from concourse.masks import make_identity
+
+F32 = mybir.dt.float32
+BF16 = mybir.dt.bfloat16
+U32 = mybir.dt.uint32
+U8 = mybir.dt.uint8
+FP8X4 = mybir.dt.float8_e4m3fn_x4
+ALU = mybir.AluOpType
+ACT = mybir.ActivationFunctionType
+
+P = 128
+D = 2048
+KR = 1024
+OUT = 512
+NB = 512
+EPS = 1e-5
+V_COLS = 240
+
+FLOPS = 2 * 128 * 2048 * (128 + 1024 + 1024) + 2 * 128 * 512 * 2048
+
+
+def tile_pinmodel_pa_kernel(tc, x, km1, b1, t2, core2, t3, core3, ln_g, ln_b, fc_w, fc_b, out):
+    nc = tc.nc
+    with ExitStack() as ctx:
+        const = ctx.enter_context(tc.tile_pool(name="const", bufs=1))
+        raw = ctx.enter_context(tc.tile_pool(name="raw", bufs=1))
+        keep = ctx.enter_context(tc.tile_pool(name="keep", bufs=1))
+        gpool = ctx.enter_context(tc.tile_pool(name="gpool", bufs=4))
+        wgpool = ctx.enter_context(tc.tile_pool(name="wgpool", bufs=2))
+        opool = ctx.enter_context(tc.psum_pool(name="opool", bufs=1))
+        wpool = ctx.enter_context(tc.psum_pool(name="wpool", bufs=4))
+
+        eps = const.tile([P, 1], F32, name="eps")
+        nc.vector.memset(eps[:], EPS)
+        warm = const.tile([P, 1], F32, name="warm")
+        nc.scalar.activation(out=warm[:], in_=eps[:], func=ACT.Sqrt)
+        vecs = const.tile([P, P], F32, name="vecs")
+        nc.vector.memset(vecs[:], 0.0)
+        e0 = const.tile([P, P], BF16, name="e0")
+        nc.vector.memset(e0[:], 0.0)
+        nc.vector.memset(e0[0:1, :], 1.0)
+        b1z = const.tile([P, D], BF16, name="b1z")
+        nc.vector.memset(b1z[:], 0.0)
+        ident_f = const.tile([P, P], F32, name="ident_f")
+        make_identity(nc, ident_f[:])
+        ident_b = const.tile([P, P], BF16, name="ident_b")
+        make_identity(nc, ident_b[:])
+
+        nc.scalar.dma_start(out=vecs[0:8, :].bitcast(BF16), in_=ln_g.rearrange("(r c) -> r c", c=256))
+        nc.scalar.dma_start(out=vecs[8:16, :].bitcast(BF16), in_=ln_b.rearrange("(r c) -> r c", c=256))
+        nc.scalar.dma_start(out=vecs[16:18, :].bitcast(BF16), in_=fc_b.rearrange("(r c) -> r c", c=256))
+        nc.scalar.dma_start(out=b1z[0:1, :], in_=b1.rearrange("(o d) -> o d", o=1))
+
+        t_sb = [raw.tile([P, KR], BF16, name="t_sb%d" % i) for i in range(2)]
+        r_sb = [[raw.tile([P, 4, D], BF16, name="r_sb%d%d" % (i, c)) for c in range(2)] for i in range(2)]
+        x_sb = raw.tile([P, P], BF16, name="x_sb")
+        km_sb = raw.tile([P, D], BF16, name="km_sb")
+        fw_sb = [raw.tile([P, D], BF16, name="fw_sb%d" % r) for r in range(4)]
+        cores = [core2.rearrange("r q d -> (r q) d"), core3.rearrange("r q d -> (r q) d")]
+
+        def load_core(i, c, d0, d1):
+            nc.sync.dma_start(
+                out=r_sb[i][c][:, :, d0:d1],
+                in_=cores[i][512 * c : 512 * c + 512, d0:d1].rearrange("(p j) d -> p j d", j=4),
+            )
+
+        nc.sync.dma_start(out=t_sb[0][:], in_=t2.rearrange("b r q -> b (r q)"))
+        load_core(0, 0, 0, 512)
+        load_core(0, 0, 512, 1024)
+        load_core(0, 0, 1024, 2048)
+        load_core(0, 1, 0, 2048)
+        nc.sync.dma_start(out=t_sb[1][:], in_=t3.rearrange("b r q -> b (r q)"))
+        nc.sync.dma_start(out=x_sb[:], in_=x.rearrange("b i j -> b (i j)"))
+        nc.sync.dma_start(out=km_sb[:], in_=km1.rearrange("i j d -> (i j) d"))
+        load_core(1, 0, 0, 2048)
+        load_core(1, 1, 0, 1024)
+        load_core(1, 1, 1024, 1536)
+        load_core(1, 1, 1536, 2048)
+        for r in range(4):
+            nc.sync.dma_start(out=fw_sb[r][:], in_=fc_w[128 * r : 128 * r + 128, :])
+
+        t_codes = []
+        t_scales = []
+
+        def prep_t(i):
+            tw = t_sb[i][:].bitcast(F32)
+            tps = wpool.tile([P, 2, 2, P], F32, tag="w", name="tps%d" % i)
+            for c in range(2):
+                for u in range(2):
+                    nc.tensor.transpose(tps[:, c, u, :], tw[:, 256 * c + u : 256 * c + 256 : 2], ident_f[:])
+            tg = keep.tile([P, 2, P, 2], F32, name="tg%d" % i, align_bytes=64)
+            nc.scalar.copy(out=tg[:], in_=tps[:].rearrange("p c u b -> p c b u"))
+            tc_w = keep.tile([P, 256], U32, name="tc_w%d" % i, align_bytes=64)
+            tc_s = keep.tile([P, 256], U8, name="tc_s%d" % i, align_bytes=64)
+            nc.vector.quantize_mx(
+                out=tc_w[:].bitcast(FP8X4),
+                scales=tc_s[:],
+                in_=tg[:].rearrange("p c b u -> p (c b u)").bitcast(BF16),
+            )
+            t_codes.append(tc_w)
+            t_scales.append(tc_s)
+
+        o_ps = [opool.tile([P, NB], F32, name="o_ps%d" % n, tag="o%d" % n) for n in range(4)]
+
+        def regroup(i, c, n):
+            g_t = gpool.tile([P, NB, 4], BF16, tag="G", name="g_t%d%d%d" % (i, c, n), align_bytes=64)
+            d0 = NB * n
+            nc.vector.tensor_copy(
+                out=g_t[:, 0:V_COLS, :].rearrange("p (c i) t -> p c t i", i=4),
+                in_=r_sb[i][c][:, :, d0 : d0 + V_COLS].rearrange("p t (c i) -> p c t i", i=4),
+            )
+            nc.scalar.copy(
+                out=g_t[:, V_COLS:NB, :].rearrange("p (c i) t -> p c t i", i=4),
+                in_=r_sb[i][c][:, :, d0 + V_COLS : d0 + NB].rearrange("p t (c i) -> p c t i", i=4),
+            )
+            return g_t
+
+        def quant_mm(i, c, n, g_t):
+            cw = keep.tile([P, NB], U32, name="cw%d%d%d" % (i, c, n), align_bytes=64)
+            cs = keep.tile([P, NB], U8, name="cs%d%d%d" % (i, c, n), align_bytes=64)
+            nc.vector.quantize_mx(out=cw[:].bitcast(FP8X4), scales=cs[:], in_=g_t[:].rearrange("p w j -> p (w j)"))
+            nc.tensor.matmul_mx(
+                out=o_ps[n][:],
+                lhsT=t_codes[i][:, 128 * c : 128 * c + 128].bitcast(FP8X4),
+                lhsT_scale=t_scales[i][:, 128 * c : 128 * c + 128],
+                rhs=cw[:].bitcast(FP8X4),
+                rhs_scale=cs[:],
+                start=(i == 0 and c == 0),
+                stop=(i == 1 and c == 1),
+            )
+
+        pre_sb = keep.tile([P, 4, 4, P], F32, name="pre_sb")
+        o_sb = keep.tile([P, 4, 4, P], F32, name="o_sb")
+        z_sb = keep.tile([P, 4, 4, P], F32, name="z_sb")
+        stats = keep.tile([P, 4, 6], F32, name="stats")
+
+        def close_bank(n):
+            nc.vector.tensor_tensor(
+                out=o_sb[:, n].rearrange("b (u e) q -> b u e q", u=2),
+                in0=o_ps[n][:].rearrange("b (u q e) -> b u e q", u=2, e=2),
+                in1=pre_sb[:, n].rearrange("b (u e) q -> b u e q", u=2),
+                op=ALU.add,
+            )
+            nc.vector.bn_stats(out=stats[:, n, :], in_=o_sb[:, n].rearrange("b t q -> b (t q)"))
+
+        prep_t(0)
+        units = [(0, c, n) for c in range(2) for n in range(4)]
+        prev = None
+        for un in units:
+            g_t = regroup(*un)
+            if prev is not None:
+                quant_mm(*prev)
+            prev = un + (g_t,)
+        quant_mm(*prev)
+
+        prep_t(1)
+        vps = wpool.tile([P, P], F32, tag="w", name="vps")
+        nc.tensor.transpose(vps[:], vecs[:], ident_f[:])
+        gbw = keep.tile([P, 18], F32, name="gbw")
+        nc.vector.tensor_copy(out=gbw[:], in_=vps[:, 0:18])
+        gbf = keep.tile([P, 36], F32, name="gbf")
+        nc.vector.tensor_copy(out=gbf[:], in_=gbw[:].bitcast(BF16))
+
+        xps = wpool.tile([P, P], BF16, tag="w", name="xps")
+        nc.tensor.transpose(xps[:], x_sb[:], ident_b[:])
+        xT = keep.tile([P, P], BF16, name="xT")
+        nc.vector.tensor_copy(out=xT[:], in_=xps[:])
+        for n in range(4):
+            pps = wpool.tile([P, NB], F32, tag="w", name="pps%d" % n)
+            nc.tensor.matmul(out=pps[:], lhsT=xT[:], rhs=km_sb[:, NB * n : NB * n + NB], start=True, stop=False)
+            nc.tensor.matmul(out=pps[:], lhsT=e0[:], rhs=b1z[:, NB * n : NB * n + NB], start=False, stop=True)
+            nc.scalar.copy(
+                out=pre_sb[:, n].rearrange("b (u e) q -> b u e q", u=2),
+                in_=pps[:].rearrange("b (u q e) -> b u e q", u=2, e=2),
+            )
+        fps = wpool.tile([P, 4, P], F32, tag="w", name="fps")
+        for t in range(4):
+            nc.tensor.transpose(fps[:, t, :], gbf[:, 32 + t : 33 + t].to_broadcast([P, P]), ident_f[:])
+        fcb = keep.tile([P, 2, P, 2], F32, name="fcb")
+        nc.scalar.copy(out=fcb[:], in_=fps[:].rearrange("m (r e) q -> m r q e", e=2))
+
+        units = [(1, c, n) for c in range(2) for n in range(4)]
+        prev = None
+        for un in units:
+            g_t = regroup(*un)
+            if prev is not None:
+                quant_mm(*prev)
+                if prev[1] == 1:
+                    close_bank(prev[2])
+            prev = un + (g_t,)
+        quant_mm(*prev)
+        close_bank(3)
+
+        mv = keep.tile([P, 2], F32, name="mv")
+        nc.vector.bn_aggr(out=mv[:], in_=stats[:].rearrange("b n s -> b (n s)"))
+        std = keep.tile([P, 1], F32, name="std")
+        nc.scalar.activation(out=std[:], in_=mv[:, 1:2], func=ACT.Sqrt, bias=eps[:], scale=1.0)
+        rstd = keep.tile([P, 1], F32, name="rstd")
+        nc.vector.reciprocal(out=rstd[:], in_=std[:])
+
+        y_pl = keep.tile([P, 4, 4, P], BF16, name="y_pl")
+        y_g = keep.tile([P, 4, P, 4], BF16, name="y_g", align_bytes=64)
+        y_w = keep.tile([P, 4 * P], U32, name="y_w", align_bytes=64)
+        y_s = keep.tile([P, 4 * P], U8, name="y_s", align_bytes=64)
+        for g in range(4):
+            nc.vector.tensor_scalar(
+                out=z_sb[:, g],
+                in0=o_sb[:, g],
+                scalar1=mv[:, 0:1],
+                scalar2=rstd[:],
+                op0=ALU.subtract,
+                op1=ALU.mult,
+            )
+            zT = opool.tile([P, 4, P], F32, name="zT%d" % g, tag="o%d" % g)
+            for t in range(4):
+                nc.tensor.transpose(zT[:, t, :], z_sb[:, g, t, :], ident_f[:])
+            for t in range(4):
+                k = 4 * g + t
+                if g % 2 == 0:
+                    nc.vector.tensor_scalar(
+                        out=y_pl[:, g, t, :],
+                        in0=zT[:, t, :],
+                        scalar1=gbf[:, k : k + 1],
+                        scalar2=gbf[:, 16 + k : 17 + k],
+                        op0=ALU.mult,
+                        op1=ALU.add,
+                    )
+                else:
+                    nc.scalar.activation(
+                        out=y_pl[:, g, t, :],
+                        in_=zT[:, t, :],
+                        func=ACT.Identity,
+                        bias=gbf[:, 16 + k : 17 + k],
+                        scale=gbf[:, k : k + 1],
+                    )
+            nc.vector.tensor_copy(
+                out=y_g[:, g].rearrange("p (c i) t -> p c t i", i=4),
+                in_=y_pl[:, g].rearrange("p t (c i) -> p c t i", i=4),
+            )
+            nc.vector.quantize_mx(
+                out=y_w[:, P * g : P * g + P].bitcast(FP8X4),
+                scales=y_s[:, P * g : P * g + P],
+                in_=y_g[:, g].rearrange("p b t -> p (b t)"),
+            )
+
+        w_w = keep.tile([P, 4, OUT], U32, name="w_w", align_bytes=64)
+        w_s = keep.tile([P, 4, OUT], U8, name="w_s", align_bytes=64)
+        for r in range(4):
+            fwv = fw_sb[r][:].bitcast(F32)
+            wg = wgpool.tile([P, 4, P, 2], F32, tag="wg", name="wg%d" % r, align_bytes=64)
+            for h in range(2):
+                wps = wpool.tile([P, 2, 2, P], F32, tag="w", name="wps%d%d" % (r, h))
+                for gg in range(2):
+                    for u in range(2):
+                        w0 = 256 * (2 * h + gg) + 128 * u
+                        nc.tensor.transpose(wps[:, gg, u, :], fwv[:, w0 : w0 + 128], ident_f[:])
+                nc.scalar.copy(out=wg[:, 2 * h : 2 * h + 2], in_=wps[:].rearrange("p g u n -> p g n u"))
+            for g in range(4):
+                nc.vector.quantize_mx(
+                    out=w_w[:, g, P * r : P * r + P].bitcast(FP8X4),
+                    scales=w_s[:, g, P * r : P * r + P],
+                    in_=wg[:, g].rearrange("p n u -> p (n u)").bitcast(BF16),
+                )
+
+        ops = wpool.tile([P, OUT], F32, tag="w", name="ops")
+        for g in range(4):
+            nc.tensor.matmul_mx(
+                out=ops[:],
+                lhsT=y_w[:, P * g : P * g + P].bitcast(FP8X4),
+                lhsT_scale=y_s[:, P * g : P * g + P],
+                rhs=w_w[:, g, :].bitcast(FP8X4),
+                rhs_scale=w_s[:, g, :],
+                start=(g == 0),
+                stop=(g == 3),
+            )
+        res = keep.tile([P, OUT], F32, name="res")
+        nc.vector.tensor_tensor(out=res[:], in0=ops[:], in1=fcb[:].rearrange("m r q e -> m (r q e)"), op=ALU.add)
+        nc.sync.dma_start(out=out.rearrange("b o n -> b (o n)"), in_=res[:])

@@ -12,270 +12,317 @@ ALU = mybir.AluOpType
 ACT = mybir.ActivationFunctionType
 
 P = 128
+PACK = 4
+K_PASS = P * PACK
 D = 2048
 KR = 1024
 OUT = 512
-NB = 512
+BANK = 512
+N_BANKS = D // BANK
 EPS = 1e-5
-V_COLS = 240
+V_SHARE = 7
 
 FLOPS = 2 * 128 * 2048 * (128 + 1024 + 1024) + 2 * 128 * 512 * 2048
 
 
+def core_chunks():
+    chunks = [(core, kpass, 2 * half, 2) for half in range(2) for core in range(2) for kpass in range(2)]
+    head, tail = chunks[0], chunks[-1]
+    return (
+        [(head[0], head[1], head[2] + b, 1) for b in range(2)]
+        + chunks[1:-1]
+        + [(tail[0], tail[1], tail[2] + b, 1) for b in range(2)]
+    )
+
+
 def tile_pinmodel_pa_kernel(tc, x, km1, b1, t2, core2, t3, core3, ln_g, ln_b, fc_w, fc_b, out):
     nc = tc.nc
+    chunks = core_chunks()
     with ExitStack() as ctx:
         const = ctx.enter_context(tc.tile_pool(name="const", bufs=1))
         raw = ctx.enter_context(tc.tile_pool(name="raw", bufs=1))
         keep = ctx.enter_context(tc.tile_pool(name="keep", bufs=1))
-        gpool = ctx.enter_context(tc.tile_pool(name="gpool", bufs=4))
-        wgpool = ctx.enter_context(tc.tile_pool(name="wgpool", bufs=2))
-        opool = ctx.enter_context(tc.psum_pool(name="opool", bufs=1))
-        wpool = ctx.enter_context(tc.psum_pool(name="wpool", bufs=4))
+        grouped_pool = ctx.enter_context(tc.tile_pool(name="grouped_pool", bufs=3))
+        w_grouped_pool = ctx.enter_context(tc.tile_pool(name="w_grouped_pool", bufs=2))
+        o_banks = ctx.enter_context(tc.psum_pool(name="o_banks", bufs=1))
+        work_banks = ctx.enter_context(tc.psum_pool(name="work_banks", bufs=1))
 
+        t_raw = [raw.tile([P, KR], BF16, name="t_raw%d" % i) for i in range(2)]
+        core_raw = [raw.tile([P, PACK, BANK * ch[3]], BF16, name="core_raw%d" % j) for j, ch in enumerate(chunks)]
+        x_raw = raw.tile([P, P], BF16, name="x_raw")
+        km_raw = raw.tile([P, D], BF16, name="km_raw")
+        w_raw = [raw.tile([P, D], BF16, name="w_raw%d" % r) for r in range(4)]
+
+        nc.scalar.dma_start(out=t_raw[0][:], in_=t2.rearrange("b r q -> b (r q)"))
         eps = const.tile([P, 1], F32, name="eps")
         nc.vector.memset(eps[:], EPS)
         warm = const.tile([P, 1], F32, name="warm")
         nc.scalar.activation(out=warm[:], in_=eps[:], func=ACT.Sqrt)
-        vecs = const.tile([P, P], F32, name="vecs")
-        nc.vector.memset(vecs[:], 0.0)
-        e0 = const.tile([P, P], BF16, name="e0")
-        nc.vector.memset(e0[:], 0.0)
-        nc.vector.memset(e0[0:1, :], 1.0)
-        b1z = const.tile([P, D], BF16, name="b1z")
-        nc.vector.memset(b1z[:], 0.0)
         ident_f = const.tile([P, P], F32, name="ident_f")
         make_identity(nc, ident_f[:])
         ident_b = const.tile([P, P], BF16, name="ident_b")
         make_identity(nc, ident_b[:])
+        vec_rows = const.tile([P, P], F32, name="vec_rows")
+        nc.vector.memset(vec_rows[:], 0.0)
+        first_row = const.tile([P, P], BF16, name="first_row")
+        nc.vector.memset(first_row[:], 0.0)
+        nc.vector.memset(first_row[0:1, :], 1.0)
+        b1_row = const.tile([P, D], BF16, name="b1_row")
+        nc.vector.memset(b1_row[:], 0.0)
 
-        nc.scalar.dma_start(out=vecs[0:8, :].bitcast(BF16), in_=ln_g.rearrange("(r c) -> r c", c=256))
-        nc.scalar.dma_start(out=vecs[8:16, :].bitcast(BF16), in_=ln_b.rearrange("(r c) -> r c", c=256))
-        nc.scalar.dma_start(out=vecs[16:18, :].bitcast(BF16), in_=fc_b.rearrange("(r c) -> r c", c=256))
-        nc.scalar.dma_start(out=b1z[0:1, :], in_=b1.rearrange("(o d) -> o d", o=1))
-
-        t_sb = [raw.tile([P, KR], BF16, name="t_sb%d" % i) for i in range(2)]
-        r_sb = [[raw.tile([P, 4, D], BF16, name="r_sb%d%d" % (i, c)) for c in range(2)] for i in range(2)]
-        x_sb = raw.tile([P, P], BF16, name="x_sb")
-        km_sb = raw.tile([P, D], BF16, name="km_sb")
-        fw_sb = [raw.tile([P, D], BF16, name="fw_sb%d" % r) for r in range(4)]
         cores = [core2.rearrange("r q d -> (r q) d"), core3.rearrange("r q d -> (r q) d")]
 
-        def load_core(i, c, d0, d1):
-            nc.sync.dma_start(
-                out=r_sb[i][c][:, :, d0:d1],
-                in_=cores[i][512 * c : 512 * c + 512, d0:d1].rearrange("(p j) d -> p j d", j=4),
-            )
+        def load_chunk(j):
+            core, kpass, bank0, banks = chunks[j]
+            rows = cores[core][K_PASS * kpass : K_PASS * (kpass + 1), BANK * bank0 : BANK * (bank0 + banks)]
+            nc.sync.dma_start(out=core_raw[j][:], in_=rows.rearrange("(p j) d -> p j d", j=PACK))
 
-        nc.sync.dma_start(out=t_sb[0][:], in_=t2.rearrange("b r q -> b (r q)"))
-        load_core(0, 0, 0, 512)
-        load_core(0, 0, 512, 1024)
-        load_core(0, 0, 1024, 2048)
-        load_core(0, 1, 0, 2048)
-        nc.sync.dma_start(out=t_sb[1][:], in_=t3.rearrange("b r q -> b (r q)"))
-        nc.sync.dma_start(out=x_sb[:], in_=x.rearrange("b i j -> b (i j)"))
-        nc.sync.dma_start(out=km_sb[:], in_=km1.rearrange("i j d -> (i j) d"))
-        load_core(1, 0, 0, 2048)
-        load_core(1, 1, 0, 1024)
-        load_core(1, 1, 1024, 1536)
-        load_core(1, 1, 1536, 2048)
+        load_chunk(0)
+        load_chunk(1)
+        nc.sync.dma_start(out=t_raw[1][:], in_=t3.rearrange("b r q -> b (r q)"))
+        nc.sync.dma_start(out=x_raw[:], in_=x.rearrange("b i j -> b (i j)"))
+        nc.sync.dma_start(out=km_raw[:], in_=km1.rearrange("i j d -> (i j) d"))
+        nc.sync.dma_start(out=b1_row[0:1, :], in_=b1.rearrange("(o d) -> o d", o=1))
+        nc.sync.dma_start(out=vec_rows[0:8, :].bitcast(BF16), in_=ln_g.rearrange("(r c) -> r c", c=256))
+        nc.sync.dma_start(out=vec_rows[8:16, :].bitcast(BF16), in_=ln_b.rearrange("(r c) -> r c", c=256))
+        nc.sync.dma_start(out=vec_rows[16:18, :].bitcast(BF16), in_=fc_b.rearrange("(r c) -> r c", c=256))
+        for j in range(2, len(chunks)):
+            load_chunk(j)
         for r in range(4):
-            nc.sync.dma_start(out=fw_sb[r][:], in_=fc_w[128 * r : 128 * r + 128, :])
+            nc.sync.dma_start(out=w_raw[r][:], in_=fc_w[P * r : P * (r + 1), :])
 
-        t_codes = []
-        t_scales = []
+        t_words = [keep.tile([P, 2 * P], U32, name="t_words%d" % i, align_bytes=64) for i in range(2)]
+        t_scales = [keep.tile([P, 2 * P], U8, name="t_scales%d" % i, align_bytes=64) for i in range(2)]
+        t_grouped = [keep.tile([P, 2, P, 2], F32, name="t_grouped%d" % i, align_bytes=64) for i in range(2)]
 
-        def prep_t(i):
-            tw = t_sb[i][:].bitcast(F32)
-            tps = wpool.tile([P, 2, 2, P], F32, tag="w", name="tps%d" % i)
-            for c in range(2):
+        def transpose_t(i):
+            pairs = t_raw[i][:].bitcast(F32)
+            flipped = work_banks.tile([P, 2, 2, P], F32, tag="work%d" % i, name="t_flipped%d" % i)
+            for kpass in range(2):
                 for u in range(2):
-                    nc.tensor.transpose(tps[:, c, u, :], tw[:, 256 * c + u : 256 * c + 256 : 2], ident_f[:])
-            tg = keep.tile([P, 2, P, 2], F32, name="tg%d" % i, align_bytes=64)
-            nc.scalar.copy(out=tg[:], in_=tps[:].rearrange("p c u b -> p c b u"))
-            tc_w = keep.tile([P, 256], U32, name="tc_w%d" % i, align_bytes=64)
-            tc_s = keep.tile([P, 256], U8, name="tc_s%d" % i, align_bytes=64)
+                    nc.tensor.transpose(
+                        flipped[:, kpass, u, :], pairs[:, 256 * kpass + u : 256 * (kpass + 1) : 2], ident_f[:]
+                    )
+            return flipped
+
+        def quantise_t(i, flipped):
+            nc.scalar.copy(out=t_grouped[i][:], in_=flipped[:].rearrange("p c u b -> p c b u"))
             nc.vector.quantize_mx(
-                out=tc_w[:].bitcast(FP8X4),
-                scales=tc_s[:],
-                in_=tg[:].rearrange("p c b u -> p (c b u)").bitcast(BF16),
+                out=t_words[i][:].bitcast(FP8X4),
+                scales=t_scales[i][:],
+                in_=t_grouped[i][:].rearrange("p c b u -> p (c b u)").bitcast(BF16),
             )
-            t_codes.append(tc_w)
-            t_scales.append(tc_s)
 
-        o_ps = [opool.tile([P, NB], F32, name="o_ps%d" % n, tag="o%d" % n) for n in range(4)]
+        o_ps = [o_banks.tile([P, BANK], F32, name="o_ps%d" % n, tag="o%d" % n) for n in range(N_BANKS)]
+        grouped = {}
 
-        def regroup(i, c, n):
-            g_t = gpool.tile([P, NB, 4], BF16, tag="G", name="g_t%d%d%d" % (i, c, n), align_bytes=64)
-            d0 = NB * n
+        def regroup(j):
+            width = BANK * chunks[j][3]
+            split = width * V_SHARE // 16
+            tile_j = grouped_pool.tile([P, width, PACK], BF16, tag="grouped", name="grouped%d" % j, align_bytes=64)
             nc.vector.tensor_copy(
-                out=g_t[:, 0:V_COLS, :].rearrange("p (c i) t -> p c t i", i=4),
-                in_=r_sb[i][c][:, :, d0 : d0 + V_COLS].rearrange("p t (c i) -> p c t i", i=4),
+                out=tile_j[:, 0:split, :].rearrange("p (c i) t -> p c t i", i=4),
+                in_=core_raw[j][:, :, 0:split].rearrange("p t (c i) -> p c t i", i=4),
             )
             nc.scalar.copy(
-                out=g_t[:, V_COLS:NB, :].rearrange("p (c i) t -> p c t i", i=4),
-                in_=r_sb[i][c][:, :, d0 + V_COLS : d0 + NB].rearrange("p t (c i) -> p c t i", i=4),
+                out=tile_j[:, split:width, :].rearrange("p (c i) t -> p c t i", i=4),
+                in_=core_raw[j][:, :, split:width].rearrange("p t (c i) -> p c t i", i=4),
             )
-            return g_t
+            grouped[j] = tile_j
 
-        def quant_mm(i, c, n, g_t):
-            cw = keep.tile([P, NB], U32, name="cw%d%d%d" % (i, c, n), align_bytes=64)
-            cs = keep.tile([P, NB], U8, name="cs%d%d%d" % (i, c, n), align_bytes=64)
-            nc.vector.quantize_mx(out=cw[:].bitcast(FP8X4), scales=cs[:], in_=g_t[:].rearrange("p w j -> p (w j)"))
-            nc.tensor.matmul_mx(
-                out=o_ps[n][:],
-                lhsT=t_codes[i][:, 128 * c : 128 * c + 128].bitcast(FP8X4),
-                lhsT_scale=t_scales[i][:, 128 * c : 128 * c + 128],
-                rhs=cw[:].bitcast(FP8X4),
-                rhs_scale=cs[:],
-                start=(i == 0 and c == 0),
-                stop=(i == 1 and c == 1),
+        def quantise_multiply(j):
+            core, kpass, bank0, banks = chunks[j]
+            width = BANK * banks
+            words = keep.tile([P, width], U32, name="core_words%d" % j, align_bytes=64)
+            scales = keep.tile([P, width], U8, name="core_scales%d" % j, align_bytes=64)
+            nc.vector.quantize_mx(
+                out=words[:].bitcast(FP8X4), scales=scales[:], in_=grouped[j][:].rearrange("p w j -> p (w j)")
             )
+            for b in range(banks):
+                nc.tensor.matmul_mx(
+                    out=o_ps[bank0 + b][:],
+                    lhsT=t_words[core][:, P * kpass : P * (kpass + 1)].bitcast(FP8X4),
+                    lhsT_scale=t_scales[core][:, P * kpass : P * (kpass + 1)],
+                    rhs=words[:, BANK * b : BANK * (b + 1)].bitcast(FP8X4),
+                    rhs_scale=scales[:, BANK * b : BANK * (b + 1)],
+                    start=(core == 0 and kpass == 0),
+                    stop=(core == 1 and kpass == 1),
+                )
 
-        pre_sb = keep.tile([P, 4, 4, P], F32, name="pre_sb")
-        o_sb = keep.tile([P, 4, 4, P], F32, name="o_sb")
-        z_sb = keep.tile([P, 4, 4, P], F32, name="z_sb")
-        stats = keep.tile([P, 4, 6], F32, name="stats")
+        order1 = keep.tile([P, N_BANKS, PACK, P], F32, name="order1")
+        o_sb = keep.tile([P, N_BANKS, PACK, P], F32, name="o_sb")
+        z_sb = keep.tile([P, N_BANKS, PACK, P], F32, name="z_sb")
+        stats = keep.tile([P, N_BANKS, 6], F32, name="stats")
 
         def close_bank(n):
             nc.vector.tensor_tensor(
                 out=o_sb[:, n].rearrange("b (u e) q -> b u e q", u=2),
                 in0=o_ps[n][:].rearrange("b (u q e) -> b u e q", u=2, e=2),
-                in1=pre_sb[:, n].rearrange("b (u e) q -> b u e q", u=2),
+                in1=order1[:, n].rearrange("b (u e) q -> b u e q", u=2),
                 op=ALU.add,
             )
             nc.vector.bn_stats(out=stats[:, n, :], in_=o_sb[:, n].rearrange("b t q -> b (t q)"))
 
-        prep_t(0)
-        units = [(0, c, n) for c in range(2) for n in range(4)]
-        prev = None
-        for un in units:
-            g_t = regroup(*un)
-            if prev is not None:
-                quant_mm(*prev)
-            prev = un + (g_t,)
-        quant_mm(*prev)
+        w_words = keep.tile([P, 4, OUT], U32, name="w_words", align_bytes=64)
+        w_scales = keep.tile([P, 4, OUT], U8, name="w_scales", align_bytes=64)
+        w_flipped = {}
+        w_grouped = {}
 
-        prep_t(1)
-        vps = wpool.tile([P, P], F32, tag="w", name="vps")
-        nc.tensor.transpose(vps[:], vecs[:], ident_f[:])
-        gbw = keep.tile([P, 18], F32, name="gbw")
-        nc.vector.tensor_copy(out=gbw[:], in_=vps[:, 0:18])
-        gbf = keep.tile([P, 36], F32, name="gbf")
-        nc.vector.tensor_copy(out=gbf[:], in_=gbw[:].bitcast(BF16))
-
-        xps = wpool.tile([P, P], BF16, tag="w", name="xps")
-        nc.tensor.transpose(xps[:], x_sb[:], ident_b[:])
-        xT = keep.tile([P, P], BF16, name="xT")
-        nc.vector.tensor_copy(out=xT[:], in_=xps[:])
-        for n in range(4):
-            pps = wpool.tile([P, NB], F32, tag="w", name="pps%d" % n)
-            nc.tensor.matmul(out=pps[:], lhsT=xT[:], rhs=km_sb[:, NB * n : NB * n + NB], start=True, stop=False)
-            nc.tensor.matmul(out=pps[:], lhsT=e0[:], rhs=b1z[:, NB * n : NB * n + NB], start=False, stop=True)
-            nc.scalar.copy(
-                out=pre_sb[:, n].rearrange("b (u e) q -> b u e q", u=2),
-                in_=pps[:].rearrange("b (u q e) -> b u e q", u=2, e=2),
+        def transpose_w(r, half):
+            pairs = w_raw[r][:].bitcast(F32)
+            flipped = work_banks.tile(
+                [P, 2, 2, P], F32, tag="work%d" % ((2 * r + half) % 4), name="w_flipped%d%d" % (r, half)
             )
-        fps = wpool.tile([P, 4, P], F32, tag="w", name="fps")
+            for g in range(2):
+                for u in range(2):
+                    first = 256 * (2 * half + g) + P * u
+                    nc.tensor.transpose(flipped[:, g, u, :], pairs[:, first : first + P], ident_f[:])
+            w_flipped[r, half] = flipped
+
+        def regroup_w(r):
+            w_grouped[r] = w_grouped_pool.tile([P, 4, P, 2], F32, tag="w_grouped", name="w_grouped%d" % r, align_bytes=64)
+            for half in range(2):
+                nc.scalar.copy(
+                    out=w_grouped[r][:, 2 * half : 2 * half + 2],
+                    in_=w_flipped[r, half][:].rearrange("p g u n -> p g n u"),
+                )
+
+        def quantise_w(r):
+            for g in range(4):
+                nc.vector.quantize_mx(
+                    out=w_words[:, g, P * r : P * (r + 1)].bitcast(FP8X4),
+                    scales=w_scales[:, g, P * r : P * (r + 1)],
+                    in_=w_grouped[r][:, g].rearrange("p n u -> p (n u)").bitcast(BF16),
+                )
+
+        t_flipped = transpose_t(0)
+        quantise_t(0, t_flipped)
+        regroup(0)
+        regroup(1)
+        quantise_multiply(0)
+
+        x_flipped = work_banks.tile([P, P], BF16, tag="work3", name="x_flipped")
+        nc.tensor.transpose(x_flipped[:], x_raw[:], ident_b[:])
+        t_flipped = transpose_t(1)
+        vec_flipped = work_banks.tile([P, P], F32, tag="work2", name="vec_flipped")
+        nc.tensor.transpose(vec_flipped[:], vec_rows[:], ident_f[:])
+        x_t = keep.tile([P, P], BF16, name="x_t")
+        nc.vector.tensor_copy(out=x_t[:], in_=x_flipped[:])
+        quantise_t(1, t_flipped)
+        vec_pairs = keep.tile([P, 18], F32, name="vec_pairs")
+        nc.vector.tensor_copy(out=vec_pairs[:], in_=vec_flipped[:, 0:18])
+        vec_cols = keep.tile([P, 36], F32, name="vec_cols")
+        nc.vector.tensor_copy(out=vec_cols[:], in_=vec_pairs[:].bitcast(BF16))
+        quantise_multiply(1)
+        order1_ps = []
+        for n in range(N_BANKS):
+            acc = work_banks.tile([P, BANK], F32, tag="work%d" % n, name="order1_ps%d" % n)
+            cols = slice(BANK * n, BANK * (n + 1))
+            nc.tensor.matmul(out=acc[:], lhsT=x_t[:], rhs=km_raw[:, cols], start=True, stop=False)
+            nc.tensor.matmul(out=acc[:], lhsT=first_row[:], rhs=b1_row[:, cols], start=False, stop=True)
+            order1_ps.append(acc)
+        for n in range(N_BANKS):
+            nc.scalar.copy(
+                out=order1[:, n].rearrange("b (u e) q -> b u e q", u=2),
+                in_=order1_ps[n][:].rearrange("b (u q e) -> b u e q", u=2, e=2),
+            )
+            if n == 1:
+                regroup(2)
+        fcb_ps = work_banks.tile([P, 4, P], F32, tag="work0", name="fcb_ps")
         for t in range(4):
-            nc.tensor.transpose(fps[:, t, :], gbf[:, 32 + t : 33 + t].to_broadcast([P, P]), ident_f[:])
+            nc.tensor.transpose(fcb_ps[:, t, :], vec_cols[:, 32 + t : 33 + t].to_broadcast([P, P]), ident_f[:])
         fcb = keep.tile([P, 2, P, 2], F32, name="fcb")
-        nc.scalar.copy(out=fcb[:], in_=fps[:].rearrange("m (r e) q -> m r q e", e=2))
 
-        units = [(1, c, n) for c in range(2) for n in range(4)]
-        prev = None
-        for un in units:
-            g_t = regroup(*un)
-            if prev is not None:
-                quant_mm(*prev)
-                if prev[1] == 1:
-                    close_bank(prev[2])
-            prev = un + (g_t,)
-        quant_mm(*prev)
+        last = len(chunks) - 1
+        for j in range(3, last + 1):
+            regroup(j)
+            if j == 3:
+                nc.scalar.copy(out=fcb[:], in_=fcb_ps[:].rearrange("m (r e) q -> m r q e", e=2))
+            quantise_multiply(j - 1)
+            if j == 6:
+                close_bank(0)
+            if j == 7:
+                close_bank(1)
+
+        for r in range(2):
+            for half in range(2):
+                transpose_w(r, half)
+        quantise_multiply(last)
+        regroup_w(0)
+        regroup_w(1)
+        close_bank(2)
+        quantise_w(0)
+        transpose_w(2, 0)
+        transpose_w(2, 1)
+        regroup_w(2)
         close_bank(3)
-
-        mv = keep.tile([P, 2], F32, name="mv")
-        nc.vector.bn_aggr(out=mv[:], in_=stats[:].rearrange("b n s -> b (n s)"))
+        mean_var = keep.tile([P, 2], F32, name="mean_var")
+        nc.vector.bn_aggr(out=mean_var[:], in_=stats[:].rearrange("b n s -> b (n s)"))
         std = keep.tile([P, 1], F32, name="std")
-        nc.scalar.activation(out=std[:], in_=mv[:, 1:2], func=ACT.Sqrt, bias=eps[:], scale=1.0)
+        nc.scalar.activation(out=std[:], in_=mean_var[:, 1:2], func=ACT.Sqrt, bias=eps[:], scale=1.0)
+        quantise_w(1)
+        transpose_w(3, 0)
+        transpose_w(3, 1)
+        regroup_w(3)
         rstd = keep.tile([P, 1], F32, name="rstd")
         nc.vector.reciprocal(out=rstd[:], in_=std[:])
 
-        y_pl = keep.tile([P, 4, 4, P], BF16, name="y_pl")
-        y_g = keep.tile([P, 4, P, 4], BF16, name="y_g", align_bytes=64)
-        y_w = keep.tile([P, 4 * P], U32, name="y_w", align_bytes=64)
-        y_s = keep.tile([P, 4 * P], U8, name="y_s", align_bytes=64)
+        y_planes = keep.tile([P, 4, PACK, P], BF16, name="y_planes")
+        y_grouped = keep.tile([P, 4, P, PACK], BF16, name="y_grouped", align_bytes=64)
+        y_words = keep.tile([P, 4 * P], U32, name="y_words", align_bytes=64)
+        y_scales = keep.tile([P, 4 * P], U8, name="y_scales", align_bytes=64)
+        z_flipped = []
         for g in range(4):
             nc.vector.tensor_scalar(
                 out=z_sb[:, g],
                 in0=o_sb[:, g],
-                scalar1=mv[:, 0:1],
+                scalar1=mean_var[:, 0:1],
                 scalar2=rstd[:],
                 op0=ALU.subtract,
                 op1=ALU.mult,
             )
-            zT = opool.tile([P, 4, P], F32, name="zT%d" % g, tag="o%d" % g)
-            for t in range(4):
-                nc.tensor.transpose(zT[:, t, :], z_sb[:, g, t, :], ident_f[:])
-            for t in range(4):
-                k = 4 * g + t
-                if g % 2 == 0:
-                    nc.vector.tensor_scalar(
-                        out=y_pl[:, g, t, :],
-                        in0=zT[:, t, :],
-                        scalar1=gbf[:, k : k + 1],
-                        scalar2=gbf[:, 16 + k : 17 + k],
-                        op0=ALU.mult,
-                        op1=ALU.add,
-                    )
-                else:
-                    nc.scalar.activation(
-                        out=y_pl[:, g, t, :],
-                        in_=zT[:, t, :],
-                        func=ACT.Identity,
-                        bias=gbf[:, 16 + k : 17 + k],
-                        scale=gbf[:, k : k + 1],
-                    )
-            nc.vector.tensor_copy(
-                out=y_g[:, g].rearrange("p (c i) t -> p c t i", i=4),
-                in_=y_pl[:, g].rearrange("p t (c i) -> p c t i", i=4),
-            )
-            nc.vector.quantize_mx(
-                out=y_w[:, P * g : P * g + P].bitcast(FP8X4),
-                scales=y_s[:, P * g : P * g + P],
-                in_=y_g[:, g].rearrange("p b t -> p (b t)"),
-            )
-
-        w_w = keep.tile([P, 4, OUT], U32, name="w_w", align_bytes=64)
-        w_s = keep.tile([P, 4, OUT], U8, name="w_s", align_bytes=64)
-        for r in range(4):
-            fwv = fw_sb[r][:].bitcast(F32)
-            wg = wgpool.tile([P, 4, P, 2], F32, tag="wg", name="wg%d" % r, align_bytes=64)
-            for h in range(2):
-                wps = wpool.tile([P, 2, 2, P], F32, tag="w", name="wps%d%d" % (r, h))
-                for gg in range(2):
-                    for u in range(2):
-                        w0 = 256 * (2 * h + gg) + 128 * u
-                        nc.tensor.transpose(wps[:, gg, u, :], fwv[:, w0 : w0 + 128], ident_f[:])
-                nc.scalar.copy(out=wg[:, 2 * h : 2 * h + 2], in_=wps[:].rearrange("p g u n -> p g n u"))
-            for g in range(4):
-                nc.vector.quantize_mx(
-                    out=w_w[:, g, P * r : P * r + P].bitcast(FP8X4),
-                    scales=w_s[:, g, P * r : P * r + P],
-                    in_=wg[:, g].rearrange("p n u -> p (n u)").bitcast(BF16),
-                )
-
-        ops = wpool.tile([P, OUT], F32, tag="w", name="ops")
+            flipped = o_banks.tile([P, PACK, P], F32, name="z_flipped%d" % g, tag="o%d" % g)
+            for t in range(PACK):
+                nc.tensor.transpose(flipped[:, t, :], z_sb[:, g, t, :], ident_f[:])
+            z_flipped.append(flipped)
+        quantise_w(2)
         for g in range(4):
+            for t in range(PACK):
+                k = PACK * g + t
+                nc.scalar.activation(
+                    out=y_planes[:, g, t, :],
+                    in_=z_flipped[g][:, t, :],
+                    func=ACT.Identity,
+                    bias=vec_cols[:, 16 + k : 17 + k],
+                    scale=vec_cols[:, k : k + 1],
+                )
+        quantise_w(3)
+        out_ps = work_banks.tile([P, OUT], F32, tag="work0", name="out_ps")
+
+        def head_pass(g):
+            nc.vector.quantize_mx(
+                out=y_words[:, P * g : P * (g + 1)].bitcast(FP8X4),
+                scales=y_scales[:, P * g : P * (g + 1)],
+                in_=y_grouped[:, g].rearrange("p b t -> p (b t)"),
+            )
             nc.tensor.matmul_mx(
-                out=ops[:],
-                lhsT=y_w[:, P * g : P * g + P].bitcast(FP8X4),
-                lhsT_scale=y_s[:, P * g : P * g + P],
-                rhs=w_w[:, g, :].bitcast(FP8X4),
-                rhs_scale=w_s[:, g, :],
+                out=out_ps[:],
+                lhsT=y_words[:, P * g : P * (g + 1)].bitcast(FP8X4),
+                lhsT_scale=y_scales[:, P * g : P * (g + 1)],
+                rhs=w_words[:, g, :].bitcast(FP8X4),
+                rhs_scale=w_scales[:, g, :],
                 start=(g == 0),
                 stop=(g == 3),
             )
-        res = keep.tile([P, OUT], F32, name="res")
-        nc.vector.tensor_tensor(out=res[:], in0=ops[:], in1=fcb[:].rearrange("m r q e -> m (r q e)"), op=ALU.add)
-        nc.sync.dma_start(out=out.rearrange("b o n -> b (o n)"), in_=res[:])
+
+        for g in range(4):
+            nc.vector.tensor_copy(
+                out=y_grouped[:, g].rearrange("p (c i) t -> p c t i", i=4),
+                in_=y_planes[:, g].rearrange("p t (c i) -> p c t i", i=4),
+            )
+            if g > 0:
+                head_pass(g - 1)
+        head_pass(3)
+        result = keep.tile([P, OUT], F32, name="result")
+        nc.vector.tensor_tensor(out=result[:], in0=out_ps[:], in1=fcb[:].rearrange("m r q e -> m (r q e)"), op=ALU.add)
+        nc.sync.dma_start(out=out.rearrange("b o n -> b (o n)"), in_=result[:])

@@ -20,7 +20,7 @@ OUT = 512
 BANK = 512
 N_BANKS = D // BANK
 EPS = 1e-5
-V_SHARE = 7
+V_SHARE = ((15, 32), (15, 32))
 
 FLOPS = 2 * 128 * 2048 * (128 + 1024 + 1024) + 2 * 128 * 512 * 2048
 
@@ -57,7 +57,7 @@ def tile_pinmodel_pa_kernel(tc, x, km1, b1, t2, core2, t3, core3, ln_g, ln_b, fc
         eps = const.tile([P, 1], F32, name="eps")
         nc.vector.memset(eps[:], EPS)
         warm = const.tile([P, 1], F32, name="warm")
-        nc.scalar.activation(out=warm[:], in_=eps[:], func=ACT.Sqrt)
+        nc.scalar.activation(out=warm[:], in_=eps[:], func=ACT.Abs_reciprocal_sqrt)
         ident_f = const.tile([P, P], F32, name="ident_f")
         make_identity(nc, ident_f[:])
         ident_b = const.tile([P, P], BF16, name="ident_b")
@@ -118,7 +118,8 @@ def tile_pinmodel_pa_kernel(tc, x, km1, b1, t2, core2, t3, core3, ln_g, ln_b, fc
 
         def regroup(j):
             width = BANK * chunks[j][3]
-            split = width * V_SHARE // 16
+            share = V_SHARE[chunks[j][2] // 2]
+            split = width * share[0] // share[1]
             tile_j = grouped_pool.tile([P, width, PACK], BF16, tag="grouped", name="grouped%d" % j, align_bytes=64)
             nc.vector.tensor_copy(
                 out=tile_j[:, 0:split, :].rearrange("p (c i) t -> p c t i", i=4),
@@ -168,32 +169,31 @@ def tile_pinmodel_pa_kernel(tc, x, km1, b1, t2, core2, t3, core3, ln_g, ln_b, fc
         w_flipped = {}
         w_grouped = {}
 
-        def transpose_w(r, half):
-            pairs = w_raw[r][:].bitcast(F32)
+        def transpose_w(g, half):
             flipped = work_banks.tile(
-                [P, 2, 2, P], F32, tag="work%d" % ((2 * r + half) % 4), name="w_flipped%d%d" % (r, half)
+                [P, 2, 2, P], F32, tag="work%d" % ((2 * g + half) % 4), name="w_flipped%d%d" % (g, half)
             )
-            for g in range(2):
+            for r in range(2):
+                pairs = w_raw[2 * half + r][:].bitcast(F32)
                 for u in range(2):
-                    first = 256 * (2 * half + g) + P * u
-                    nc.tensor.transpose(flipped[:, g, u, :], pairs[:, first : first + P], ident_f[:])
-            w_flipped[r, half] = flipped
+                    first = 256 * g + P * u
+                    nc.tensor.transpose(flipped[:, r, u, :], pairs[:, first : first + P], ident_f[:])
+            w_flipped[g, half] = flipped
 
-        def regroup_w(r):
-            w_grouped[r] = w_grouped_pool.tile([P, 4, P, 2], F32, tag="w_grouped", name="w_grouped%d" % r, align_bytes=64)
+        def regroup_w(g):
+            w_grouped[g] = w_grouped_pool.tile([P, 4, P, 2], F32, tag="w_grouped", name="w_grouped%d" % g, align_bytes=64)
             for half in range(2):
                 nc.scalar.copy(
-                    out=w_grouped[r][:, 2 * half : 2 * half + 2],
-                    in_=w_flipped[r, half][:].rearrange("p g u n -> p g n u"),
+                    out=w_grouped[g][:, 2 * half : 2 * half + 2],
+                    in_=w_flipped[g, half][:].rearrange("p r u n -> p r n u"),
                 )
 
-        def quantise_w(r):
-            for g in range(4):
-                nc.vector.quantize_mx(
-                    out=w_words[:, g, P * r : P * (r + 1)].bitcast(FP8X4),
-                    scales=w_scales[:, g, P * r : P * (r + 1)],
-                    in_=w_grouped[r][:, g].rearrange("p n u -> p (n u)").bitcast(BF16),
-                )
+        def quantise_w(g):
+            nc.vector.quantize_mx(
+                out=w_words[:, g, :].bitcast(FP8X4),
+                scales=w_scales[:, g, :],
+                in_=w_grouped[g][:].rearrange("p r n u -> p (r n u)").bitcast(BF16),
+            )
 
         t_flipped = transpose_t(0)
         quantise_t(0, t_flipped)
@@ -236,36 +236,24 @@ def tile_pinmodel_pa_kernel(tc, x, km1, b1, t2, core2, t3, core3, ln_g, ln_b, fc
         last = len(chunks) - 1
         for j in range(3, last + 1):
             regroup(j)
-            if j == 3:
-                nc.scalar.copy(out=fcb[:], in_=fcb_ps[:].rearrange("m (r e) q -> m r q e", e=2))
             quantise_multiply(j - 1)
             if j == 6:
                 close_bank(0)
             if j == 7:
                 close_bank(1)
 
-        for r in range(2):
-            for half in range(2):
-                transpose_w(r, half)
         quantise_multiply(last)
-        regroup_w(0)
-        regroup_w(1)
         close_bank(2)
-        quantise_w(0)
-        transpose_w(2, 0)
-        transpose_w(2, 1)
-        regroup_w(2)
         close_bank(3)
+
         mean_var = keep.tile([P, 2], F32, name="mean_var")
         nc.vector.bn_aggr(out=mean_var[:], in_=stats[:].rearrange("b n s -> b (n s)"))
-        std = keep.tile([P, 1], F32, name="std")
-        nc.scalar.activation(out=std[:], in_=mean_var[:, 1:2], func=ACT.Sqrt, bias=eps[:], scale=1.0)
-        quantise_w(1)
-        transpose_w(3, 0)
-        transpose_w(3, 1)
-        regroup_w(3)
         rstd = keep.tile([P, 1], F32, name="rstd")
-        nc.vector.reciprocal(out=rstd[:], in_=std[:])
+        nc.scalar.activation(out=rstd[:], in_=mean_var[:, 1:2], func=ACT.Abs_reciprocal_sqrt, bias=eps[:], scale=1.0)
+        neg_mean = keep.tile([P, 1], F32, name="neg_mean")
+        nc.vector.tensor_scalar_mul(out=neg_mean[:], in0=mean_var[:, 0:1], scalar1=-1.0)
+        shift = keep.tile([P, 1], F32, name="shift")
+        nc.scalar.activation(out=shift[:], in_=neg_mean[:], func=ACT.Identity, scale=rstd[:])
 
         y_planes = keep.tile([P, 4, PACK, P], BF16, name="y_planes")
         y_grouped = keep.tile([P, 4, P, PACK], BF16, name="y_grouped", align_bytes=64)
@@ -273,38 +261,62 @@ def tile_pinmodel_pa_kernel(tc, x, km1, b1, t2, core2, t3, core3, ln_g, ln_b, fc
         y_scales = keep.tile([P, 4 * P], U8, name="y_scales", align_bytes=64)
         z_flipped = []
         for g in range(4):
-            nc.vector.tensor_scalar(
-                out=z_sb[:, g],
-                in0=o_sb[:, g],
-                scalar1=mean_var[:, 0:1],
-                scalar2=rstd[:],
-                op0=ALU.subtract,
-                op1=ALU.mult,
-            )
+            if g % 2 == 0:
+                nc.vector.tensor_scalar(
+                    out=z_sb[:, g],
+                    in0=o_sb[:, g],
+                    scalar1=mean_var[:, 0:1],
+                    scalar2=rstd[:],
+                    op0=ALU.subtract,
+                    op1=ALU.mult,
+                )
+            else:
+                nc.scalar.activation(out=z_sb[:, g], in_=o_sb[:, g], func=ACT.Identity, bias=shift[:], scale=rstd[:])
             flipped = o_banks.tile([P, PACK, P], F32, name="z_flipped%d" % g, tag="o%d" % g)
             for t in range(PACK):
                 nc.tensor.transpose(flipped[:, t, :], z_sb[:, g, t, :], ident_f[:])
             z_flipped.append(flipped)
-        quantise_w(2)
         for g in range(4):
             for t in range(PACK):
                 k = PACK * g + t
-                nc.scalar.activation(
-                    out=y_planes[:, g, t, :],
-                    in_=z_flipped[g][:, t, :],
-                    func=ACT.Identity,
-                    bias=vec_cols[:, 16 + k : 17 + k],
-                    scale=vec_cols[:, k : k + 1],
-                )
-        quantise_w(3)
-        out_ps = work_banks.tile([P, OUT], F32, tag="work0", name="out_ps")
-
-        def head_pass(g):
+                if g % 2 == 0:
+                    nc.vector.tensor_scalar(
+                        out=y_planes[:, g, t, :],
+                        in0=z_flipped[g][:, t, :],
+                        scalar1=vec_cols[:, k : k + 1],
+                        scalar2=vec_cols[:, 16 + k : 17 + k],
+                        op0=ALU.mult,
+                        op1=ALU.add,
+                    )
+                else:
+                    nc.scalar.activation(
+                        out=y_planes[:, g, t, :],
+                        in_=z_flipped[g][:, t, :],
+                        func=ACT.Identity,
+                        bias=vec_cols[:, 16 + k : 17 + k],
+                        scale=vec_cols[:, k : k + 1],
+                    )
+        for g in range(4):
+            nc.vector.tensor_copy(
+                out=y_grouped[:, g].rearrange("p (c i) t -> p c t i", i=4),
+                in_=y_planes[:, g].rearrange("p t (c i) -> p c t i", i=4),
+            )
+        for g in range(4):
             nc.vector.quantize_mx(
                 out=y_words[:, P * g : P * (g + 1)].bitcast(FP8X4),
                 scales=y_scales[:, P * g : P * (g + 1)],
                 in_=y_grouped[:, g].rearrange("p b t -> p (b t)"),
             )
+
+        nc.scalar.copy(out=fcb[:], in_=fcb_ps[:].rearrange("m (r e) q -> m r q e", e=2))
+        for g in range(4):
+            for half in range(2):
+                transpose_w(g, half)
+            regroup_w(g)
+            quantise_w(g)
+
+        out_ps = work_banks.tile([P, OUT], F32, tag="work0", name="out_ps")
+        for g in range(4):
             nc.tensor.matmul_mx(
                 out=out_ps[:],
                 lhsT=y_words[:, P * g : P * (g + 1)].bitcast(FP8X4),
@@ -314,15 +326,6 @@ def tile_pinmodel_pa_kernel(tc, x, km1, b1, t2, core2, t3, core3, ln_g, ln_b, fc
                 start=(g == 0),
                 stop=(g == 3),
             )
-
-        for g in range(4):
-            nc.vector.tensor_copy(
-                out=y_grouped[:, g].rearrange("p (c i) t -> p c t i", i=4),
-                in_=y_planes[:, g].rearrange("p t (c i) -> p c t i", i=4),
-            )
-            if g > 0:
-                head_pass(g - 1)
-        head_pass(3)
         result = keep.tile([P, OUT], F32, name="result")
         nc.vector.tensor_tensor(out=result[:], in0=out_ps[:], in1=fcb[:].rearrange("m r q e -> m (r q e)"), op=ALU.add)
         nc.sync.dma_start(out=out.rearrange("b o n -> b (o n)"), in_=result[:])

@@ -20,7 +20,7 @@ OUT = 512
 BANK = 512
 N_BANKS = D // BANK
 EPS = 1e-5
-V_SHARE = ((15, 32), (15, 32))
+V_SHARE = (15, 32)
 
 FLOPS = 2 * 128 * 2048 * (128 + 1024 + 1024) + 2 * 128 * 512 * 2048
 
@@ -39,10 +39,11 @@ def tile_pinmodel_pa_kernel(tc, x, km1, b1, t2, core2, t3, core3, ln_g, ln_b, fc
     nc = tc.nc
     chunks = core_chunks()
     with ExitStack() as ctx:
+        ctx.enter_context(tc.manual_schedule())
         const = ctx.enter_context(tc.tile_pool(name="const", bufs=1))
         raw = ctx.enter_context(tc.tile_pool(name="raw", bufs=1))
         keep = ctx.enter_context(tc.tile_pool(name="keep", bufs=1))
-        grouped_pool = ctx.enter_context(tc.tile_pool(name="grouped_pool", bufs=3))
+        grouped_pool = ctx.enter_context(tc.tile_pool(name="grouped_pool", bufs=4))
         w_grouped_pool = ctx.enter_context(tc.tile_pool(name="w_grouped_pool", bufs=2))
         o_banks = ctx.enter_context(tc.psum_pool(name="o_banks", bufs=1))
         work_banks = ctx.enter_context(tc.psum_pool(name="work_banks", bufs=1))
@@ -53,7 +54,6 @@ def tile_pinmodel_pa_kernel(tc, x, km1, b1, t2, core2, t3, core3, ln_g, ln_b, fc
         km_raw = raw.tile([P, D], BF16, name="km_raw")
         w_raw = [raw.tile([P, D], BF16, name="w_raw%d" % r) for r in range(4)]
 
-        nc.scalar.dma_start(out=t_raw[0][:], in_=t2.rearrange("b r q -> b (r q)"))
         eps = const.tile([P, 1], F32, name="eps")
         nc.vector.memset(eps[:], EPS)
         warm = const.tile([P, 1], F32, name="warm")
@@ -78,15 +78,18 @@ def tile_pinmodel_pa_kernel(tc, x, km1, b1, t2, core2, t3, core3, ln_g, ln_b, fc
             nc.sync.dma_start(out=core_raw[j][:], in_=rows.rearrange("(p j) d -> p j d", j=PACK))
 
         load_chunk(0)
+        nc.sync.dma_start(out=t_raw[0][:], in_=t2.rearrange("b r q -> b (r q)"))
         load_chunk(1)
         nc.sync.dma_start(out=t_raw[1][:], in_=t3.rearrange("b r q -> b (r q)"))
         nc.sync.dma_start(out=x_raw[:], in_=x.rearrange("b i j -> b (i j)"))
         nc.sync.dma_start(out=km_raw[:], in_=km1.rearrange("i j d -> (i j) d"))
         nc.sync.dma_start(out=b1_row[0:1, :], in_=b1.rearrange("(o d) -> o d", o=1))
+        for j in range(2, 6):
+            load_chunk(j)
         nc.sync.dma_start(out=vec_rows[0:8, :].bitcast(BF16), in_=ln_g.rearrange("(r c) -> r c", c=256))
         nc.sync.dma_start(out=vec_rows[8:16, :].bitcast(BF16), in_=ln_b.rearrange("(r c) -> r c", c=256))
         nc.sync.dma_start(out=vec_rows[16:18, :].bitcast(BF16), in_=fc_b.rearrange("(r c) -> r c", c=256))
-        for j in range(2, len(chunks)):
+        for j in range(6, len(chunks)):
             load_chunk(j)
         for r in range(4):
             nc.sync.dma_start(out=w_raw[r][:], in_=fc_w[P * r : P * (r + 1), :])
@@ -105,8 +108,10 @@ def tile_pinmodel_pa_kernel(tc, x, km1, b1, t2, core2, t3, core3, ln_g, ln_b, fc
                     )
             return flipped
 
-        def quantise_t(i, flipped):
+        def regroup_t(i, flipped):
             nc.scalar.copy(out=t_grouped[i][:], in_=flipped[:].rearrange("p c u b -> p c b u"))
+
+        def quantise_t(i):
             nc.vector.quantize_mx(
                 out=t_words[i][:].bitcast(FP8X4),
                 scales=t_scales[i][:],
@@ -118,8 +123,7 @@ def tile_pinmodel_pa_kernel(tc, x, km1, b1, t2, core2, t3, core3, ln_g, ln_b, fc
 
         def regroup(j):
             width = BANK * chunks[j][3]
-            share = V_SHARE[chunks[j][2] // 2]
-            split = width * share[0] // share[1]
+            split = width * V_SHARE[0] // V_SHARE[1]
             tile_j = grouped_pool.tile([P, width, PACK], BF16, tag="grouped", name="grouped%d" % j, align_bytes=64)
             nc.vector.tensor_copy(
                 out=tile_j[:, 0:split, :].rearrange("p (c i) t -> p c t i", i=4),
@@ -195,25 +199,22 @@ def tile_pinmodel_pa_kernel(tc, x, km1, b1, t2, core2, t3, core3, ln_g, ln_b, fc
                 in_=w_grouped[g][:].rearrange("p r n u -> p (r n u)").bitcast(BF16),
             )
 
-        t_flipped = transpose_t(0)
-        quantise_t(0, t_flipped)
+        last = len(chunks) - 1
         regroup(0)
+        t_flipped = transpose_t(0)
+        regroup_t(0, t_flipped)
         regroup(1)
+        quantise_t(0)
         quantise_multiply(0)
 
         x_flipped = work_banks.tile([P, P], BF16, tag="work3", name="x_flipped")
         nc.tensor.transpose(x_flipped[:], x_raw[:], ident_b[:])
         t_flipped = transpose_t(1)
-        vec_flipped = work_banks.tile([P, P], F32, tag="work2", name="vec_flipped")
-        nc.tensor.transpose(vec_flipped[:], vec_rows[:], ident_f[:])
         x_t = keep.tile([P, P], BF16, name="x_t")
         nc.vector.tensor_copy(out=x_t[:], in_=x_flipped[:])
-        quantise_t(1, t_flipped)
-        vec_pairs = keep.tile([P, 18], F32, name="vec_pairs")
-        nc.vector.tensor_copy(out=vec_pairs[:], in_=vec_flipped[:, 0:18])
-        vec_cols = keep.tile([P, 36], F32, name="vec_cols")
-        nc.vector.tensor_copy(out=vec_cols[:], in_=vec_pairs[:].bitcast(BF16))
+        regroup_t(1, t_flipped)
         quantise_multiply(1)
+        quantise_t(1)
         order1_ps = []
         for n in range(N_BANKS):
             acc = work_banks.tile([P, BANK], F32, tag="work%d" % n, name="order1_ps%d" % n)
@@ -221,31 +222,46 @@ def tile_pinmodel_pa_kernel(tc, x, km1, b1, t2, core2, t3, core3, ln_g, ln_b, fc
             nc.tensor.matmul(out=acc[:], lhsT=x_t[:], rhs=km_raw[:, cols], start=True, stop=False)
             nc.tensor.matmul(out=acc[:], lhsT=first_row[:], rhs=b1_row[:, cols], start=False, stop=True)
             order1_ps.append(acc)
-        for n in range(N_BANKS):
+
+        def keep_order1(n):
             nc.scalar.copy(
                 out=order1[:, n].rearrange("b (u e) q -> b u e q", u=2),
                 in_=order1_ps[n][:].rearrange("b (u q e) -> b u e q", u=2, e=2),
             )
-            if n == 1:
-                regroup(2)
-        fcb_ps = work_banks.tile([P, 4, P], F32, tag="work0", name="fcb_ps")
-        for t in range(4):
-            nc.tensor.transpose(fcb_ps[:, t, :], vec_cols[:, 32 + t : 33 + t].to_broadcast([P, P]), ident_f[:])
-        fcb = keep.tile([P, 2, P, 2], F32, name="fcb")
 
-        last = len(chunks) - 1
+        vec_pairs = keep.tile([P, 18], F32, name="vec_pairs")
+        vec_cols = keep.tile([P, 36], F32, name="vec_cols")
+        fcb = keep.tile([P, 2, P, 2], F32, name="fcb")
+        regroup(2)
         for j in range(3, last + 1):
+            if j <= 4:
+                keep_order1(2 * (j - 3))
+                keep_order1(2 * (j - 3) + 1)
             regroup(j)
             quantise_multiply(j - 1)
-            if j == 6:
-                close_bank(0)
-            if j == 7:
-                close_bank(1)
+            if j == 6 or j == 7:
+                close_bank(j - 6)
+            if j == 8:
+                vec_flipped = work_banks.tile([P, P], F32, tag="work2", name="vec_flipped")
+                nc.tensor.transpose(vec_flipped[:], vec_rows[:], ident_f[:])
+                nc.vector.tensor_copy(out=vec_pairs[:], in_=vec_flipped[:, 0:18])
+                nc.vector.tensor_copy(out=vec_cols[:], in_=vec_pairs[:].bitcast(BF16))
+                fcb_ps = work_banks.tile([P, 4, P], F32, tag="work3", name="fcb_ps")
+                for t in range(4):
+                    nc.tensor.transpose(fcb_ps[:, t, :], vec_cols[:, 32 + t : 33 + t].to_broadcast([P, P]), ident_f[:])
 
+        nc.scalar.copy(out=fcb[:], in_=fcb_ps[:].rearrange("m (r e) q -> m r q e", e=2))
+        transpose_w(0, 0)
+        transpose_w(0, 1)
+        transpose_w(1, 0)
         quantise_multiply(last)
+        transpose_w(1, 1)
+        regroup_w(0)
         close_bank(2)
+        regroup_w(1)
+        transpose_w(2, 0)
+        transpose_w(2, 1)
         close_bank(3)
-
         mean_var = keep.tile([P, 2], F32, name="mean_var")
         nc.vector.bn_aggr(out=mean_var[:], in_=stats[:].rearrange("b n s -> b (n s)"))
         rstd = keep.tile([P, 1], F32, name="rstd")
@@ -254,14 +270,20 @@ def tile_pinmodel_pa_kernel(tc, x, km1, b1, t2, core2, t3, core3, ln_g, ln_b, fc
         nc.vector.tensor_scalar_mul(out=neg_mean[:], in0=mean_var[:, 0:1], scalar1=-1.0)
         shift = keep.tile([P, 1], F32, name="shift")
         nc.scalar.activation(out=shift[:], in_=neg_mean[:], func=ACT.Identity, scale=rstd[:])
+        quantise_w(0)
+        transpose_w(3, 0)
+        transpose_w(3, 1)
 
         y_planes = keep.tile([P, 4, PACK, P], BF16, name="y_planes")
         y_grouped = keep.tile([P, 4, P, PACK], BF16, name="y_grouped", align_bytes=64)
         y_words = keep.tile([P, 4 * P], U32, name="y_words", align_bytes=64)
         y_scales = keep.tile([P, 4 * P], U8, name="y_scales", align_bytes=64)
-        z_flipped = []
-        for g in range(4):
-            if g % 2 == 0:
+        z_flipped = {}
+        on_vector = (0, 2)
+        on_scalar = (1, 3)
+
+        def normalise(g):
+            if g in on_vector:
                 nc.vector.tensor_scalar(
                     out=z_sb[:, g],
                     in0=o_sb[:, g],
@@ -272,14 +294,17 @@ def tile_pinmodel_pa_kernel(tc, x, km1, b1, t2, core2, t3, core3, ln_g, ln_b, fc
                 )
             else:
                 nc.scalar.activation(out=z_sb[:, g], in_=o_sb[:, g], func=ACT.Identity, bias=shift[:], scale=rstd[:])
+
+        def transpose_z(g):
             flipped = o_banks.tile([P, PACK, P], F32, name="z_flipped%d" % g, tag="o%d" % g)
             for t in range(PACK):
                 nc.tensor.transpose(flipped[:, t, :], z_sb[:, g, t, :], ident_f[:])
-            z_flipped.append(flipped)
-        for g in range(4):
+            z_flipped[g] = flipped
+
+        def scale_shift(g):
             for t in range(PACK):
                 k = PACK * g + t
-                if g % 2 == 0:
+                if g in on_vector:
                     nc.vector.tensor_scalar(
                         out=y_planes[:, g, t, :],
                         in0=z_flipped[g][:, t, :],
@@ -296,36 +321,57 @@ def tile_pinmodel_pa_kernel(tc, x, km1, b1, t2, core2, t3, core3, ln_g, ln_b, fc
                         bias=vec_cols[:, 16 + k : 17 + k],
                         scale=vec_cols[:, k : k + 1],
                     )
-        for g in range(4):
+
+        def regroup_y(g):
             nc.vector.tensor_copy(
                 out=y_grouped[:, g].rearrange("p (c i) t -> p c t i", i=4),
                 in_=y_planes[:, g].rearrange("p t (c i) -> p c t i", i=4),
             )
-        for g in range(4):
+
+        def quantise_y(g):
             nc.vector.quantize_mx(
                 out=y_words[:, P * g : P * (g + 1)].bitcast(FP8X4),
                 scales=y_scales[:, P * g : P * (g + 1)],
                 in_=y_grouped[:, g].rearrange("p b t -> p (b t)"),
             )
 
-        nc.scalar.copy(out=fcb[:], in_=fcb_ps[:].rearrange("m (r e) q -> m r q e", e=2))
-        for g in range(4):
-            for half in range(2):
-                transpose_w(g, half)
-            regroup_w(g)
-            quantise_w(g)
+        for g in on_vector + on_scalar:
+            normalise(g)
+            transpose_z(g)
+        quantise_w(1)
+        regroup_w(2)
+        scale_shift(0)
+        scale_shift(2)
+        scale_shift(1)
+        regroup_w(3)
+        scale_shift(3)
+        regroup_y(0)
+        regroup_y(2)
+        quantise_w(2)
+        quantise_y(0)
+        quantise_y(2)
+        regroup_y(1)
+        quantise_w(3)
+        quantise_y(1)
+        regroup_y(3)
+        quantise_y(3)
 
         out_ps = work_banks.tile([P, OUT], F32, tag="work0", name="out_ps")
-        for g in range(4):
+        head_order = on_vector + on_scalar
+        for g in head_order:
             nc.tensor.matmul_mx(
                 out=out_ps[:],
                 lhsT=y_words[:, P * g : P * (g + 1)].bitcast(FP8X4),
                 lhsT_scale=y_scales[:, P * g : P * (g + 1)],
                 rhs=w_words[:, g, :].bitcast(FP8X4),
                 rhs_scale=w_scales[:, g, :],
-                start=(g == 0),
-                stop=(g == 3),
+                start=(g == head_order[0]),
+                stop=(g == head_order[-1]),
             )
         result = keep.tile([P, OUT], F32, name="result")
-        nc.vector.tensor_tensor(out=result[:], in0=out_ps[:], in1=fcb[:].rearrange("m r q e -> m (r q e)"), op=ALU.add)
-        nc.sync.dma_start(out=out.rearrange("b o n -> b (o n)"), in_=result[:])
+        fcb_row = fcb[:].rearrange("m r q e -> m (r q e)")
+        out_rows = out.rearrange("b o n -> b (o n)")
+        for half in range(2):
+            cols = slice(OUT // 2 * half, OUT // 2 * (half + 1))
+            nc.vector.tensor_tensor(out=result[:, cols], in0=out_ps[:, cols], in1=fcb_row[:, cols], op=ALU.add)
+            nc.sync.dma_start(out=out_rows[:, cols], in_=result[:, cols])

@@ -39,7 +39,6 @@ def tile_pinmodel_pa_kernel(tc, x, km1, b1, t2, core2, t3, core3, ln_g, ln_b, fc
     nc = tc.nc
     chunks = core_chunks()
     with ExitStack() as ctx:
-        ctx.enter_context(tc.manual_schedule())
         const = ctx.enter_context(tc.tile_pool(name="const", bufs=1))
         raw = ctx.enter_context(tc.tile_pool(name="raw", bufs=1))
         keep = ctx.enter_context(tc.tile_pool(name="keep", bufs=1))
@@ -84,13 +83,11 @@ def tile_pinmodel_pa_kernel(tc, x, km1, b1, t2, core2, t3, core3, ln_g, ln_b, fc
         nc.sync.dma_start(out=x_raw[:], in_=x.rearrange("b i j -> b (i j)"))
         nc.sync.dma_start(out=km_raw[:], in_=km1.rearrange("i j d -> (i j) d"))
         nc.sync.dma_start(out=b1_row[0:1, :], in_=b1.rearrange("(o d) -> o d", o=1))
-        for j in range(2, 6):
+        for j in range(2, len(chunks)):
             load_chunk(j)
         nc.sync.dma_start(out=vec_rows[0:8, :].bitcast(BF16), in_=ln_g.rearrange("(r c) -> r c", c=256))
         nc.sync.dma_start(out=vec_rows[8:16, :].bitcast(BF16), in_=ln_b.rearrange("(r c) -> r c", c=256))
         nc.sync.dma_start(out=vec_rows[16:18, :].bitcast(BF16), in_=fc_b.rearrange("(r c) -> r c", c=256))
-        for j in range(6, len(chunks)):
-            load_chunk(j)
         for r in range(4):
             nc.sync.dma_start(out=w_raw[r][:], in_=fc_w[P * r : P * (r + 1), :])
 
@@ -108,10 +105,8 @@ def tile_pinmodel_pa_kernel(tc, x, km1, b1, t2, core2, t3, core3, ln_g, ln_b, fc
                     )
             return flipped
 
-        def regroup_t(i, flipped):
+        def quantise_t(i, flipped):
             nc.scalar.copy(out=t_grouped[i][:], in_=flipped[:].rearrange("p c u b -> p c b u"))
-
-        def quantise_t(i):
             nc.vector.quantize_mx(
                 out=t_words[i][:].bitcast(FP8X4),
                 scales=t_scales[i][:],
@@ -199,12 +194,10 @@ def tile_pinmodel_pa_kernel(tc, x, km1, b1, t2, core2, t3, core3, ln_g, ln_b, fc
                 in_=w_grouped[g][:].rearrange("p r n u -> p (r n u)").bitcast(BF16),
             )
 
-        last = len(chunks) - 1
-        regroup(0)
         t_flipped = transpose_t(0)
-        regroup_t(0, t_flipped)
+        quantise_t(0, t_flipped)
+        regroup(0)
         regroup(1)
-        quantise_t(0)
         quantise_multiply(0)
 
         x_flipped = work_banks.tile([P, P], BF16, tag="work3", name="x_flipped")
@@ -212,9 +205,8 @@ def tile_pinmodel_pa_kernel(tc, x, km1, b1, t2, core2, t3, core3, ln_g, ln_b, fc
         t_flipped = transpose_t(1)
         x_t = keep.tile([P, P], BF16, name="x_t")
         nc.vector.tensor_copy(out=x_t[:], in_=x_flipped[:])
-        regroup_t(1, t_flipped)
+        quantise_t(1, t_flipped)
         quantise_multiply(1)
-        quantise_t(1)
         order1_ps = []
         for n in range(N_BANKS):
             acc = work_banks.tile([P, BANK], F32, tag="work%d" % n, name="order1_ps%d" % n)
@@ -222,46 +214,37 @@ def tile_pinmodel_pa_kernel(tc, x, km1, b1, t2, core2, t3, core3, ln_g, ln_b, fc
             nc.tensor.matmul(out=acc[:], lhsT=x_t[:], rhs=km_raw[:, cols], start=True, stop=False)
             nc.tensor.matmul(out=acc[:], lhsT=first_row[:], rhs=b1_row[:, cols], start=False, stop=True)
             order1_ps.append(acc)
-
-        def keep_order1(n):
+        for n in range(N_BANKS):
             nc.scalar.copy(
                 out=order1[:, n].rearrange("b (u e) q -> b u e q", u=2),
                 in_=order1_ps[n][:].rearrange("b (u q e) -> b u e q", u=2, e=2),
             )
+            if n == 1:
+                regroup(2)
 
-        vec_pairs = keep.tile([P, 18], F32, name="vec_pairs")
-        vec_cols = keep.tile([P, 36], F32, name="vec_cols")
-        fcb = keep.tile([P, 2, P, 2], F32, name="fcb")
-        regroup(2)
+        last = len(chunks) - 1
         for j in range(3, last + 1):
-            if j <= 4:
-                keep_order1(2 * (j - 3))
-                keep_order1(2 * (j - 3) + 1)
             regroup(j)
             quantise_multiply(j - 1)
-            if j == 6 or j == 7:
-                close_bank(j - 6)
-            if j == 8:
-                vec_flipped = work_banks.tile([P, P], F32, tag="work2", name="vec_flipped")
-                nc.tensor.transpose(vec_flipped[:], vec_rows[:], ident_f[:])
-                nc.vector.tensor_copy(out=vec_pairs[:], in_=vec_flipped[:, 0:18])
-                nc.vector.tensor_copy(out=vec_cols[:], in_=vec_pairs[:].bitcast(BF16))
-                fcb_ps = work_banks.tile([P, 4, P], F32, tag="work3", name="fcb_ps")
-                for t in range(4):
-                    nc.tensor.transpose(fcb_ps[:, t, :], vec_cols[:, 32 + t : 33 + t].to_broadcast([P, P]), ident_f[:])
+            if j == 6:
+                close_bank(0)
+            if j == 7:
+                close_bank(1)
 
-        nc.scalar.copy(out=fcb[:], in_=fcb_ps[:].rearrange("m (r e) q -> m r q e", e=2))
-        transpose_w(0, 0)
-        transpose_w(0, 1)
-        transpose_w(1, 0)
+        vec_flipped = work_banks.tile([P, P], F32, tag="work2", name="vec_flipped")
+        nc.tensor.transpose(vec_flipped[:], vec_rows[:], ident_f[:])
+        vec_pairs = keep.tile([P, 18], F32, name="vec_pairs")
+        nc.vector.tensor_copy(out=vec_pairs[:], in_=vec_flipped[:, 0:18])
+        vec_cols = keep.tile([P, 36], F32, name="vec_cols")
+        nc.vector.tensor_copy(out=vec_cols[:], in_=vec_pairs[:].bitcast(BF16))
+        fcb_ps = work_banks.tile([P, 4, P], F32, tag="work0", name="fcb_ps")
+        for t in range(4):
+            nc.tensor.transpose(fcb_ps[:, t, :], vec_cols[:, 32 + t : 33 + t].to_broadcast([P, P]), ident_f[:])
+        fcb = keep.tile([P, 2, P, 2], F32, name="fcb")
         quantise_multiply(last)
-        transpose_w(1, 1)
-        regroup_w(0)
         close_bank(2)
-        regroup_w(1)
-        transpose_w(2, 0)
-        transpose_w(2, 1)
         close_bank(3)
+
         mean_var = keep.tile([P, 2], F32, name="mean_var")
         nc.vector.bn_aggr(out=mean_var[:], in_=stats[:].rearrange("b n s -> b (n s)"))
         rstd = keep.tile([P, 1], F32, name="rstd")
@@ -270,20 +253,14 @@ def tile_pinmodel_pa_kernel(tc, x, km1, b1, t2, core2, t3, core3, ln_g, ln_b, fc
         nc.vector.tensor_scalar_mul(out=neg_mean[:], in0=mean_var[:, 0:1], scalar1=-1.0)
         shift = keep.tile([P, 1], F32, name="shift")
         nc.scalar.activation(out=shift[:], in_=neg_mean[:], func=ACT.Identity, scale=rstd[:])
-        quantise_w(0)
-        transpose_w(3, 0)
-        transpose_w(3, 1)
 
         y_planes = keep.tile([P, 4, PACK, P], BF16, name="y_planes")
         y_grouped = keep.tile([P, 4, P, PACK], BF16, name="y_grouped", align_bytes=64)
         y_words = keep.tile([P, 4 * P], U32, name="y_words", align_bytes=64)
         y_scales = keep.tile([P, 4 * P], U8, name="y_scales", align_bytes=64)
-        z_flipped = {}
-        on_vector = (0, 2)
-        on_scalar = (1, 3)
-
-        def normalise(g):
-            if g in on_vector:
+        z_flipped = []
+        for g in range(4):
+            if g % 2 == 0:
                 nc.vector.tensor_scalar(
                     out=z_sb[:, g],
                     in0=o_sb[:, g],
@@ -294,17 +271,14 @@ def tile_pinmodel_pa_kernel(tc, x, km1, b1, t2, core2, t3, core3, ln_g, ln_b, fc
                 )
             else:
                 nc.scalar.activation(out=z_sb[:, g], in_=o_sb[:, g], func=ACT.Identity, bias=shift[:], scale=rstd[:])
-
-        def transpose_z(g):
             flipped = o_banks.tile([P, PACK, P], F32, name="z_flipped%d" % g, tag="o%d" % g)
             for t in range(PACK):
                 nc.tensor.transpose(flipped[:, t, :], z_sb[:, g, t, :], ident_f[:])
-            z_flipped[g] = flipped
-
-        def scale_shift(g):
+            z_flipped.append(flipped)
+        for g in range(4):
             for t in range(PACK):
                 k = PACK * g + t
-                if g in on_vector:
+                if g % 2 == 0:
                     nc.vector.tensor_scalar(
                         out=y_planes[:, g, t, :],
                         in0=z_flipped[g][:, t, :],
@@ -321,52 +295,35 @@ def tile_pinmodel_pa_kernel(tc, x, km1, b1, t2, core2, t3, core3, ln_g, ln_b, fc
                         bias=vec_cols[:, 16 + k : 17 + k],
                         scale=vec_cols[:, k : k + 1],
                     )
-
-        def regroup_y(g):
+        for g in range(4):
             nc.vector.tensor_copy(
                 out=y_grouped[:, g].rearrange("p (c i) t -> p c t i", i=4),
                 in_=y_planes[:, g].rearrange("p t (c i) -> p c t i", i=4),
             )
-
-        def quantise_y(g):
+        for g in range(4):
             nc.vector.quantize_mx(
                 out=y_words[:, P * g : P * (g + 1)].bitcast(FP8X4),
                 scales=y_scales[:, P * g : P * (g + 1)],
                 in_=y_grouped[:, g].rearrange("p b t -> p (b t)"),
             )
 
-        for g in on_vector + on_scalar:
-            normalise(g)
-            transpose_z(g)
-        quantise_w(1)
-        regroup_w(2)
-        scale_shift(0)
-        scale_shift(2)
-        scale_shift(1)
-        regroup_w(3)
-        scale_shift(3)
-        regroup_y(0)
-        regroup_y(2)
-        quantise_w(2)
-        quantise_y(0)
-        quantise_y(2)
-        regroup_y(1)
-        quantise_w(3)
-        quantise_y(1)
-        regroup_y(3)
-        quantise_y(3)
+        nc.scalar.copy(out=fcb[:], in_=fcb_ps[:].rearrange("m (r e) q -> m r q e", e=2))
+        for g in range(4):
+            for half in range(2):
+                transpose_w(g, half)
+            regroup_w(g)
+            quantise_w(g)
 
         out_ps = work_banks.tile([P, OUT], F32, tag="work0", name="out_ps")
-        head_order = on_vector + on_scalar
-        for g in head_order:
+        for g in range(4):
             nc.tensor.matmul_mx(
                 out=out_ps[:],
                 lhsT=y_words[:, P * g : P * (g + 1)].bitcast(FP8X4),
                 lhsT_scale=y_scales[:, P * g : P * (g + 1)],
                 rhs=w_words[:, g, :].bitcast(FP8X4),
                 rhs_scale=w_scales[:, g, :],
-                start=(g == head_order[0]),
-                stop=(g == head_order[-1]),
+                start=(g == 0),
+                stop=(g == 3),
             )
         result = keep.tile([P, OUT], F32, name="result")
         fcb_row = fcb[:].rearrange("m r q e -> m (r q e)")

@@ -20,7 +20,7 @@ OUT = 512
 BANK = 512
 N_BANKS = D // BANK
 EPS = 1e-5
-V_SHARE = (15, 32)
+PIECE = 256
 
 FLOPS = 2 * 128 * 2048 * (128 + 1024 + 1024) + 2 * 128 * 512 * 2048
 
@@ -118,16 +118,12 @@ def tile_pinmodel_pa_kernel(tc, x, km1, b1, t2, core2, t3, core3, ln_g, ln_b, fc
 
         def regroup(j):
             width = BANK * chunks[j][3]
-            split = width * V_SHARE[0] // V_SHARE[1]
             tile_j = grouped_pool.tile([P, width, PACK], BF16, tag="grouped", name="grouped%d" % j, align_bytes=64)
-            nc.vector.tensor_copy(
-                out=tile_j[:, 0:split, :].rearrange("p (c i) t -> p c t i", i=4),
-                in_=core_raw[j][:, :, 0:split].rearrange("p t (c i) -> p c t i", i=4),
-            )
-            nc.scalar.copy(
-                out=tile_j[:, split:width, :].rearrange("p (c i) t -> p c t i", i=4),
-                in_=core_raw[j][:, :, split:width].rearrange("p t (c i) -> p c t i", i=4),
-            )
+            for lo in range(0, width, PIECE):
+                nc.any.tensor_copy(
+                    out=tile_j[:, lo : lo + PIECE, :].rearrange("p (c i) t -> p c t i", i=4),
+                    in_=core_raw[j][:, :, lo : lo + PIECE].rearrange("p t (c i) -> p c t i", i=4),
+                )
             grouped[j] = tile_j
 
         def quantise_multiply(j):

@@ -20,38 +20,58 @@ OUT = 512
 BANK = 512
 N_BANKS = D // BANK
 EPS = 1e-5
-PIECE = 256
+RUN = 8
 
 FLOPS = 2 * 128 * 2048 * (128 + 1024 + 1024) + 2 * 128 * 512 * 2048
 
-
-def core_chunks():
-    chunks = [(core, kpass, 2 * half, 2) for half in range(2) for core in range(2) for kpass in range(2)]
-    head, tail = chunks[0], chunks[-1]
-    return (
-        [(head[0], head[1], head[2] + b, 1) for b in range(2)]
-        + chunks[1:-1]
-        + [(tail[0], tail[1], tail[2] + b, 1) for b in range(2)]
-    )
-
+LOADS = [
+    (0, 0, 512),
+    (0, 512, 512),
+    (1, 512, 512),
+    (1, 0, 512),
+    (2, 0, 1024),
+    (3, 0, 1024),
+    (0, 1024, 1024),
+    (1, 1024, 1024),
+    (2, 1024, 1024),
+    (3, 1024, 512),
+    (3, 1536, 512),
+]
+PIECES = [
+    (0, 0, 256),
+    (1, 0, 256),
+    (2, 0, 0),
+    (3, 0, 512),
+    (4, 0, 512),
+    (4, 512, 0),
+    (5, 0, 512),
+    (5, 512, 0),
+    (6, 0, 512),
+    (6, 512, 0),
+    (7, 0, 512),
+    (7, 512, 0),
+    (8, 0, 512),
+    (8, 512, 0),
+    (9, 0, 0),
+    (10, 0, 256),
+]
 
 def tile_pinmodel_pa_kernel(tc, x, km1, b1, t2, core2, t3, core3, ln_g, ln_b, fc_w, fc_b, out):
     nc = tc.nc
-    chunks = core_chunks()
     with ExitStack() as ctx:
         const = ctx.enter_context(tc.tile_pool(name="const", bufs=1))
         raw = ctx.enter_context(tc.tile_pool(name="raw", bufs=1))
         keep = ctx.enter_context(tc.tile_pool(name="keep", bufs=1))
-        grouped_pool = ctx.enter_context(tc.tile_pool(name="grouped_pool", bufs=4))
-        w_grouped_pool = ctx.enter_context(tc.tile_pool(name="w_grouped_pool", bufs=2))
+        grouped_pool = ctx.enter_context(tc.tile_pool(name="grouped_pool", bufs=6))
         o_banks = ctx.enter_context(tc.psum_pool(name="o_banks", bufs=1))
         work_banks = ctx.enter_context(tc.psum_pool(name="work_banks", bufs=1))
 
         t_raw = [raw.tile([P, KR], BF16, name="t_raw%d" % i) for i in range(2)]
-        core_raw = [raw.tile([P, PACK, BANK * ch[3]], BF16, name="core_raw%d" % j) for j, ch in enumerate(chunks)]
+        core_raw = [raw.tile([P, PACK, load[2]], BF16, name="core_raw%d" % i) for i, load in enumerate(LOADS)]
         x_raw = raw.tile([P, P], BF16, name="x_raw")
         km_raw = raw.tile([P, D], BF16, name="km_raw")
         w_raw = [raw.tile([P, D], BF16, name="w_raw%d" % r) for r in range(4)]
+        fcb = raw.tile([P, OUT], BF16, name="fcb")
 
         eps = const.tile([P, 1], F32, name="eps")
         nc.vector.memset(eps[:], EPS)
@@ -71,29 +91,40 @@ def tile_pinmodel_pa_kernel(tc, x, km1, b1, t2, core2, t3, core3, ln_g, ln_b, fc
 
         cores = [core2.rearrange("r q d -> (r q) d"), core3.rearrange("r q d -> (r q) d")]
 
-        def load_chunk(j):
-            core, kpass, bank0, banks = chunks[j]
-            rows = cores[core][K_PASS * kpass : K_PASS * (kpass + 1), BANK * bank0 : BANK * (bank0 + banks)]
-            nc.sync.dma_start(out=core_raw[j][:], in_=rows.rearrange("(p j) d -> p j d", j=PACK))
+        def load_core(i):
+            kpass, col, width = LOADS[i]
+            first = K_PASS * (kpass % 2)
+            rows = cores[kpass // 2][first : first + K_PASS, col : col + width]
+            nc.sync.dma_start(out=core_raw[i][:], in_=rows.rearrange("(p j) d -> p j d", j=PACK))
 
-        load_chunk(0)
+        load_core(0)
+        load_core(1)
         nc.sync.dma_start(out=t_raw[0][:], in_=t2.rearrange("b r q -> b (r q)"))
-        load_chunk(1)
+        load_core(2)
+        load_core(3)
+        load_core(4)
         nc.sync.dma_start(out=t_raw[1][:], in_=t3.rearrange("b r q -> b (r q)"))
         nc.sync.dma_start(out=x_raw[:], in_=x.rearrange("b i j -> b (i j)"))
+        load_core(5)
         nc.sync.dma_start(out=km_raw[:], in_=km1.rearrange("i j d -> (i j) d"))
         nc.sync.dma_start(out=b1_row[0:1, :], in_=b1.rearrange("(o d) -> o d", o=1))
-        for j in range(2, len(chunks)):
-            load_chunk(j)
+        load_core(6)
+        load_core(7)
         nc.sync.dma_start(out=vec_rows[0:8, :].bitcast(BF16), in_=ln_g.rearrange("(r c) -> r c", c=256))
         nc.sync.dma_start(out=vec_rows[8:16, :].bitcast(BF16), in_=ln_b.rearrange("(r c) -> r c", c=256))
-        nc.sync.dma_start(out=vec_rows[16:18, :].bitcast(BF16), in_=fc_b.rearrange("(r c) -> r c", c=256))
-        for r in range(4):
-            nc.sync.dma_start(out=w_raw[r][:], in_=fc_w[P * r : P * (r + 1), :])
+        load_core(8)
+        load_core(9)
+        load_core(10)
+        nc.sync.dma_start(out=w_raw[0][:], in_=fc_w[P * 0 : P * 1, :])
+        nc.sync.dma_start(out=w_raw[1][:], in_=fc_w[P * 1 : P * 2, :])
+        nc.sync.dma_start(out=w_raw[2][:], in_=fc_w[P * 2 : P * 3, :])
+        nc.sync.dma_start(out=w_raw[3][:], in_=fc_w[P * 3 : P * 4, :])
+        nc.sync.dma_start(out=fcb[:], in_=fc_b.partition_broadcast(P))
 
         t_words = [keep.tile([P, 2 * P], U32, name="t_words%d" % i, align_bytes=64) for i in range(2)]
         t_scales = [keep.tile([P, 2 * P], U8, name="t_scales%d" % i, align_bytes=64) for i in range(2)]
         t_grouped = [keep.tile([P, 2, P, 2], F32, name="t_grouped%d" % i, align_bytes=64) for i in range(2)]
+        t_flipped = {}
 
         def transpose_t(i):
             pairs = t_raw[i][:].bitcast(F32)
@@ -103,10 +134,12 @@ def tile_pinmodel_pa_kernel(tc, x, km1, b1, t2, core2, t3, core3, ln_g, ln_b, fc
                     nc.tensor.transpose(
                         flipped[:, kpass, u, :], pairs[:, 256 * kpass + u : 256 * (kpass + 1) : 2], ident_f[:]
                     )
-            return flipped
+            t_flipped[i] = flipped
 
-        def quantise_t(i, flipped):
-            nc.scalar.copy(out=t_grouped[i][:], in_=flipped[:].rearrange("p c u b -> p c b u"))
+        def empty_t(i):
+            nc.scalar.copy(out=t_grouped[i][:], in_=t_flipped[i][:].rearrange("p c u b -> p c b u"))
+
+        def quantise_t(i):
             nc.vector.quantize_mx(
                 out=t_words[i][:].bitcast(FP8X4),
                 scales=t_scales[i][:],
@@ -115,54 +148,86 @@ def tile_pinmodel_pa_kernel(tc, x, km1, b1, t2, core2, t3, core3, ln_g, ln_b, fc
 
         o_ps = [o_banks.tile([P, BANK], F32, name="o_ps%d" % n, tag="o%d" % n) for n in range(N_BANKS)]
         grouped = {}
+        core_words = {}
+        core_scales = {}
 
         def regroup(j):
-            width = BANK * chunks[j][3]
-            tile_j = grouped_pool.tile([P, width, PACK], BF16, tag="grouped", name="grouped%d" % j, align_bytes=64)
-            for lo in range(0, width, PIECE):
-                nc.any.tensor_copy(
-                    out=tile_j[:, lo : lo + PIECE, :].rearrange("p (c i) t -> p c t i", i=4),
-                    in_=core_raw[j][:, :, lo : lo + PIECE].rearrange("p t (c i) -> p c t i", i=4),
-                )
+            load, col, cut = PIECES[j]
+            tile_j = grouped_pool.tile([P, BANK, PACK], BF16, tag="grouped", name="grouped%d" % j, align_bytes=64)
+            for copy, lo, hi in ((nc.vector.tensor_copy, 0, cut), (nc.scalar.copy, cut, BANK)):
+                if lo < hi:
+                    copy(
+                        out=tile_j[:, lo:hi, :].rearrange("p (c i) t -> p c t i", i=RUN),
+                        in_=core_raw[load][:, :, col + lo : col + hi].rearrange("p t (c i) -> p c t i", i=RUN),
+                    )
             grouped[j] = tile_j
 
-        def quantise_multiply(j):
-            core, kpass, bank0, banks = chunks[j]
-            width = BANK * banks
-            words = keep.tile([P, width], U32, name="core_words%d" % j, align_bytes=64)
-            scales = keep.tile([P, width], U8, name="core_scales%d" % j, align_bytes=64)
+        def quantise(j):
+            core_words[j] = keep.tile([P, BANK], U32, name="core_words%d" % j, align_bytes=64)
+            core_scales[j] = keep.tile([P, BANK], U8, name="core_scales%d" % j, align_bytes=64)
             nc.vector.quantize_mx(
-                out=words[:].bitcast(FP8X4), scales=scales[:], in_=grouped[j][:].rearrange("p w j -> p (w j)")
+                out=core_words[j][:].bitcast(FP8X4),
+                scales=core_scales[j][:],
+                in_=grouped[j][:].rearrange("p w j -> p (w j)"),
             )
-            for b in range(banks):
-                nc.tensor.matmul_mx(
-                    out=o_ps[bank0 + b][:],
-                    lhsT=t_words[core][:, P * kpass : P * (kpass + 1)].bitcast(FP8X4),
-                    lhsT_scale=t_scales[core][:, P * kpass : P * (kpass + 1)],
-                    rhs=words[:, BANK * b : BANK * (b + 1)].bitcast(FP8X4),
-                    rhs_scale=scales[:, BANK * b : BANK * (b + 1)],
-                    start=(core == 0 and kpass == 0),
-                    stop=(core == 1 and kpass == 1),
-                )
+
+        def multiply(j):
+            load, col, cut = PIECES[j]
+            kpass, first_col, width = LOADS[load]
+            t_cols = slice(P * (kpass % 2), P * (kpass % 2 + 1))
+            nc.tensor.matmul_mx(
+                out=o_ps[(first_col + col) // BANK][:],
+                lhsT=t_words[kpass // 2][:, t_cols].bitcast(FP8X4),
+                lhsT_scale=t_scales[kpass // 2][:, t_cols],
+                rhs=core_words[j][:].bitcast(FP8X4),
+                rhs_scale=core_scales[j][:],
+                start=(kpass == 0),
+                stop=(kpass == 3),
+            )
 
         order1 = keep.tile([P, N_BANKS, PACK, P], F32, name="order1")
         o_sb = keep.tile([P, N_BANKS, PACK, P], F32, name="o_sb")
         z_sb = keep.tile([P, N_BANKS, PACK, P], F32, name="z_sb")
         stats = keep.tile([P, N_BANKS, 6], F32, name="stats")
+        x_t = keep.tile([P, P], BF16, name="x_t")
+        order1_ps = {}
+        x_flipped = []
 
-        def close_bank(n):
+        def transpose_x():
+            x_flipped.append(work_banks.tile([P, P], BF16, tag="work3", name="x_flipped"))
+            nc.tensor.transpose(x_flipped[0][:], x_raw[:], ident_b[:])
+
+        def empty_x():
+            nc.vector.tensor_copy(out=x_t[:], in_=x_flipped[0][:])
+
+        def multiply_order1(n):
+            acc = work_banks.tile([P, BANK], F32, tag="work%d" % n, name="order1_ps%d" % n)
+            cols = slice(BANK * n, BANK * (n + 1))
+            nc.tensor.matmul(out=acc[:], lhsT=x_t[:], rhs=km_raw[:, cols], start=True, stop=False)
+            nc.tensor.matmul(out=acc[:], lhsT=first_row[:], rhs=b1_row[:, cols], start=False, stop=True)
+            order1_ps[n] = acc
+
+        def empty_order1(n):
+            nc.scalar.copy(
+                out=order1[:, n].rearrange("b (u e) q -> b u e q", u=2),
+                in_=order1_ps[n][:].rearrange("b (u q e) -> b u e q", u=2, e=2),
+            )
+
+        def add_bank(n):
             nc.vector.tensor_tensor(
                 out=o_sb[:, n].rearrange("b (u e) q -> b u e q", u=2),
                 in0=o_ps[n][:].rearrange("b (u q e) -> b u e q", u=2, e=2),
                 in1=order1[:, n].rearrange("b (u e) q -> b u e q", u=2),
                 op=ALU.add,
             )
+
+        def bank_stats(n):
             nc.vector.bn_stats(out=stats[:, n, :], in_=o_sb[:, n].rearrange("b t q -> b (t q)"))
 
         w_words = keep.tile([P, 4, OUT], U32, name="w_words", align_bytes=64)
         w_scales = keep.tile([P, 4, OUT], U8, name="w_scales", align_bytes=64)
+        w_grouped = [keep.tile([P, 4, P, 2], F32, name="w_grouped%d" % g, align_bytes=64) for g in range(4)]
         w_flipped = {}
-        w_grouped = {}
 
         def transpose_w(g, half):
             flipped = work_banks.tile(
@@ -175,13 +240,11 @@ def tile_pinmodel_pa_kernel(tc, x, km1, b1, t2, core2, t3, core3, ln_g, ln_b, fc
                     nc.tensor.transpose(flipped[:, r, u, :], pairs[:, first : first + P], ident_f[:])
             w_flipped[g, half] = flipped
 
-        def regroup_w(g):
-            w_grouped[g] = w_grouped_pool.tile([P, 4, P, 2], F32, tag="w_grouped", name="w_grouped%d" % g, align_bytes=64)
-            for half in range(2):
-                nc.scalar.copy(
-                    out=w_grouped[g][:, 2 * half : 2 * half + 2],
-                    in_=w_flipped[g, half][:].rearrange("p r u n -> p r n u"),
-                )
+        def empty_w(g, half):
+            nc.scalar.copy(
+                out=w_grouped[g][:, 2 * half : 2 * half + 2],
+                in_=w_flipped[g, half][:].rearrange("p r u n -> p r n u"),
+            )
 
         def quantise_w(g):
             nc.vector.quantize_mx(
@@ -190,130 +253,106 @@ def tile_pinmodel_pa_kernel(tc, x, km1, b1, t2, core2, t3, core3, ln_g, ln_b, fc
                 in_=w_grouped[g][:].rearrange("p r n u -> p (r n u)").bitcast(BF16),
             )
 
-        t_flipped = transpose_t(0)
-        quantise_t(0, t_flipped)
-        regroup(0)
-        regroup(1)
-        quantise_multiply(0)
-
-        x_flipped = work_banks.tile([P, P], BF16, tag="work3", name="x_flipped")
-        nc.tensor.transpose(x_flipped[:], x_raw[:], ident_b[:])
-        t_flipped = transpose_t(1)
-        x_t = keep.tile([P, P], BF16, name="x_t")
-        nc.vector.tensor_copy(out=x_t[:], in_=x_flipped[:])
-        quantise_t(1, t_flipped)
-        quantise_multiply(1)
-        order1_ps = []
-        for n in range(N_BANKS):
-            acc = work_banks.tile([P, BANK], F32, tag="work%d" % n, name="order1_ps%d" % n)
-            cols = slice(BANK * n, BANK * (n + 1))
-            nc.tensor.matmul(out=acc[:], lhsT=x_t[:], rhs=km_raw[:, cols], start=True, stop=False)
-            nc.tensor.matmul(out=acc[:], lhsT=first_row[:], rhs=b1_row[:, cols], start=False, stop=True)
-            order1_ps.append(acc)
-        for n in range(N_BANKS):
-            nc.scalar.copy(
-                out=order1[:, n].rearrange("b (u e) q -> b u e q", u=2),
-                in_=order1_ps[n][:].rearrange("b (u q e) -> b u e q", u=2, e=2),
-            )
-            if n == 1:
-                regroup(2)
-
-        last = len(chunks) - 1
-        for j in range(3, last + 1):
-            regroup(j)
-            quantise_multiply(j - 1)
-            if j == 6:
-                close_bank(0)
-            if j == 7:
-                close_bank(1)
-
-        vec_flipped = work_banks.tile([P, P], F32, tag="work2", name="vec_flipped")
-        nc.tensor.transpose(vec_flipped[:], vec_rows[:], ident_f[:])
-        vec_pairs = keep.tile([P, 18], F32, name="vec_pairs")
-        nc.vector.tensor_copy(out=vec_pairs[:], in_=vec_flipped[:, 0:18])
-        vec_cols = keep.tile([P, 36], F32, name="vec_cols")
-        nc.vector.tensor_copy(out=vec_cols[:], in_=vec_pairs[:].bitcast(BF16))
-        fcb_ps = work_banks.tile([P, 4, P], F32, tag="work0", name="fcb_ps")
-        for t in range(4):
-            nc.tensor.transpose(fcb_ps[:, t, :], vec_cols[:, 32 + t : 33 + t].to_broadcast([P, P]), ident_f[:])
-        fcb = keep.tile([P, 2, P, 2], F32, name="fcb")
-        quantise_multiply(last)
-        close_bank(2)
-        close_bank(3)
-
         mean_var = keep.tile([P, 2], F32, name="mean_var")
-        nc.vector.bn_aggr(out=mean_var[:], in_=stats[:].rearrange("b n s -> b (n s)"))
         rstd = keep.tile([P, 1], F32, name="rstd")
-        nc.scalar.activation(out=rstd[:], in_=mean_var[:, 1:2], func=ACT.Abs_reciprocal_sqrt, bias=eps[:], scale=1.0)
         neg_mean = keep.tile([P, 1], F32, name="neg_mean")
-        nc.vector.tensor_scalar_mul(out=neg_mean[:], in0=mean_var[:, 0:1], scalar1=-1.0)
         shift = keep.tile([P, 1], F32, name="shift")
-        nc.scalar.activation(out=shift[:], in_=neg_mean[:], func=ACT.Identity, scale=rstd[:])
-
+        vec_pairs = keep.tile([P, 16], F32, name="vec_pairs")
+        vec_cols = keep.tile([P, 32], F32, name="vec_cols")
         y_planes = keep.tile([P, 4, PACK, P], BF16, name="y_planes")
         y_grouped = keep.tile([P, 4, P, PACK], BF16, name="y_grouped", align_bytes=64)
         y_words = keep.tile([P, 4 * P], U32, name="y_words", align_bytes=64)
         y_scales = keep.tile([P, 4 * P], U8, name="y_scales", align_bytes=64)
-        z_flipped = []
-        for g in range(4):
-            if g % 2 == 0:
-                nc.vector.tensor_scalar(
-                    out=z_sb[:, g],
-                    in0=o_sb[:, g],
-                    scalar1=mean_var[:, 0:1],
-                    scalar2=rstd[:],
-                    op0=ALU.subtract,
-                    op1=ALU.mult,
-                )
-            else:
-                nc.scalar.activation(out=z_sb[:, g], in_=o_sb[:, g], func=ACT.Identity, bias=shift[:], scale=rstd[:])
-            flipped = o_banks.tile([P, PACK, P], F32, name="z_flipped%d" % g, tag="o%d" % g)
+        z_flipped = {}
+        vec_flipped = []
+
+        def transpose_vectors():
+            vec_flipped.append(work_banks.tile([P, P], F32, tag="work2", name="vec_flipped"))
+            nc.tensor.transpose(vec_flipped[0][:], vec_rows[:], ident_f[:])
+
+        def empty_vectors():
+            nc.vector.tensor_copy(out=vec_pairs[:], in_=vec_flipped[0][:, 0:16])
+
+        def widen_vectors():
+            nc.vector.tensor_copy(out=vec_cols[:], in_=vec_pairs[:].bitcast(BF16))
+
+        def aggregate():
+            nc.vector.bn_aggr(out=mean_var[:], in_=stats[:].rearrange("b n s -> b (n s)"))
+
+        def inverse_deviation():
+            nc.scalar.activation(
+                out=rstd[:], in_=mean_var[:, 1:2], func=ACT.Abs_reciprocal_sqrt, bias=eps[:], scale=1.0
+            )
+
+        def negate_mean():
+            nc.vector.tensor_scalar_mul(out=neg_mean[:], in0=mean_var[:, 0:1], scalar1=-1.0)
+
+        def scale_shift():
+            nc.scalar.activation(out=shift[:], in_=neg_mean[:], func=ACT.Identity, scale=rstd[:])
+
+        def normalise_on_vector(g):
+            nc.vector.tensor_scalar(
+                out=z_sb[:, g],
+                in0=o_sb[:, g],
+                scalar1=mean_var[:, 0:1],
+                scalar2=rstd[:],
+                op0=ALU.subtract,
+                op1=ALU.mult,
+            )
+
+        def normalise_on_scalar(g):
+            nc.scalar.activation(out=z_sb[:, g], in_=o_sb[:, g], func=ACT.Identity, bias=shift[:], scale=rstd[:])
+
+        def transpose_z(g):
+            z_flipped[g] = o_banks.tile([P, PACK, P], F32, name="z_flipped%d" % g, tag="o%d" % g)
             for t in range(PACK):
-                nc.tensor.transpose(flipped[:, t, :], z_sb[:, g, t, :], ident_f[:])
-            z_flipped.append(flipped)
-        for g in range(4):
+                nc.tensor.transpose(z_flipped[g][:, t, :], z_sb[:, g, t, :], ident_f[:])
+
+        def affine_on_vector(g):
             for t in range(PACK):
                 k = PACK * g + t
-                if g % 2 == 0:
-                    nc.vector.tensor_scalar(
-                        out=y_planes[:, g, t, :],
-                        in0=z_flipped[g][:, t, :],
-                        scalar1=vec_cols[:, k : k + 1],
-                        scalar2=vec_cols[:, 16 + k : 17 + k],
-                        op0=ALU.mult,
-                        op1=ALU.add,
-                    )
-                else:
-                    nc.scalar.activation(
-                        out=y_planes[:, g, t, :],
-                        in_=z_flipped[g][:, t, :],
-                        func=ACT.Identity,
-                        bias=vec_cols[:, 16 + k : 17 + k],
-                        scale=vec_cols[:, k : k + 1],
-                    )
-        for g in range(4):
+                nc.vector.tensor_scalar(
+                    out=y_planes[:, g, t, :],
+                    in0=z_flipped[g][:, t, :],
+                    scalar1=vec_cols[:, k : k + 1],
+                    scalar2=vec_cols[:, 16 + k : 17 + k],
+                    op0=ALU.mult,
+                    op1=ALU.add,
+                )
+
+        def affine_on_scalar(g):
+            for t in range(PACK):
+                k = PACK * g + t
+                nc.scalar.activation(
+                    out=y_planes[:, g, t, :],
+                    in_=z_flipped[g][:, t, :],
+                    func=ACT.Identity,
+                    bias=vec_cols[:, 16 + k : 17 + k],
+                    scale=vec_cols[:, k : k + 1],
+                )
+
+        def regroup_y(g):
             nc.vector.tensor_copy(
-                out=y_grouped[:, g].rearrange("p (c i) t -> p c t i", i=4),
-                in_=y_planes[:, g].rearrange("p t (c i) -> p c t i", i=4),
+                out=y_grouped[:, g].rearrange("p (c i) t -> p c t i", i=RUN),
+                in_=y_planes[:, g].rearrange("p t (c i) -> p c t i", i=RUN),
             )
-        for g in range(4):
+
+        def quantise_y(g):
             nc.vector.quantize_mx(
                 out=y_words[:, P * g : P * (g + 1)].bitcast(FP8X4),
                 scales=y_scales[:, P * g : P * (g + 1)],
                 in_=y_grouped[:, g].rearrange("p b t -> p (b t)"),
             )
 
-        nc.scalar.copy(out=fcb[:], in_=fcb_ps[:].rearrange("m (r e) q -> m r q e", e=2))
-        for g in range(4):
-            for half in range(2):
-                transpose_w(g, half)
-            regroup_w(g)
-            quantise_w(g)
+        out_ps = []
+        result = keep.tile([P, OUT], F32, name="result")
+        out_rows = out.rearrange("b o n -> b (o n)")
 
-        out_ps = work_banks.tile([P, OUT], F32, tag="work0", name="out_ps")
-        for g in range(4):
+        def multiply_y(g):
+            if g == 0:
+                out_ps.append(work_banks.tile([P, OUT], F32, tag="work0", name="out_ps"))
             nc.tensor.matmul_mx(
-                out=out_ps[:],
+                out=out_ps[0][:],
                 lhsT=y_words[:, P * g : P * (g + 1)].bitcast(FP8X4),
                 lhsT_scale=y_scales[:, P * g : P * (g + 1)],
                 rhs=w_words[:, g, :].bitcast(FP8X4),
@@ -321,10 +360,135 @@ def tile_pinmodel_pa_kernel(tc, x, km1, b1, t2, core2, t3, core3, ln_g, ln_b, fc
                 start=(g == 0),
                 stop=(g == 3),
             )
-        result = keep.tile([P, OUT], F32, name="result")
-        fcb_row = fcb[:].rearrange("m r q e -> m (r q e)")
-        out_rows = out.rearrange("b o n -> b (o n)")
-        for half in range(2):
+
+        def finish(half):
             cols = slice(OUT // 2 * half, OUT // 2 * (half + 1))
-            nc.vector.tensor_tensor(out=result[:, cols], in0=out_ps[:, cols], in1=fcb_row[:, cols], op=ALU.add)
+            nc.vector.tensor_tensor(out=result[:, cols], in0=out_ps[0][:, cols], in1=fcb[:, cols], op=ALU.add)
             nc.sync.dma_start(out=out_rows[:, cols], in_=result[:, cols])
+
+        ctx.enter_context(tc.manual_schedule())
+        regroup(0)
+        regroup(1)
+        quantise(0)
+        transpose_t(0)
+        empty_t(0)
+        quantise(1)
+        regroup(2)
+        quantise_t(0)
+        multiply(0)
+        multiply(1)
+        regroup(3)
+        quantise(2)
+        multiply(2)
+        quantise(3)
+        multiply(3)
+        regroup(4)
+        regroup(5)
+        transpose_t(1)
+        transpose_x()
+        empty_x()
+        quantise(4)
+        empty_t(1)
+        multiply_order1(0)
+        multiply_order1(1)
+        multiply_order1(2)
+        multiply_order1(3)
+        quantise(5)
+        regroup(6)
+        quantise_t(1)
+        multiply(4)
+        multiply(5)
+        regroup(7)
+        quantise(6)
+        multiply(6)
+        empty_order1(0)
+        empty_order1(1)
+        quantise(7)
+        multiply(7)
+        regroup(8)
+        regroup(9)
+        add_bank(0)
+        quantise(8)
+        multiply(8)
+        regroup(10)
+        regroup(11)
+        add_bank(1)
+        quantise(9)
+        multiply(9)
+        quantise(10)
+        multiply(10)
+        bank_stats(0)
+        empty_order1(2)
+        empty_order1(3)
+        regroup(12)
+        regroup(13)
+        transpose_vectors()
+        bank_stats(1)
+        quantise(11)
+        empty_vectors()
+        multiply(11)
+        quantise(12)
+        multiply(12)
+        regroup(14)
+        quantise(13)
+        multiply(13)
+        regroup(15)
+        quantise(14)
+        multiply(14)
+        transpose_w(0, 0)
+        quantise(15)
+        multiply(15)
+        transpose_w(0, 1)
+        empty_w(0, 0)
+        transpose_w(1, 0)
+        transpose_w(1, 1)
+        add_bank(2)
+        empty_w(0, 1)
+        add_bank(3)
+        empty_w(1, 0)
+        empty_w(1, 1)
+        transpose_w(2, 0)
+        transpose_w(2, 1)
+        transpose_w(3, 0)
+        transpose_w(3, 1)
+        bank_stats(2)
+        bank_stats(3)
+        widen_vectors()
+        aggregate()
+        inverse_deviation()
+        negate_mean()
+        scale_shift()
+        normalise_on_vector(0)
+        transpose_z(0)
+        normalise_on_scalar(1)
+        transpose_z(1)
+        normalise_on_vector(2)
+        normalise_on_vector(3)
+        transpose_z(2)
+        transpose_z(3)
+        quantise_w(0)
+        empty_w(2, 0)
+        affine_on_scalar(0)
+        quantise_w(1)
+        affine_on_scalar(1)
+        empty_w(2, 1)
+        affine_on_scalar(2)
+        affine_on_scalar(3)
+        empty_w(3, 0)
+        empty_w(3, 1)
+        regroup_y(0)
+        regroup_y(1)
+        quantise_y(0)
+        quantise_w(2)
+        quantise_y(1)
+        regroup_y(2)
+        regroup_y(3)
+        quantise_y(2)
+        quantise_w(3)
+        quantise_y(3)
+        multiply_y(0)
+        multiply_y(1)
+        multiply_y(2)
+        multiply_y(3)
+        finish(0)
+        finish(1)

@@ -38,22 +38,16 @@ LOADS = [
     (3, 1536, 512),
 ]
 PIECES = [
-    (0, 0, 256),
-    (1, 0, 256),
-    (2, 0, 0),
-    (3, 0, 512),
-    (4, 0, 512),
-    (4, 512, 0),
-    (5, 0, 512),
-    (5, 512, 0),
-    (6, 0, 512),
-    (6, 512, 0),
-    (7, 0, 512),
-    (7, 512, 0),
-    (8, 0, 512),
-    (8, 512, 0),
-    (9, 0, 0),
-    (10, 0, 256),
+    (0, 0, 512, 256),
+    (0, 512, 512, 256),
+    (1, 0, 1024, 512),
+    (2, 0, 1024, 512),
+    (3, 0, 1024, 512),
+    (0, 1024, 1024, 512),
+    (1, 1024, 1024, 512),
+    (2, 1024, 1024, 512),
+    (3, 1024, 512, 0),
+    (3, 1536, 512, 256),
 ]
 
 def tile_pinmodel_pa_kernel(tc, x, km1, b1, t2, core2, t3, core3, ln_g, ln_b, fc_w, fc_b, out):
@@ -62,7 +56,7 @@ def tile_pinmodel_pa_kernel(tc, x, km1, b1, t2, core2, t3, core3, ln_g, ln_b, fc
         const = ctx.enter_context(tc.tile_pool(name="const", bufs=1))
         raw = ctx.enter_context(tc.tile_pool(name="raw", bufs=1))
         keep = ctx.enter_context(tc.tile_pool(name="keep", bufs=1))
-        grouped_pool = ctx.enter_context(tc.tile_pool(name="grouped_pool", bufs=6))
+        grouped_pool = ctx.enter_context(tc.tile_pool(name="grouped_pool", bufs=3))
         o_banks = ctx.enter_context(tc.psum_pool(name="o_banks", bufs=1))
         work_banks = ctx.enter_context(tc.psum_pool(name="work_banks", bufs=1))
 
@@ -114,9 +108,9 @@ def tile_pinmodel_pa_kernel(tc, x, km1, b1, t2, core2, t3, core3, ln_g, ln_b, fc
         nc.sync.dma_start(out=vec_rows[8:16, :].bitcast(BF16), in_=ln_b.rearrange("(r c) -> r c", c=256))
         load_core(8)
         load_core(9)
-        load_core(10)
         nc.sync.dma_start(out=w_raw[0][:], in_=fc_w[P * 0 : P * 1, :])
         nc.sync.dma_start(out=w_raw[1][:], in_=fc_w[P * 1 : P * 2, :])
+        load_core(10)
         nc.sync.dma_start(out=w_raw[2][:], in_=fc_w[P * 2 : P * 3, :])
         nc.sync.dma_start(out=w_raw[3][:], in_=fc_w[P * 3 : P * 4, :])
         nc.sync.dma_start(out=fcb[:], in_=fc_b.partition_broadcast(P))
@@ -151,20 +145,26 @@ def tile_pinmodel_pa_kernel(tc, x, km1, b1, t2, core2, t3, core3, ln_g, ln_b, fc
         core_words = {}
         core_scales = {}
 
+        def loaded(kpass, lo, hi):
+            for i, (load_pass, first, width) in enumerate(LOADS):
+                if load_pass == kpass and first <= lo and hi <= first + width:
+                    return core_raw[i][:, :, lo - first : hi - first]
+
         def regroup(j):
-            load, col, cut = PIECES[j]
-            tile_j = grouped_pool.tile([P, BANK, PACK], BF16, tag="grouped", name="grouped%d" % j, align_bytes=64)
-            for copy, lo, hi in ((nc.vector.tensor_copy, 0, cut), (nc.scalar.copy, cut, BANK)):
+            kpass, col, width, cut = PIECES[j]
+            tile_j = grouped_pool.tile([P, width, PACK], BF16, tag="grouped", name="grouped%d" % j, align_bytes=64)
+            for copy, lo, hi in ((nc.vector.tensor_copy, 0, cut), (nc.scalar.copy, cut, width)):
                 if lo < hi:
                     copy(
                         out=tile_j[:, lo:hi, :].rearrange("p (c i) t -> p c t i", i=RUN),
-                        in_=core_raw[load][:, :, col + lo : col + hi].rearrange("p t (c i) -> p c t i", i=RUN),
+                        in_=loaded(kpass, col + lo, col + hi).rearrange("p t (c i) -> p c t i", i=RUN),
                     )
             grouped[j] = tile_j
 
         def quantise(j):
-            core_words[j] = keep.tile([P, BANK], U32, name="core_words%d" % j, align_bytes=64)
-            core_scales[j] = keep.tile([P, BANK], U8, name="core_scales%d" % j, align_bytes=64)
+            width = PIECES[j][2]
+            core_words[j] = keep.tile([P, width], U32, name="core_words%d" % j, align_bytes=64)
+            core_scales[j] = keep.tile([P, width], U8, name="core_scales%d" % j, align_bytes=64)
             nc.vector.quantize_mx(
                 out=core_words[j][:].bitcast(FP8X4),
                 scales=core_scales[j][:],
@@ -172,18 +172,18 @@ def tile_pinmodel_pa_kernel(tc, x, km1, b1, t2, core2, t3, core3, ln_g, ln_b, fc
             )
 
         def multiply(j):
-            load, col, cut = PIECES[j]
-            kpass, first_col, width = LOADS[load]
+            kpass, col, width, cut = PIECES[j]
             t_cols = slice(P * (kpass % 2), P * (kpass % 2 + 1))
-            nc.tensor.matmul_mx(
-                out=o_ps[(first_col + col) // BANK][:],
-                lhsT=t_words[kpass // 2][:, t_cols].bitcast(FP8X4),
-                lhsT_scale=t_scales[kpass // 2][:, t_cols],
-                rhs=core_words[j][:].bitcast(FP8X4),
-                rhs_scale=core_scales[j][:],
-                start=(kpass == 0),
-                stop=(kpass == 3),
-            )
+            for lo in range(0, width, BANK):
+                nc.tensor.matmul_mx(
+                    out=o_ps[(col + lo) // BANK][:],
+                    lhsT=t_words[kpass // 2][:, t_cols].bitcast(FP8X4),
+                    lhsT_scale=t_scales[kpass // 2][:, t_cols],
+                    rhs=core_words[j][:, lo : lo + BANK].bitcast(FP8X4),
+                    rhs_scale=core_scales[j][:, lo : lo + BANK],
+                    start=(kpass == 0),
+                    stop=(kpass == 3),
+                )
 
         order1 = keep.tile([P, N_BANKS, PACK, P], F32, name="order1")
         o_sb = keep.tile([P, N_BANKS, PACK, P], F32, name="o_sb")
@@ -224,15 +224,13 @@ def tile_pinmodel_pa_kernel(tc, x, km1, b1, t2, core2, t3, core3, ln_g, ln_b, fc
         def bank_stats(n):
             nc.vector.bn_stats(out=stats[:, n, :], in_=o_sb[:, n].rearrange("b t q -> b (t q)"))
 
-        w_words = keep.tile([P, 4, OUT], U32, name="w_words", align_bytes=64)
-        w_scales = keep.tile([P, 4, OUT], U8, name="w_scales", align_bytes=64)
-        w_grouped = [keep.tile([P, 4, P, 2], F32, name="w_grouped%d" % g, align_bytes=64) for g in range(4)]
+        w_words = keep.tile([P, 2, 4, OUT // 2], U32, name="w_words", align_bytes=64)
+        w_scales = keep.tile([P, 2, 4, OUT // 2], U8, name="w_scales", align_bytes=64)
+        w_grouped = keep.tile([P, 2, 4, 2, P, 2], F32, name="w_grouped", align_bytes=64)
         w_flipped = {}
 
         def transpose_w(g, half):
-            flipped = work_banks.tile(
-                [P, 2, 2, P], F32, tag="work%d" % ((2 * g + half) % 4), name="w_flipped%d%d" % (g, half)
-            )
+            flipped = work_banks.tile([P, 2, 2, P], F32, tag="work%d" % g, name="w_flipped%d%d" % (g, half))
             for r in range(2):
                 pairs = w_raw[2 * half + r][:].bitcast(F32)
                 for u in range(2):
@@ -241,16 +239,13 @@ def tile_pinmodel_pa_kernel(tc, x, km1, b1, t2, core2, t3, core3, ln_g, ln_b, fc
             w_flipped[g, half] = flipped
 
         def empty_w(g, half):
-            nc.scalar.copy(
-                out=w_grouped[g][:, 2 * half : 2 * half + 2],
-                in_=w_flipped[g, half][:].rearrange("p r u n -> p r n u"),
-            )
+            nc.scalar.copy(out=w_grouped[:, half, g], in_=w_flipped[g, half][:].rearrange("p r u n -> p r n u"))
 
-        def quantise_w(g):
+        def quantise_w(half, g0):
             nc.vector.quantize_mx(
-                out=w_words[:, g, :].bitcast(FP8X4),
-                scales=w_scales[:, g, :],
-                in_=w_grouped[g][:].rearrange("p r n u -> p (r n u)").bitcast(BF16),
+                out=w_words[:, half, g0 : g0 + 2].rearrange("p g n -> p (g n)").bitcast(FP8X4),
+                scales=w_scales[:, half, g0 : g0 + 2].rearrange("p g n -> p (g n)"),
+                in_=w_grouped[:, half, g0 : g0 + 2].rearrange("p g r n u -> p (g r n u)").bitcast(BF16),
             )
 
         mean_var = keep.tile([P, 2], F32, name="mean_var")
@@ -271,10 +266,10 @@ def tile_pinmodel_pa_kernel(tc, x, km1, b1, t2, core2, t3, core3, ln_g, ln_b, fc
             nc.tensor.transpose(vec_flipped[0][:], vec_rows[:], ident_f[:])
 
         def empty_vectors():
-            nc.vector.tensor_copy(out=vec_pairs[:], in_=vec_flipped[0][:, 0:16])
+            nc.scalar.copy(out=vec_pairs[:], in_=vec_flipped[0][:, 0:16])
 
         def widen_vectors():
-            nc.vector.tensor_copy(out=vec_cols[:], in_=vec_pairs[:].bitcast(BF16))
+            nc.scalar.copy(out=vec_cols[:], in_=vec_pairs[:].bitcast(BF16))
 
         def aggregate():
             nc.vector.bn_aggr(out=mean_var[:], in_=stats[:].rearrange("b n s -> b (n s)"))
@@ -337,33 +332,33 @@ def tile_pinmodel_pa_kernel(tc, x, km1, b1, t2, core2, t3, core3, ln_g, ln_b, fc
                 in_=y_planes[:, g].rearrange("p t (c i) -> p c t i", i=RUN),
             )
 
-        def quantise_y(g):
+        def quantise_y(g0):
             nc.vector.quantize_mx(
-                out=y_words[:, P * g : P * (g + 1)].bitcast(FP8X4),
-                scales=y_scales[:, P * g : P * (g + 1)],
-                in_=y_grouped[:, g].rearrange("p b t -> p (b t)"),
+                out=y_words[:, P * g0 : P * (g0 + 2)].bitcast(FP8X4),
+                scales=y_scales[:, P * g0 : P * (g0 + 2)],
+                in_=y_grouped[:, g0 : g0 + 2].rearrange("p g b t -> p (g b t)"),
             )
 
-        out_ps = []
+        out_ps = {}
         result = keep.tile([P, OUT], F32, name="result")
         out_rows = out.rearrange("b o n -> b (o n)")
 
-        def multiply_y(g):
+        def multiply_y(half, g):
             if g == 0:
-                out_ps.append(work_banks.tile([P, OUT], F32, tag="work0", name="out_ps"))
+                out_ps[half] = work_banks.tile([P, OUT // 2], F32, tag="work%d" % half, name="out_ps%d" % half)
             nc.tensor.matmul_mx(
-                out=out_ps[0][:],
+                out=out_ps[half][:],
                 lhsT=y_words[:, P * g : P * (g + 1)].bitcast(FP8X4),
                 lhsT_scale=y_scales[:, P * g : P * (g + 1)],
-                rhs=w_words[:, g, :].bitcast(FP8X4),
-                rhs_scale=w_scales[:, g, :],
+                rhs=w_words[:, half, g].bitcast(FP8X4),
+                rhs_scale=w_scales[:, half, g],
                 start=(g == 0),
                 stop=(g == 3),
             )
 
         def finish(half):
             cols = slice(OUT // 2 * half, OUT // 2 * (half + 1))
-            nc.vector.tensor_tensor(out=result[:, cols], in0=out_ps[0][:, cols], in1=fcb[:, cols], op=ALU.add)
+            nc.vector.tensor_tensor(out=result[:, cols], in0=out_ps[half][:], in1=fcb[:, cols], op=ALU.add)
             nc.sync.dma_start(out=out_rows[:, cols], in_=result[:, cols])
 
         ctx.enter_context(tc.manual_schedule())
@@ -373,87 +368,64 @@ def tile_pinmodel_pa_kernel(tc, x, km1, b1, t2, core2, t3, core3, ln_g, ln_b, fc
         transpose_t(0)
         empty_t(0)
         quantise(1)
-        regroup(2)
         quantise_t(0)
         multiply(0)
         multiply(1)
-        regroup(3)
+        regroup(2)
         quantise(2)
         multiply(2)
-        quantise(3)
-        multiply(3)
-        regroup(4)
-        regroup(5)
+        regroup(3)
         transpose_t(1)
         transpose_x()
         empty_x()
-        quantise(4)
+        quantise(3)
         empty_t(1)
         multiply_order1(0)
         multiply_order1(1)
         multiply_order1(2)
         multiply_order1(3)
-        quantise(5)
-        regroup(6)
+        regroup(4)
         quantise_t(1)
+        multiply(3)
+        quantise(4)
         multiply(4)
-        multiply(5)
-        regroup(7)
-        quantise(6)
-        multiply(6)
         empty_order1(0)
         empty_order1(1)
-        quantise(7)
-        multiply(7)
-        regroup(8)
-        regroup(9)
+        regroup(5)
         add_bank(0)
-        quantise(8)
-        multiply(8)
-        regroup(10)
-        regroup(11)
         add_bank(1)
-        quantise(9)
-        multiply(9)
-        quantise(10)
-        multiply(10)
+        regroup(6)
+        quantise(5)
+        multiply(5)
         bank_stats(0)
         empty_order1(2)
         empty_order1(3)
-        regroup(12)
-        regroup(13)
-        transpose_vectors()
+        regroup(7)
+        quantise(6)
+        multiply(6)
         bank_stats(1)
-        quantise(11)
+        transpose_vectors()
+        regroup(8)
+        quantise(7)
+        multiply(7)
+        regroup(9)
+        quantise(8)
+        multiply(8)
         empty_vectors()
-        multiply(11)
-        quantise(12)
-        multiply(12)
-        regroup(14)
-        quantise(13)
-        multiply(13)
-        regroup(15)
-        quantise(14)
-        multiply(14)
+        widen_vectors()
         transpose_w(0, 0)
-        quantise(15)
-        multiply(15)
-        transpose_w(0, 1)
-        empty_w(0, 0)
+        quantise(9)
+        multiply(9)
         transpose_w(1, 0)
-        transpose_w(1, 1)
-        add_bank(2)
-        empty_w(0, 1)
-        add_bank(3)
-        empty_w(1, 0)
-        empty_w(1, 1)
         transpose_w(2, 0)
-        transpose_w(2, 1)
         transpose_w(3, 0)
-        transpose_w(3, 1)
+        empty_w(0, 0)
+        add_bank(2)
+        empty_w(1, 0)
+        add_bank(3)
+        empty_w(2, 0)
         bank_stats(2)
         bank_stats(3)
-        widen_vectors()
         aggregate()
         inverse_deviation()
         negate_mean()
@@ -466,29 +438,36 @@ def tile_pinmodel_pa_kernel(tc, x, km1, b1, t2, core2, t3, core3, ln_g, ln_b, fc
         normalise_on_vector(3)
         transpose_z(2)
         transpose_z(3)
-        quantise_w(0)
-        empty_w(2, 0)
-        affine_on_scalar(0)
-        quantise_w(1)
-        affine_on_scalar(1)
-        empty_w(2, 1)
-        affine_on_scalar(2)
-        affine_on_scalar(3)
         empty_w(3, 0)
+        transpose_w(0, 1)
+        transpose_w(1, 1)
+        transpose_w(2, 1)
+        transpose_w(3, 1)
+        quantise_w(0, 0)
+        quantise_w(0, 2)
+        affine_on_scalar(0)
+        affine_on_scalar(1)
+        affine_on_scalar(2)
+        affine_on_vector(3)
+        empty_w(0, 1)
+        empty_w(1, 1)
+        empty_w(2, 1)
         empty_w(3, 1)
         regroup_y(0)
         regroup_y(1)
-        quantise_y(0)
-        quantise_w(2)
-        quantise_y(1)
-        regroup_y(2)
         regroup_y(3)
+        quantise_y(0)
+        regroup_y(2)
+        quantise_w(1, 0)
         quantise_y(2)
-        quantise_w(3)
-        quantise_y(3)
-        multiply_y(0)
-        multiply_y(1)
-        multiply_y(2)
-        multiply_y(3)
+        quantise_w(1, 2)
+        multiply_y(0, 0)
+        multiply_y(0, 1)
+        multiply_y(0, 2)
+        multiply_y(0, 3)
         finish(0)
+        multiply_y(1, 0)
+        multiply_y(1, 1)
+        multiply_y(1, 2)
+        multiply_y(1, 3)
         finish(1)

@@ -27,15 +27,13 @@ FLOPS = 2 * 128 * 2048 * (128 + 1024 + 1024) + 2 * 128 * 512 * 2048
 LOADS = [
     (0, 0, 512),
     (0, 512, 512),
-    (1, 512, 512),
-    (1, 0, 512),
+    (1, 0, 1024),
     (2, 0, 1024),
     (3, 0, 1024),
     (0, 1024, 1024),
     (1, 1024, 1024),
     (2, 1024, 1024),
-    (3, 1024, 512),
-    (3, 1536, 512),
+    (3, 1024, 1024),
 ]
 PIECES = [
     (0, 0, 512, 256),
@@ -96,21 +94,19 @@ def tile_pinmodel_pa_kernel(tc, x, km1, b1, t2, core2, t3, core3, ln_g, ln_b, fc
         nc.sync.dma_start(out=t_raw[0][:], in_=t2.rearrange("b r q -> b (r q)"))
         load_core(2)
         load_core(3)
-        load_core(4)
         nc.sync.dma_start(out=t_raw[1][:], in_=t3.rearrange("b r q -> b (r q)"))
         nc.sync.dma_start(out=x_raw[:], in_=x.rearrange("b i j -> b (i j)"))
-        load_core(5)
+        load_core(4)
         nc.sync.dma_start(out=km_raw[:], in_=km1.rearrange("i j d -> (i j) d"))
         nc.sync.dma_start(out=b1_row[0:1, :], in_=b1.rearrange("(o d) -> o d", o=1))
+        load_core(5)
         load_core(6)
-        load_core(7)
         nc.sync.dma_start(out=vec_rows[0:8, :].bitcast(BF16), in_=ln_g.rearrange("(r c) -> r c", c=256))
         nc.sync.dma_start(out=vec_rows[8:16, :].bitcast(BF16), in_=ln_b.rearrange("(r c) -> r c", c=256))
+        load_core(7)
         load_core(8)
-        load_core(9)
         nc.sync.dma_start(out=w_raw[0][:], in_=fc_w[P * 0 : P * 1, :])
         nc.sync.dma_start(out=w_raw[1][:], in_=fc_w[P * 1 : P * 2, :])
-        load_core(10)
         nc.sync.dma_start(out=w_raw[2][:], in_=fc_w[P * 2 : P * 3, :])
         nc.sync.dma_start(out=w_raw[3][:], in_=fc_w[P * 3 : P * 4, :])
         nc.sync.dma_start(out=fcb[:], in_=fc_b.partition_broadcast(P))
@@ -372,11 +368,11 @@ def tile_pinmodel_pa_kernel(tc, x, km1, b1, t2, core2, t3, core3, ln_g, ln_b, fc
         multiply(0)
         multiply(1)
         regroup(2)
+        transpose_t(1)
+        transpose_x()
         quantise(2)
         multiply(2)
         regroup(3)
-        transpose_t(1)
-        transpose_x()
         empty_x()
         quantise(3)
         empty_t(1)
@@ -409,56 +405,54 @@ def tile_pinmodel_pa_kernel(tc, x, km1, b1, t2, core2, t3, core3, ln_g, ln_b, fc
         quantise(7)
         multiply(7)
         regroup(9)
+        transpose_w(0, 0)
+        transpose_w(1, 0)
         quantise(8)
         multiply(8)
         empty_vectors()
         widen_vectors()
-        transpose_w(0, 0)
         quantise(9)
         multiply(9)
-        transpose_w(1, 0)
         transpose_w(2, 0)
         transpose_w(3, 0)
         empty_w(0, 0)
+        transpose_w(0, 1)
         add_bank(2)
         empty_w(1, 0)
+        transpose_w(1, 1)
         add_bank(3)
         empty_w(2, 0)
         bank_stats(2)
+        empty_w(3, 0)
         bank_stats(3)
         aggregate()
         inverse_deviation()
-        negate_mean()
-        scale_shift()
         normalise_on_vector(0)
         transpose_z(0)
-        normalise_on_scalar(1)
+        empty_w(0, 1)
+        normalise_on_vector(1)
         transpose_z(1)
         normalise_on_vector(2)
         normalise_on_vector(3)
         transpose_z(2)
         transpose_z(3)
-        empty_w(3, 0)
-        transpose_w(0, 1)
-        transpose_w(1, 1)
         transpose_w(2, 1)
         transpose_w(3, 1)
         quantise_w(0, 0)
-        quantise_w(0, 2)
         affine_on_scalar(0)
+        quantise_w(0, 2)
         affine_on_scalar(1)
-        affine_on_scalar(2)
-        affine_on_vector(3)
-        empty_w(0, 1)
         empty_w(1, 1)
+        affine_on_scalar(2)
+        affine_on_scalar(3)
         empty_w(2, 1)
         empty_w(3, 1)
         regroup_y(0)
         regroup_y(1)
-        regroup_y(3)
+        quantise_w(1, 0)
         quantise_y(0)
         regroup_y(2)
-        quantise_w(1, 0)
+        regroup_y(3)
         quantise_y(2)
         quantise_w(1, 2)
         multiply_y(0, 0)

@@ -41,10 +41,10 @@ PIECES = [
     (1, 0, 1024, 512),
     (2, 0, 1024, 512),
     (3, 0, 1024, 512),
-    (0, 1024, 1024, 512),
-    (1, 1024, 1024, 512),
-    (2, 1024, 1024, 512),
-    (3, 1024, 512, 0),
+    (0, 1024, 1024, 576),
+    (1, 1024, 1024, 576),
+    (2, 1024, 1024, 576),
+    (3, 1024, 512, 256),
     (3, 1536, 512, 256),
 ]
 
@@ -184,7 +184,11 @@ def tile_pinmodel_pa_kernel(tc, x, km1, b1, t2, core2, t3, core3, ln_g, ln_b, fc
         order1 = keep.tile([P, N_BANKS, PACK, P], F32, name="order1")
         o_sb = keep.tile([P, N_BANKS, PACK, P], F32, name="o_sb")
         z_sb = keep.tile([P, N_BANKS, PACK, P], F32, name="z_sb")
-        stats = keep.tile([P, N_BANKS, 6], F32, name="stats")
+        sums = keep.tile([P, 3], F32, name="sums")
+        squares = keep.tile([P, 3], F32, name="squares")
+        products = keep.tile([P, 3], F32, name="products")
+        stats = keep.tile([P, 15], F32, name="stats")
+        nc.vector.memset(stats[:, 0:9:3], float(BANK))
         x_t = keep.tile([P, P], BF16, name="x_t")
         order1_ps = {}
         x_flipped = []
@@ -203,22 +207,45 @@ def tile_pinmodel_pa_kernel(tc, x, km1, b1, t2, core2, t3, core3, ln_g, ln_b, fc
             nc.tensor.matmul(out=acc[:], lhsT=first_row[:], rhs=b1_row[:, cols], start=False, stop=True)
             order1_ps[n] = acc
 
+        def by_parity(bank):
+            return bank.rearrange("b (x e) -> b e x", e=2)
+
+        def runs(tile, n):
+            return tile[:, n].rearrange("b (e u) q -> b e (u q)", e=2)
+
         def empty_order1(n):
-            nc.scalar.copy(
-                out=order1[:, n].rearrange("b (u e) q -> b u e q", u=2),
-                in_=order1_ps[n][:].rearrange("b (u q e) -> b u e q", u=2, e=2),
-            )
+            nc.scalar.copy(out=runs(order1, n), in_=by_parity(order1_ps[n][:]))
 
         def add_bank(n):
-            nc.vector.tensor_tensor(
-                out=o_sb[:, n].rearrange("b (u e) q -> b u e q", u=2),
-                in0=o_ps[n][:].rearrange("b (u q e) -> b u e q", u=2, e=2),
-                in1=order1[:, n].rearrange("b (u e) q -> b u e q", u=2),
-                op=ALU.add,
-            )
+            if n < 3:
+                nc.vector.scalar_tensor_tensor(
+                    out=runs(o_sb, n),
+                    in0=by_parity(o_ps[n][:]),
+                    scalar=1.0,
+                    in1=runs(order1, n),
+                    op0=ALU.mult,
+                    op1=ALU.add,
+                    accum_out=sums[:, n : n + 1],
+                )
+            else:
+                nc.vector.tensor_tensor(
+                    out=runs(o_sb, n), in0=by_parity(o_ps[n][:]), in1=runs(order1, n), op=ALU.add
+                )
+
+        def square_bank(n):
+            nc.scalar.activation(out=z_sb[:, n], in_=o_sb[:, n], func=ACT.Square, accum_out=squares[:, n : n + 1])
+
+        def means():
+            nc.vector.tensor_scalar_mul(out=stats[:, 1:9:3], in0=sums[:], scalar1=1.0 / BANK)
+
+        def mean_products():
+            nc.vector.tensor_tensor(out=products[:], in0=sums[:], in1=stats[:, 1:9:3], op=ALU.mult)
+
+        def deviations():
+            nc.vector.tensor_tensor(out=stats[:, 2:9:3], in0=squares[:], in1=products[:], op=ALU.subtract)
 
         def bank_stats(n):
-            nc.vector.bn_stats(out=stats[:, n, :], in_=o_sb[:, n].rearrange("b t q -> b (t q)"))
+            nc.vector.bn_stats(out=stats[:, 9:15], in_=o_sb[:, n].rearrange("b t q -> b (t q)"))
 
         w_words = keep.tile([P, 2, 4, OUT // 2], U32, name="w_words", align_bytes=64)
         w_scales = keep.tile([P, 2, 4, OUT // 2], U8, name="w_scales", align_bytes=64)
@@ -246,8 +273,6 @@ def tile_pinmodel_pa_kernel(tc, x, km1, b1, t2, core2, t3, core3, ln_g, ln_b, fc
 
         mean_var = keep.tile([P, 2], F32, name="mean_var")
         rstd = keep.tile([P, 1], F32, name="rstd")
-        neg_mean = keep.tile([P, 1], F32, name="neg_mean")
-        shift = keep.tile([P, 1], F32, name="shift")
         vec_pairs = keep.tile([P, 16], F32, name="vec_pairs")
         vec_cols = keep.tile([P, 32], F32, name="vec_cols")
         y_planes = keep.tile([P, 4, PACK, P], BF16, name="y_planes")
@@ -268,20 +293,14 @@ def tile_pinmodel_pa_kernel(tc, x, km1, b1, t2, core2, t3, core3, ln_g, ln_b, fc
             nc.scalar.copy(out=vec_cols[:], in_=vec_pairs[:].bitcast(BF16))
 
         def aggregate():
-            nc.vector.bn_aggr(out=mean_var[:], in_=stats[:].rearrange("b n s -> b (n s)"))
+            nc.vector.bn_aggr(out=mean_var[:], in_=stats[:])
 
         def inverse_deviation():
             nc.scalar.activation(
                 out=rstd[:], in_=mean_var[:, 1:2], func=ACT.Abs_reciprocal_sqrt, bias=eps[:], scale=1.0
             )
 
-        def negate_mean():
-            nc.vector.tensor_scalar_mul(out=neg_mean[:], in0=mean_var[:, 0:1], scalar1=-1.0)
-
-        def scale_shift():
-            nc.scalar.activation(out=shift[:], in_=neg_mean[:], func=ACT.Identity, scale=rstd[:])
-
-        def normalise_on_vector(g):
+        def normalise(g):
             nc.vector.tensor_scalar(
                 out=z_sb[:, g],
                 in0=o_sb[:, g],
@@ -291,36 +310,22 @@ def tile_pinmodel_pa_kernel(tc, x, km1, b1, t2, core2, t3, core3, ln_g, ln_b, fc
                 op1=ALU.mult,
             )
 
-        def normalise_on_scalar(g):
-            nc.scalar.activation(out=z_sb[:, g], in_=o_sb[:, g], func=ACT.Identity, bias=shift[:], scale=rstd[:])
-
         def transpose_z(g):
             z_flipped[g] = o_banks.tile([P, PACK, P], F32, name="z_flipped%d" % g, tag="o%d" % g)
             for t in range(PACK):
                 nc.tensor.transpose(z_flipped[g][:, t, :], z_sb[:, g, t, :], ident_f[:])
 
-        def affine_on_vector(g):
-            for t in range(PACK):
-                k = PACK * g + t
-                nc.vector.tensor_scalar(
-                    out=y_planes[:, g, t, :],
-                    in0=z_flipped[g][:, t, :],
-                    scalar1=vec_cols[:, k : k + 1],
-                    scalar2=vec_cols[:, 16 + k : 17 + k],
-                    op0=ALU.mult,
-                    op1=ALU.add,
-                )
-
-        def affine_on_scalar(g):
-            for t in range(PACK):
-                k = PACK * g + t
-                nc.scalar.activation(
-                    out=y_planes[:, g, t, :],
-                    in_=z_flipped[g][:, t, :],
-                    func=ACT.Identity,
-                    bias=vec_cols[:, 16 + k : 17 + k],
-                    scale=vec_cols[:, k : k + 1],
-                )
+        def affine(g):
+            for u in range(2):
+                for e in range(2):
+                    k = PACK * g + 2 * u + e
+                    nc.scalar.activation(
+                        out=y_planes[:, g, 2 * u + e, :],
+                        in_=z_flipped[g][:, 2 * e + u, :],
+                        func=ACT.Identity,
+                        bias=vec_cols[:, 16 + k : 17 + k],
+                        scale=vec_cols[:, k : k + 1],
+                    )
 
         def regroup_y(g):
             nc.vector.tensor_copy(
@@ -378,13 +383,13 @@ def tile_pinmodel_pa_kernel(tc, x, km1, b1, t2, core2, t3, core3, ln_g, ln_b, fc
         empty_t(1)
         multiply_order1(0)
         multiply_order1(1)
-        multiply_order1(2)
-        multiply_order1(3)
         regroup(4)
         quantise_t(1)
         multiply(3)
         quantise(4)
         multiply(4)
+        multiply_order1(2)
+        multiply_order1(3)
         empty_order1(0)
         empty_order1(1)
         regroup(5)
@@ -393,13 +398,13 @@ def tile_pinmodel_pa_kernel(tc, x, km1, b1, t2, core2, t3, core3, ln_g, ln_b, fc
         regroup(6)
         quantise(5)
         multiply(5)
-        bank_stats(0)
+        square_bank(0)
         empty_order1(2)
         empty_order1(3)
         regroup(7)
         quantise(6)
         multiply(6)
-        bank_stats(1)
+        square_bank(1)
         transpose_vectors()
         regroup(8)
         quantise(7)
@@ -421,30 +426,33 @@ def tile_pinmodel_pa_kernel(tc, x, km1, b1, t2, core2, t3, core3, ln_g, ln_b, fc
         empty_w(1, 0)
         transpose_w(1, 1)
         add_bank(3)
+        square_bank(2)
+        means()
         empty_w(2, 0)
-        bank_stats(2)
-        empty_w(3, 0)
         bank_stats(3)
+        empty_w(3, 0)
+        mean_products()
+        deviations()
         aggregate()
         inverse_deviation()
-        normalise_on_vector(0)
+        normalise(0)
         transpose_z(0)
         empty_w(0, 1)
-        normalise_on_vector(1)
+        normalise(1)
         transpose_z(1)
-        normalise_on_vector(2)
-        normalise_on_vector(3)
+        normalise(2)
+        normalise(3)
         transpose_z(2)
         transpose_z(3)
         transpose_w(2, 1)
         transpose_w(3, 1)
         quantise_w(0, 0)
-        affine_on_scalar(0)
+        affine(0)
         quantise_w(0, 2)
-        affine_on_scalar(1)
+        affine(1)
         empty_w(1, 1)
-        affine_on_scalar(2)
-        affine_on_scalar(3)
+        affine(2)
+        affine(3)
         empty_w(2, 1)
         empty_w(3, 1)
         regroup_y(0)

@@ -264,11 +264,11 @@ def tile_pinmodel_pa_kernel(tc, x, km1, b1, t2, core2, t3, core3, ln_g, ln_b, fc
         def empty_w(g, half):
             nc.scalar.copy(out=w_grouped[:, half, g], in_=w_flipped[g, half][:].rearrange("p r u n -> p r n u"))
 
-        def quantise_w(half, g0):
+        def quantise_w(half, lo, hi):
             nc.vector.quantize_mx(
-                out=w_words[:, half, g0 : g0 + 2].rearrange("p g n -> p (g n)").bitcast(FP8X4),
-                scales=w_scales[:, half, g0 : g0 + 2].rearrange("p g n -> p (g n)"),
-                in_=w_grouped[:, half, g0 : g0 + 2].rearrange("p g r n u -> p (g r n u)").bitcast(BF16),
+                out=w_words[:, half, lo:hi].rearrange("p g n -> p (g n)").bitcast(FP8X4),
+                scales=w_scales[:, half, lo:hi].rearrange("p g n -> p (g n)"),
+                in_=w_grouped[:, half, lo:hi].rearrange("p g r n u -> p (g r n u)").bitcast(BF16),
             )
 
         mean_var = keep.tile([P, 2], F32, name="mean_var")
@@ -333,11 +333,11 @@ def tile_pinmodel_pa_kernel(tc, x, km1, b1, t2, core2, t3, core3, ln_g, ln_b, fc
                 in_=y_planes[:, g].rearrange("p t (c i) -> p c t i", i=RUN),
             )
 
-        def quantise_y(g0):
+        def quantise_y(lo, hi):
             nc.vector.quantize_mx(
-                out=y_words[:, P * g0 : P * (g0 + 2)].bitcast(FP8X4),
-                scales=y_scales[:, P * g0 : P * (g0 + 2)],
-                in_=y_grouped[:, g0 : g0 + 2].rearrange("p g b t -> p (g b t)"),
+                out=y_words[:, P * lo : P * hi].bitcast(FP8X4),
+                scales=y_scales[:, P * lo : P * hi],
+                in_=y_grouped[:, lo:hi].rearrange("p g b t -> p (g b t)"),
             )
 
         out_ps = {}
@@ -438,6 +438,7 @@ def tile_pinmodel_pa_kernel(tc, x, km1, b1, t2, core2, t3, core3, ln_g, ln_b, fc
         normalise(0)
         transpose_z(0)
         empty_w(0, 1)
+        empty_w(1, 1)
         normalise(1)
         transpose_z(1)
         normalise(2)
@@ -446,30 +447,31 @@ def tile_pinmodel_pa_kernel(tc, x, km1, b1, t2, core2, t3, core3, ln_g, ln_b, fc
         transpose_z(3)
         transpose_w(2, 1)
         transpose_w(3, 1)
-        quantise_w(0, 0)
+        quantise_w(0, 0, 2)
         affine(0)
-        quantise_w(0, 2)
+        quantise_w(0, 2, 4)
         affine(1)
-        empty_w(1, 1)
+        quantise_w(1, 0, 2)
         affine(2)
         affine(3)
         empty_w(2, 1)
         empty_w(3, 1)
         regroup_y(0)
         regroup_y(1)
-        quantise_w(1, 0)
-        quantise_y(0)
         regroup_y(2)
+        quantise_y(0, 2)
         regroup_y(3)
-        quantise_y(2)
-        quantise_w(1, 2)
+        quantise_y(2, 3)
+        quantise_w(1, 2, 3)
+        quantise_y(3, 4)
         multiply_y(0, 0)
         multiply_y(0, 1)
-        multiply_y(0, 2)
-        multiply_y(0, 3)
-        finish(0)
         multiply_y(1, 0)
         multiply_y(1, 1)
+        multiply_y(0, 2)
+        multiply_y(0, 3)
+        quantise_w(1, 3, 4)
+        finish(0)
         multiply_y(1, 2)
         multiply_y(1, 3)
         finish(1)

@@ -38,7 +38,7 @@ LOADS = [
 PIECES = [
     (0, 0, 512, 256),
     (0, 512, 512, 256),
-    (1, 0, 1024, 512),
+    (1, 0, 1024, 640),
     (2, 0, 1024, 512),
     (3, 0, 1024, 512),
     (0, 1024, 1024, 576),
@@ -394,12 +394,12 @@ def tile_pinmodel_pa_kernel(tc, x, km1, b1, t2, core2, t3, core3, ln_g, ln_b, fc
         empty_order1(1)
         regroup(5)
         add_bank(0)
+        empty_order1(2)
         add_bank(1)
         regroup(6)
         quantise(5)
         multiply(5)
         square_bank(0)
-        empty_order1(2)
         empty_order1(3)
         regroup(7)
         quantise(6)
@@ -411,9 +411,9 @@ def tile_pinmodel_pa_kernel(tc, x, km1, b1, t2, core2, t3, core3, ln_g, ln_b, fc
         multiply(7)
         regroup(9)
         transpose_w(0, 0)
-        transpose_w(1, 0)
         quantise(8)
         multiply(8)
+        transpose_w(1, 0)
         empty_vectors()
         widen_vectors()
         quantise(9)
@@ -428,13 +428,14 @@ def tile_pinmodel_pa_kernel(tc, x, km1, b1, t2, core2, t3, core3, ln_g, ln_b, fc
         add_bank(3)
         square_bank(2)
         means()
+        mean_products()
         empty_w(2, 0)
         bank_stats(3)
         empty_w(3, 0)
-        mean_products()
         deviations()
         aggregate()
         inverse_deviation()
+        quantise_w(0, 0, 1)
         normalise(0)
         transpose_z(0)
         empty_w(0, 1)
@@ -447,7 +448,7 @@ def tile_pinmodel_pa_kernel(tc, x, km1, b1, t2, core2, t3, core3, ln_g, ln_b, fc
         transpose_z(3)
         transpose_w(2, 1)
         transpose_w(3, 1)
-        quantise_w(0, 0, 2)
+        quantise_w(0, 1, 2)
         affine(0)
         quantise_w(0, 2, 4)
         affine(1)
@@ -462,8 +463,8 @@ def tile_pinmodel_pa_kernel(tc, x, km1, b1, t2, core2, t3, core3, ln_g, ln_b, fc
         quantise_y(0, 2)
         regroup_y(3)
         quantise_y(2, 3)
-        quantise_w(1, 2, 3)
         quantise_y(3, 4)
+        quantise_w(1, 2, 3)
         multiply_y(0, 0)
         multiply_y(0, 1)
         multiply_y(1, 0)

@@ -39,7 +39,7 @@ PIECES = [
     (0, 0, 512, 256),
     (0, 512, 512, 256),
     (1, 0, 1024, 640),
-    (2, 0, 1024, 512),
+    (2, 0, 1024, 576),
     (3, 0, 1024, 512),
     (0, 1024, 1024, 576),
     (1, 1024, 1024, 576),
@@ -91,14 +91,14 @@ def tile_pinmodel_pa_kernel(tc, x, km1, b1, t2, core2, t3, core3, ln_g, ln_b, fc
 
         load_core(0)
         load_core(1)
-        nc.sync.dma_start(out=t_raw[0][:], in_=t2.rearrange("b r q -> b (r q)"))
         load_core(2)
+        nc.sync.dma_start(out=t_raw[0][:], in_=t2.rearrange("b r q -> b (r q)"))
         load_core(3)
         nc.sync.dma_start(out=t_raw[1][:], in_=t3.rearrange("b r q -> b (r q)"))
         nc.sync.dma_start(out=x_raw[:], in_=x.rearrange("b i j -> b (i j)"))
-        load_core(4)
         nc.sync.dma_start(out=km_raw[:], in_=km1.rearrange("i j d -> (i j) d"))
         nc.sync.dma_start(out=b1_row[0:1, :], in_=b1.rearrange("(o d) -> o d", o=1))
+        load_core(4)
         load_core(5)
         load_core(6)
         nc.sync.dma_start(out=vec_rows[0:8, :].bitcast(BF16), in_=ln_g.rearrange("(r c) -> r c", c=256))
@@ -260,6 +260,19 @@ def tile_pinmodel_pa_kernel(tc, x, km1, b1, t2, core2, t3, core3, ln_g, ln_b, fc
                     first = 256 * g + P * u
                     nc.tensor.transpose(flipped[:, r, u, :], pairs[:, first : first + P], ident_f[:])
             w_flipped[g, half] = flipped
+
+        def keep_clock(bank, passes):
+            spare = o_banks.tile([P, BANK], F32, name="spare%d" % bank, tag="o%d" % bank)
+            for i in range(passes):
+                nc.tensor.matmul_mx(
+                    out=spare[:],
+                    lhsT=t_words[1][:, 0:P].bitcast(FP8X4),
+                    lhsT_scale=t_scales[1][:, 0:P],
+                    rhs=core_words[0][:].bitcast(FP8X4),
+                    rhs_scale=core_scales[0][:],
+                    start=True,
+                    stop=True,
+                )
 
         def empty_w(g, half):
             nc.scalar.copy(out=w_grouped[:, half, g], in_=w_flipped[g, half][:].rearrange("p r u n -> p r n u"))
@@ -425,6 +438,7 @@ def tile_pinmodel_pa_kernel(tc, x, km1, b1, t2, core2, t3, core3, ln_g, ln_b, fc
         add_bank(2)
         empty_w(1, 0)
         transpose_w(1, 1)
+        keep_clock(1, 2)
         add_bank(3)
         square_bank(2)
         means()
@@ -450,6 +464,7 @@ def tile_pinmodel_pa_kernel(tc, x, km1, b1, t2, core2, t3, core3, ln_g, ln_b, fc
         transpose_w(3, 1)
         quantise_w(0, 1, 2)
         affine(0)
+        keep_clock(0, 2)
         quantise_w(0, 2, 4)
         affine(1)
         quantise_w(1, 0, 2)

@@ -91,14 +91,14 @@ def tile_pinmodel_pa_kernel(tc, x, km1, b1, t2, core2, t3, core3, ln_g, ln_b, fc
 
         load_core(0)
         load_core(1)
-        load_core(2)
         nc.sync.dma_start(out=t_raw[0][:], in_=t2.rearrange("b r q -> b (r q)"))
+        load_core(2)
         load_core(3)
         nc.sync.dma_start(out=t_raw[1][:], in_=t3.rearrange("b r q -> b (r q)"))
         nc.sync.dma_start(out=x_raw[:], in_=x.rearrange("b i j -> b (i j)"))
+        load_core(4)
         nc.sync.dma_start(out=km_raw[:], in_=km1.rearrange("i j d -> (i j) d"))
         nc.sync.dma_start(out=b1_row[0:1, :], in_=b1.rearrange("(o d) -> o d", o=1))
-        load_core(4)
         load_core(5)
         load_core(6)
         nc.sync.dma_start(out=vec_rows[0:8, :].bitcast(BF16), in_=ln_g.rearrange("(r c) -> r c", c=256))

@@ -25,8 +25,7 @@ RUN = 8
 FLOPS = 2 * 128 * 2048 * (128 + 1024 + 1024) + 2 * 128 * 512 * 2048
 
 LOADS = [
-    (0, 0, 512),
-    (0, 512, 512),
+    (0, 0, 1024),
     (1, 0, 1024),
     (2, 0, 1024),
     (3, 0, 1024),
@@ -38,14 +37,14 @@ LOADS = [
 PIECES = [
     (0, 0, 512, 256),
     (0, 512, 512, 256),
-    (1, 0, 1024, 640),
-    (2, 0, 1024, 576),
-    (3, 0, 1024, 512),
-    (0, 1024, 1024, 576),
-    (1, 1024, 1024, 576),
-    (2, 1024, 1024, 576),
-    (3, 1024, 512, 256),
-    (3, 1536, 512, 256),
+    (1, 0, 1024, 544),
+    (2, 0, 1024, 544),
+    (3, 0, 1024, 576),
+    (0, 1024, 1024, 544),
+    (1, 1024, 1024, 544),
+    (2, 1024, 1024, 544),
+    (3, 1024, 512, 288),
+    (3, 1536, 512, 288),
 ]
 
 def tile_pinmodel_pa_kernel(tc, x, km1, b1, t2, core2, t3, core3, ln_g, ln_b, fc_w, fc_b, out):
@@ -93,18 +92,17 @@ def tile_pinmodel_pa_kernel(tc, x, km1, b1, t2, core2, t3, core3, ln_g, ln_b, fc
         load_core(1)
         nc.sync.dma_start(out=t_raw[0][:], in_=t2.rearrange("b r q -> b (r q)"))
         load_core(2)
-        load_core(3)
         nc.sync.dma_start(out=t_raw[1][:], in_=t3.rearrange("b r q -> b (r q)"))
         nc.sync.dma_start(out=x_raw[:], in_=x.rearrange("b i j -> b (i j)"))
-        load_core(4)
+        load_core(3)
         nc.sync.dma_start(out=km_raw[:], in_=km1.rearrange("i j d -> (i j) d"))
         nc.sync.dma_start(out=b1_row[0:1, :], in_=b1.rearrange("(o d) -> o d", o=1))
+        load_core(4)
         load_core(5)
-        load_core(6)
         nc.sync.dma_start(out=vec_rows[0:8, :].bitcast(BF16), in_=ln_g.rearrange("(r c) -> r c", c=256))
         nc.sync.dma_start(out=vec_rows[8:16, :].bitcast(BF16), in_=ln_b.rearrange("(r c) -> r c", c=256))
+        load_core(6)
         load_core(7)
-        load_core(8)
         nc.sync.dma_start(out=w_raw[0][:], in_=fc_w[P * 0 : P * 1, :])
         nc.sync.dma_start(out=w_raw[1][:], in_=fc_w[P * 1 : P * 2, :])
         nc.sync.dma_start(out=w_raw[2][:], in_=fc_w[P * 2 : P * 3, :])
@@ -380,36 +378,37 @@ def tile_pinmodel_pa_kernel(tc, x, km1, b1, t2, core2, t3, core3, ln_g, ln_b, fc
         regroup(1)
         quantise(0)
         transpose_t(0)
-        empty_t(0)
-        quantise(1)
-        quantise_t(0)
-        multiply(0)
-        multiply(1)
         regroup(2)
+        quantise(1)
+        empty_t(0)
+        regroup(3)
+        quantise_t(0)
+        quantise(2)
         transpose_t(1)
         transpose_x()
-        quantise(2)
+        multiply(0)
+        multiply(1)
         multiply(2)
-        regroup(3)
+        empty_t(1)
         empty_x()
         quantise(3)
-        empty_t(1)
+        quantise_t(1)
+        regroup(4)
         multiply_order1(0)
         multiply_order1(1)
-        regroup(4)
-        quantise_t(1)
         multiply(3)
+        empty_order1(0)
+        empty_order1(1)
         quantise(4)
         multiply(4)
         multiply_order1(2)
         multiply_order1(3)
-        empty_order1(0)
-        empty_order1(1)
         regroup(5)
         add_bank(0)
-        empty_order1(2)
         add_bank(1)
+        empty_order1(2)
         regroup(6)
+        transpose_vectors()
         quantise(5)
         multiply(5)
         square_bank(0)
@@ -418,7 +417,6 @@ def tile_pinmodel_pa_kernel(tc, x, km1, b1, t2, core2, t3, core3, ln_g, ln_b, fc
         quantise(6)
         multiply(6)
         square_bank(1)
-        transpose_vectors()
         regroup(8)
         quantise(7)
         multiply(7)

@@ -42,9 +42,9 @@ PIECES = [
     (3, 0, 1024, 576),
     (0, 1024, 1024, 544),
     (1, 1024, 1024, 544),
-    (2, 1024, 1024, 544),
-    (3, 1024, 512, 288),
-    (3, 1536, 512, 288),
+    (2, 1024, 1024, 528),
+    (3, 1024, 512, 240),
+    (3, 1536, 512, 240),
 ]
 
 def tile_pinmodel_pa_kernel(tc, x, km1, b1, t2, core2, t3, core3, ln_g, ln_b, fc_w, fc_b, out):
@@ -237,7 +237,7 @@ def tile_pinmodel_pa_kernel(tc, x, km1, b1, t2, core2, t3, core3, ln_g, ln_b, fc
             nc.vector.tensor_scalar_mul(out=stats[:, 1:9:3], in0=sums[:], scalar1=1.0 / BANK)
 
         def mean_products():
-            nc.vector.tensor_tensor(out=products[:], in0=sums[:], in1=stats[:, 1:9:3], op=ALU.mult)
+            nc.vector.scalar_tensor_tensor(out=products[:], in0=sums[:], scalar=1.0 / BANK, in1=sums[:], op0=ALU.mult, op1=ALU.mult)
 
         def deviations():
             nc.vector.tensor_tensor(out=stats[:, 2:9:3], in0=squares[:], in1=products[:], op=ALU.subtract)
@@ -274,6 +274,9 @@ def tile_pinmodel_pa_kernel(tc, x, km1, b1, t2, core2, t3, core3, ln_g, ln_b, fc
 
         def empty_w(g, half):
             nc.scalar.copy(out=w_grouped[:, half, g], in_=w_flipped[g, half][:].rearrange("p r u n -> p r n u"))
+
+        def empty_w_vector(g, half):
+            nc.vector.tensor_copy(out=w_grouped[:, half, g], in_=w_flipped[g, half][:].rearrange("p r u n -> p r n u"))
 
         def quantise_w(half, lo, hi):
             nc.vector.quantize_mx(
@@ -411,12 +414,12 @@ def tile_pinmodel_pa_kernel(tc, x, km1, b1, t2, core2, t3, core3, ln_g, ln_b, fc
         transpose_vectors()
         quantise(5)
         multiply(5)
-        square_bank(0)
         empty_order1(3)
+        empty_vectors()
         regroup(7)
         quantise(6)
         multiply(6)
-        square_bank(1)
+        widen_vectors()
         regroup(8)
         quantise(7)
         multiply(7)
@@ -425,12 +428,12 @@ def tile_pinmodel_pa_kernel(tc, x, km1, b1, t2, core2, t3, core3, ln_g, ln_b, fc
         quantise(8)
         multiply(8)
         transpose_w(1, 0)
-        empty_vectors()
-        widen_vectors()
         quantise(9)
         multiply(9)
         transpose_w(2, 0)
         transpose_w(3, 0)
+        square_bank(0)
+        square_bank(1)
         empty_w(0, 0)
         transpose_w(0, 1)
         add_bank(2)
@@ -443,14 +446,13 @@ def tile_pinmodel_pa_kernel(tc, x, km1, b1, t2, core2, t3, core3, ln_g, ln_b, fc
         mean_products()
         empty_w(2, 0)
         bank_stats(3)
-        empty_w(3, 0)
         deviations()
         aggregate()
         inverse_deviation()
-        quantise_w(0, 0, 1)
+        empty_w_vector(0, 1)
+        empty_w(3, 0)
         normalise(0)
         transpose_z(0)
-        empty_w(0, 1)
         empty_w(1, 1)
         normalise(1)
         transpose_z(1)
@@ -460,17 +462,17 @@ def tile_pinmodel_pa_kernel(tc, x, km1, b1, t2, core2, t3, core3, ln_g, ln_b, fc
         transpose_z(3)
         transpose_w(2, 1)
         transpose_w(3, 1)
-        quantise_w(0, 1, 2)
+        quantise_w(0, 0, 2)
         affine(0)
         keep_clock(0, 2)
         quantise_w(0, 2, 4)
         affine(1)
+        regroup_y(0)
         quantise_w(1, 0, 2)
         affine(2)
         affine(3)
         empty_w(2, 1)
         empty_w(3, 1)
-        regroup_y(0)
         regroup_y(1)
         regroup_y(2)
         quantise_y(0, 2)

@@ -37,14 +37,14 @@ LOADS = [
 PIECES = [
     (0, 0, 512, 256),
     (0, 512, 512, 256),
-    (1, 0, 1024, 544),
-    (2, 0, 1024, 544),
-    (3, 0, 1024, 576),
-    (0, 1024, 1024, 544),
-    (1, 1024, 1024, 544),
-    (2, 1024, 1024, 528),
-    (3, 1024, 512, 240),
-    (3, 1536, 512, 240),
+    (1, 0, 1024, 576),
+    (2, 0, 1024, 576),
+    (3, 0, 1024, 608),
+    (0, 1024, 1024, 512),
+    (1, 1024, 1024, 512),
+    (2, 1024, 1024, 512),
+    (3, 1024, 512, 224),
+    (3, 1536, 512, 224),
 ]
 
 def tile_pinmodel_pa_kernel(tc, x, km1, b1, t2, core2, t3, core3, ln_g, ln_b, fc_w, fc_b, out):
@@ -88,9 +88,9 @@ def tile_pinmodel_pa_kernel(tc, x, km1, b1, t2, core2, t3, core3, ln_g, ln_b, fc
             rows = cores[kpass // 2][first : first + K_PASS, col : col + width]
             nc.sync.dma_start(out=core_raw[i][:], in_=rows.rearrange("(p j) d -> p j d", j=PACK))
 
+        nc.sync.dma_start(out=t_raw[0][:], in_=t2.rearrange("b r q -> b (r q)"))
         load_core(0)
         load_core(1)
-        nc.sync.dma_start(out=t_raw[0][:], in_=t2.rearrange("b r q -> b (r q)"))
         load_core(2)
         nc.sync.dma_start(out=t_raw[1][:], in_=t3.rearrange("b r q -> b (r q)"))
         nc.sync.dma_start(out=x_raw[:], in_=x.rearrange("b i j -> b (i j)"))
@@ -377,20 +377,20 @@ def tile_pinmodel_pa_kernel(tc, x, km1, b1, t2, core2, t3, core3, ln_g, ln_b, fc
             nc.sync.dma_start(out=out_rows[:, cols], in_=result[:, cols])
 
         ctx.enter_context(tc.manual_schedule())
+        transpose_t(0)
+        empty_t(0)
+        quantise_t(0)
         regroup(0)
         regroup(1)
         quantise(0)
-        transpose_t(0)
+        multiply(0)
         regroup(2)
         quantise(1)
-        empty_t(0)
-        regroup(3)
-        quantise_t(0)
-        quantise(2)
+        multiply(1)
         transpose_t(1)
         transpose_x()
-        multiply(0)
-        multiply(1)
+        regroup(3)
+        quantise(2)
         multiply(2)
         empty_t(1)
         empty_x()
@@ -399,22 +399,22 @@ def tile_pinmodel_pa_kernel(tc, x, km1, b1, t2, core2, t3, core3, ln_g, ln_b, fc
         regroup(4)
         multiply_order1(0)
         multiply_order1(1)
+        multiply_order1(2)
+        multiply_order1(3)
         multiply(3)
         empty_order1(0)
         empty_order1(1)
+        empty_order1(2)
         quantise(4)
         multiply(4)
-        multiply_order1(2)
-        multiply_order1(3)
         regroup(5)
         add_bank(0)
         add_bank(1)
-        empty_order1(2)
+        empty_order1(3)
         regroup(6)
         transpose_vectors()
         quantise(5)
         multiply(5)
-        empty_order1(3)
         empty_vectors()
         regroup(7)
         quantise(6)

@@ -43,9 +43,12 @@ PIECES = [
     (0, 1024, 1024, 512),
     (1, 1024, 1024, 512),
     (2, 1024, 1024, 512),
-    (3, 1024, 512, 224),
-    (3, 1536, 512, 224),
+    (3, 1024, 512, 240),
+    (3, 1536, 512, 240),
 ]
+
+SUMS = [(0, 512), (512, 512), (1024, 512), (1536, 256), (1792, 256)]
+
 
 def tile_pinmodel_pa_kernel(tc, x, km1, b1, t2, core2, t3, core3, ln_g, ln_b, fc_w, fc_b, out):
     nc = tc.nc
@@ -134,7 +137,7 @@ def tile_pinmodel_pa_kernel(tc, x, km1, b1, t2, core2, t3, core3, ln_g, ln_b, fc
                 in_=t_grouped[i][:].rearrange("p c b u -> p (c b u)").bitcast(BF16),
             )
 
-        o_ps = [o_banks.tile([P, BANK], F32, name="o_ps%d" % n, tag="o%d" % n) for n in range(N_BANKS)]
+        o_ps = {}
         grouped = {}
         core_words = {}
         core_scales = {}
@@ -155,29 +158,35 @@ def tile_pinmodel_pa_kernel(tc, x, km1, b1, t2, core2, t3, core3, ln_g, ln_b, fc
                     )
             grouped[j] = tile_j
 
-        def quantise(j):
+        def quantise(j, lo=0, hi=None):
             width = PIECES[j][2]
-            core_words[j] = keep.tile([P, width], U32, name="core_words%d" % j, align_bytes=64)
-            core_scales[j] = keep.tile([P, width], U8, name="core_scales%d" % j, align_bytes=64)
+            hi = hi or width
+            if lo == 0:
+                core_words[j] = keep.tile([P, width], U32, name="core_words%d" % j, align_bytes=64)
+                core_scales[j] = keep.tile([P, width], U8, name="core_scales%d" % j, align_bytes=64)
             nc.vector.quantize_mx(
-                out=core_words[j][:].bitcast(FP8X4),
-                scales=core_scales[j][:],
-                in_=grouped[j][:].rearrange("p w j -> p (w j)"),
+                out=core_words[j][:, lo:hi].bitcast(FP8X4),
+                scales=core_scales[j][:, lo:hi],
+                in_=grouped[j][:, lo:hi, :].rearrange("p w j -> p (w j)"),
             )
 
-        def multiply(j):
+        def multiply(j, lo=0, hi=None):
             kpass, col, width, cut = PIECES[j]
             t_cols = slice(P * (kpass % 2), P * (kpass % 2 + 1))
-            for lo in range(0, width, BANK):
-                nc.tensor.matmul_mx(
-                    out=o_ps[(col + lo) // BANK][:],
-                    lhsT=t_words[kpass // 2][:, t_cols].bitcast(FP8X4),
-                    lhsT_scale=t_scales[kpass // 2][:, t_cols],
-                    rhs=core_words[j][:, lo : lo + BANK].bitcast(FP8X4),
-                    rhs_scale=core_scales[j][:, lo : lo + BANK],
-                    start=(kpass == 0),
-                    stop=(kpass == 3),
-                )
+            for n, (first, columns) in enumerate(SUMS):
+                if col + lo <= first < col + (hi or width):
+                    if kpass == 0:
+                        o_ps[n] = o_banks.tile([P, BANK], F32, name="o_ps%d" % n, tag="o%d" % n)
+                    here = slice(first - col, first - col + columns)
+                    nc.tensor.matmul_mx(
+                        out=o_ps[n][:, 0:columns],
+                        lhsT=t_words[kpass // 2][:, t_cols].bitcast(FP8X4),
+                        lhsT_scale=t_scales[kpass // 2][:, t_cols],
+                        rhs=core_words[j][:, here].bitcast(FP8X4),
+                        rhs_scale=core_scales[j][:, here],
+                        start=(kpass == 0),
+                        stop=(kpass == 3),
+                    )
 
         order1 = keep.tile([P, N_BANKS, PACK, P], F32, name="order1")
         o_sb = keep.tile([P, N_BANKS, PACK, P], F32, name="o_sb")
@@ -185,21 +194,22 @@ def tile_pinmodel_pa_kernel(tc, x, km1, b1, t2, core2, t3, core3, ln_g, ln_b, fc
         sums = keep.tile([P, 3], F32, name="sums")
         squares = keep.tile([P, 3], F32, name="squares")
         products = keep.tile([P, 3], F32, name="products")
-        stats = keep.tile([P, 15], F32, name="stats")
+        stats = keep.tile([P, 21], F32, name="stats")
         nc.vector.memset(stats[:, 0:9:3], float(BANK))
         x_t = keep.tile([P, P], BF16, name="x_t")
         order1_ps = {}
         x_flipped = []
 
         def transpose_x():
-            x_flipped.append(work_banks.tile([P, P], BF16, tag="work3", name="x_flipped"))
+            x_flipped.append(work_banks.tile([P, P], BF16, tag="work2", name="x_flipped"))
             nc.tensor.transpose(x_flipped[0][:], x_raw[:], ident_b[:])
 
         def empty_x():
             nc.vector.tensor_copy(out=x_t[:], in_=x_flipped[0][:])
 
         def multiply_order1(n):
-            acc = work_banks.tile([P, BANK], F32, tag="work%d" % n, name="order1_ps%d" % n)
+            pool, tag = (work_banks, "work%d" % n) if n < 3 else (o_banks, "o4")
+            acc = pool.tile([P, BANK], F32, tag=tag, name="order1_ps%d" % n)
             cols = slice(BANK * n, BANK * (n + 1))
             nc.tensor.matmul(out=acc[:], lhsT=x_t[:], rhs=km_raw[:, cols], start=True, stop=False)
             nc.tensor.matmul(out=acc[:], lhsT=first_row[:], rhs=b1_row[:, cols], start=False, stop=True)
@@ -212,23 +222,30 @@ def tile_pinmodel_pa_kernel(tc, x, km1, b1, t2, core2, t3, core3, ln_g, ln_b, fc
             return tile[:, n].rearrange("b (e u) q -> b e (u q)", e=2)
 
         def empty_order1(n):
-            nc.scalar.copy(out=runs(order1, n), in_=by_parity(order1_ps[n][:]))
+            if n < 3:
+                nc.scalar.copy(out=runs(order1, n), in_=by_parity(order1_ps[n][:]))
+            else:
+                nc.scalar.copy(
+                    out=order1[:, n].rearrange("b (u e) q -> b u e q", e=2),
+                    in_=order1_ps[n][:].rearrange("b (u q e) -> b u e q", u=2, e=2),
+                )
 
         def add_bank(n):
-            if n < 3:
-                nc.vector.scalar_tensor_tensor(
-                    out=runs(o_sb, n),
-                    in0=by_parity(o_ps[n][:]),
-                    scalar=1.0,
-                    in1=runs(order1, n),
-                    op0=ALU.mult,
-                    op1=ALU.add,
-                    accum_out=sums[:, n : n + 1],
-                )
-            else:
-                nc.vector.tensor_tensor(
-                    out=runs(o_sb, n), in0=by_parity(o_ps[n][:]), in1=runs(order1, n), op=ALU.add
-                )
+            nc.vector.scalar_tensor_tensor(
+                out=runs(o_sb, n),
+                in0=by_parity(o_ps[n][:]),
+                scalar=1.0,
+                in1=runs(order1, n),
+                op0=ALU.mult,
+                op1=ALU.add,
+                accum_out=sums[:, n : n + 1],
+            )
+
+        def add_last(u):
+            mine = slice(2 * u, 2 * u + 2)
+            nc.vector.tensor_tensor(
+                out=o_sb[:, 3, mine, :], in0=by_parity(o_ps[3 + u][:, 0 : BANK // 2]), in1=order1[:, 3, mine, :], op=ALU.add
+            )
 
         def square_bank(n):
             nc.scalar.activation(out=z_sb[:, n], in_=o_sb[:, n], func=ACT.Square, accum_out=squares[:, n : n + 1])
@@ -242,8 +259,11 @@ def tile_pinmodel_pa_kernel(tc, x, km1, b1, t2, core2, t3, core3, ln_g, ln_b, fc
         def deviations():
             nc.vector.tensor_tensor(out=stats[:, 2:9:3], in0=squares[:], in1=products[:], op=ALU.subtract)
 
-        def bank_stats(n):
-            nc.vector.bn_stats(out=stats[:, 9:15], in_=o_sb[:, n].rearrange("b t q -> b (t q)"))
+        def last_stats(u):
+            nc.vector.bn_stats(
+                out=stats[:, 9 + 6 * u : 15 + 6 * u],
+                in_=o_sb[:, 3, 2 * u : 2 * u + 2, :].rearrange("b t q -> b (t q)"),
+            )
 
         w_words = keep.tile([P, 2, 4, OUT // 2], U32, name="w_words", align_bytes=64)
         w_scales = keep.tile([P, 2, 4, OUT // 2], U8, name="w_scales", align_bytes=64)
@@ -251,7 +271,8 @@ def tile_pinmodel_pa_kernel(tc, x, km1, b1, t2, core2, t3, core3, ln_g, ln_b, fc
         w_flipped = {}
 
         def transpose_w(g, half):
-            flipped = work_banks.tile([P, 2, 2, P], F32, tag="work%d" % g, name="w_flipped%d%d" % (g, half))
+            pool, tag = (work_banks, "work%d" % g) if g < 3 else (o_banks, "o1")
+            flipped = pool.tile([P, 2, 2, P], F32, tag=tag, name="w_flipped%d%d" % (g, half))
             for r in range(2):
                 pairs = w_raw[2 * half + r][:].bitcast(F32)
                 for u in range(2):
@@ -314,28 +335,29 @@ def tile_pinmodel_pa_kernel(tc, x, km1, b1, t2, core2, t3, core3, ln_g, ln_b, fc
                 out=rstd[:], in_=mean_var[:, 1:2], func=ACT.Abs_reciprocal_sqrt, bias=eps[:], scale=1.0
             )
 
-        def normalise(g):
+        def normalise(g, lo=0, hi=PACK):
             nc.vector.tensor_scalar(
-                out=z_sb[:, g],
-                in0=o_sb[:, g],
+                out=z_sb[:, g, lo:hi],
+                in0=o_sb[:, g, lo:hi],
                 scalar1=mean_var[:, 0:1],
                 scalar2=rstd[:],
                 op0=ALU.subtract,
                 op1=ALU.mult,
             )
 
-        def transpose_z(g):
-            z_flipped[g] = o_banks.tile([P, PACK, P], F32, name="z_flipped%d" % g, tag="o%d" % g)
-            for t in range(PACK):
-                nc.tensor.transpose(z_flipped[g][:, t, :], z_sb[:, g, t, :], ident_f[:])
+        def transpose_z(g, bank, lo=0, hi=PACK):
+            flipped = o_banks.tile([P, hi - lo, P], F32, name="z_flipped%d_%d" % (g, lo), tag="o%d" % bank)
+            for t in range(lo, hi):
+                nc.tensor.transpose(flipped[:, t - lo, :], z_sb[:, g, t, :], ident_f[:])
+                z_flipped[g, t] = flipped[:, t - lo, :]
 
-        def affine(g):
-            for u in range(2):
-                for e in range(2):
+        def affine(g, halves=(0, 1)):
+            for e in halves:
+                for u in range(2):
                     k = PACK * g + 2 * u + e
                     nc.scalar.activation(
                         out=y_planes[:, g, 2 * u + e, :],
-                        in_=z_flipped[g][:, 2 * e + u, :],
+                        in_=z_flipped[g, 2 * e + u if g < 3 else 2 * u + e],
                         func=ACT.Identity,
                         bias=vec_cols[:, 16 + k : 17 + k],
                         scale=vec_cols[:, k : k + 1],
@@ -427,44 +449,51 @@ def tile_pinmodel_pa_kernel(tc, x, km1, b1, t2, core2, t3, core3, ln_g, ln_b, fc
         transpose_w(0, 0)
         quantise(8)
         multiply(8)
+        quantise(9, 0, 256)
+        quantise(9, 256, 512)
+        multiply(9, 0, 256)
+        multiply(9, 256, 512)
         transpose_w(1, 0)
-        quantise(9)
-        multiply(9)
         transpose_w(2, 0)
         transpose_w(3, 0)
         square_bank(0)
-        square_bank(1)
         empty_w(0, 0)
+        square_bank(1)
         transpose_w(0, 1)
         add_bank(2)
-        empty_w(1, 0)
-        transpose_w(1, 1)
-        keep_clock(1, 2)
-        add_bank(3)
+        keep_clock(0, 2)
+        add_last(0)
+        add_last(1)
         square_bank(2)
+        empty_w(1, 0)
         means()
         mean_products()
+        transpose_w(1, 1)
         empty_w(2, 0)
-        bank_stats(3)
+        last_stats(0)
+        last_stats(1)
         deviations()
         aggregate()
         inverse_deviation()
         empty_w_vector(0, 1)
         empty_w(3, 0)
-        normalise(0)
-        transpose_z(0)
+        normalise(0, 0, 2)
+        transpose_z(0, 0, 0, 2)
+        normalise(0, 2, 4)
+        transpose_z(0, 2, 2, 4)
         empty_w(1, 1)
         normalise(1)
-        transpose_z(1)
+        transpose_z(1, 3)
         normalise(2)
         normalise(3)
-        transpose_z(2)
-        transpose_z(3)
+        transpose_z(2, 4)
+        affine(0, (0,))
+        transpose_z(3, 0)
         transpose_w(2, 1)
         transpose_w(3, 1)
         quantise_w(0, 0, 2)
-        affine(0)
-        keep_clock(0, 2)
+        affine(0, (1,))
+        keep_clock(2, 2)
         quantise_w(0, 2, 4)
         affine(1)
         regroup_y(0)

@@ -102,10 +102,10 @@ def tile_pinmodel_pa_kernel(tc, x, km1, b1, t2, core2, t3, core3, ln_g, ln_b, fc
         nc.sync.dma_start(out=b1_row[0:1, :], in_=b1.rearrange("(o d) -> o d", o=1))
         load_core(4)
         load_core(5)
-        nc.sync.dma_start(out=vec_rows[0:8, :].bitcast(BF16), in_=ln_g.rearrange("(r c) -> r c", c=256))
-        nc.sync.dma_start(out=vec_rows[8:16, :].bitcast(BF16), in_=ln_b.rearrange("(r c) -> r c", c=256))
         load_core(6)
         load_core(7)
+        nc.sync.dma_start(out=vec_rows[0:8, :].bitcast(BF16), in_=ln_g.rearrange("(r c) -> r c", c=256))
+        nc.sync.dma_start(out=vec_rows[8:16, :].bitcast(BF16), in_=ln_b.rearrange("(r c) -> r c", c=256))
         nc.sync.dma_start(out=w_raw[0][:], in_=fc_w[P * 0 : P * 1, :])
         nc.sync.dma_start(out=w_raw[1][:], in_=fc_w[P * 1 : P * 2, :])
         nc.sync.dma_start(out=w_raw[2][:], in_=fc_w[P * 2 : P * 3, :])
@@ -434,15 +434,13 @@ def tile_pinmodel_pa_kernel(tc, x, km1, b1, t2, core2, t3, core3, ln_g, ln_b, fc
         add_bank(1)
         empty_order1(3)
         regroup(6)
-        transpose_vectors()
         quantise(5)
         multiply(5)
-        empty_vectors()
         regroup(7)
         quantise(6)
         multiply(6)
-        widen_vectors()
         regroup(8)
+        transpose_vectors()
         quantise(7)
         multiply(7)
         regroup(9)
@@ -454,11 +452,13 @@ def tile_pinmodel_pa_kernel(tc, x, km1, b1, t2, core2, t3, core3, ln_g, ln_b, fc
         multiply(9, 0, 256)
         multiply(9, 256, 512)
         transpose_w(1, 0)
-        transpose_w(2, 0)
-        transpose_w(3, 0)
+        empty_vectors()
         square_bank(0)
         empty_w(0, 0)
+        widen_vectors()
         square_bank(1)
+        transpose_w(2, 0)
+        transpose_w(3, 0)
         transpose_w(0, 1)
         add_bank(2)
         keep_clock(0, 2)

from contextlib import ExitStack

import concourse.mybir as mybir
from concourse.masks import make_identity

F32 = mybir.dt.float32
BF16 = mybir.dt.bfloat16
U32 = mybir.dt.uint32
U8 = mybir.dt.uint8
FP8X4 = mybir.dt.float8_e4m3fn_x4
ALU = mybir.AluOpType
ACT = mybir.ActivationFunctionType

P = 128
PACK = 4
K_PASS = P * PACK
D = 2048
KR = 1024
OUT = 512
BANK = 512
N_BANKS = D // BANK
EPS = 1e-5
RUN = 8

FLOPS = 2 * 128 * 2048 * (128 + 1024 + 1024) + 2 * 128 * 512 * 2048

LOADS = [
    (0, 0, 1024),
    (1, 0, 1024),
    (2, 0, 1024),
    (3, 0, 1024),
    (0, 1024, 1024),
    (1, 1024, 1024),
    (2, 1024, 1024),
    (3, 1024, 1024),
]
PIECES = [
    (0, 0, 512, 256),
    (0, 512, 512, 256),
    (1, 0, 1024, 576),
    (2, 0, 1024, 576),
    (3, 0, 1024, 608),
    (0, 1024, 1024, 512),
    (1, 1024, 1024, 512),
    (2, 1024, 1024, 512),
    (3, 1024, 512, 240),
    (3, 1536, 512, 240),
]

SUMS = [(0, 512), (512, 512), (1024, 512), (1536, 256), (1792, 256)]


def tile_pinmodel_pa_kernel(tc, x, km1, b1, t2, core2, t3, core3, ln_g, ln_b, fc_w, fc_b, out):
    nc = tc.nc
    with ExitStack() as ctx:
        const = ctx.enter_context(tc.tile_pool(name="const", bufs=1))
        raw = ctx.enter_context(tc.tile_pool(name="raw", bufs=1))
        keep = ctx.enter_context(tc.tile_pool(name="keep", bufs=1))
        grouped_pool = ctx.enter_context(tc.tile_pool(name="grouped_pool", bufs=3))
        o_banks = ctx.enter_context(tc.psum_pool(name="o_banks", bufs=1))
        work_banks = ctx.enter_context(tc.psum_pool(name="work_banks", bufs=1))

        t_raw = [raw.tile([P, KR], BF16, name="t_raw%d" % i) for i in range(2)]
        core_raw = [raw.tile([P, PACK, load[2]], BF16, name="core_raw%d" % i) for i, load in enumerate(LOADS)]
        x_raw = raw.tile([P, P], BF16, name="x_raw")
        km_raw = raw.tile([P, D], BF16, name="km_raw")
        w_raw = [raw.tile([P, D], BF16, name="w_raw%d" % r) for r in range(4)]
        fcb = raw.tile([P, OUT], BF16, name="fcb")

        eps = const.tile([P, 1], F32, name="eps")
        nc.vector.memset(eps[:], EPS)
        warm = const.tile([P, 1], F32, name="warm")
        nc.scalar.activation(out=warm[:], in_=eps[:], func=ACT.Abs_reciprocal_sqrt)
        ident_f = const.tile([P, P], F32, name="ident_f")
        make_identity(nc, ident_f[:])
        ident_b = const.tile([P, P], BF16, name="ident_b")
        make_identity(nc, ident_b[:])
        vec_rows = const.tile([P, P], F32, name="vec_rows")
        nc.vector.memset(vec_rows[:], 0.0)
        first_row = const.tile([P, P], BF16, name="first_row")
        nc.vector.memset(first_row[:], 0.0)
        nc.vector.memset(first_row[0:1, :], 1.0)
        b1_row = const.tile([P, D], BF16, name="b1_row")
        nc.vector.memset(b1_row[:], 0.0)

        cores = [core2.rearrange("r q d -> (r q) d"), core3.rearrange("r q d -> (r q) d")]

        def load_core(i):
            kpass, col, width = LOADS[i]
            first = K_PASS * (kpass % 2)
            rows = cores[kpass // 2][first : first + K_PASS, col : col + width]
            nc.sync.dma_start(out=core_raw[i][:], in_=rows.rearrange("(p j) d -> p j d", j=PACK))

        nc.sync.dma_start(out=t_raw[0][:], in_=t2.rearrange("b r q -> b (r q)"))
        load_core(0)
        load_core(1)
        load_core(2)
        nc.sync.dma_start(out=t_raw[1][:], in_=t3.rearrange("b r q -> b (r q)"))
        nc.sync.dma_start(out=x_raw[:], in_=x.rearrange("b i j -> b (i j)"))
        load_core(3)
        nc.sync.dma_start(out=km_raw[:], in_=km1.rearrange("i j d -> (i j) d"))
        nc.sync.dma_start(out=b1_row[0:1, :], in_=b1.rearrange("(o d) -> o d", o=1))
        load_core(4)
        load_core(5)
        load_core(6)
        load_core(7)
        nc.sync.dma_start(out=vec_rows[0:8, :].bitcast(BF16), in_=ln_g.rearrange("(r c) -> r c", c=256))
        nc.sync.dma_start(out=vec_rows[8:16, :].bitcast(BF16), in_=ln_b.rearrange("(r c) -> r c", c=256))
        nc.sync.dma_start(out=w_raw[0][:], in_=fc_w[P * 0 : P * 1, :])
        nc.sync.dma_start(out=w_raw[1][:], in_=fc_w[P * 1 : P * 2, :])
        nc.sync.dma_start(out=w_raw[2][:], in_=fc_w[P * 2 : P * 3, :])
        nc.sync.dma_start(out=w_raw[3][:], in_=fc_w[P * 3 : P * 4, :])
        nc.sync.dma_start(out=fcb[:], in_=fc_b.partition_broadcast(P))

        t_words = [keep.tile([P, 2 * P], U32, name="t_words%d" % i, align_bytes=64) for i in range(2)]
        t_scales = [keep.tile([P, 2 * P], U8, name="t_scales%d" % i, align_bytes=64) for i in range(2)]
        t_grouped = [keep.tile([P, 2, P, 2], F32, name="t_grouped%d" % i, align_bytes=64) for i in range(2)]
        t_flipped = {}

        def transpose_t(i):
            pairs = t_raw[i][:].bitcast(F32)
            flipped = work_banks.tile([P, 2, 2, P], F32, tag="work%d" % i, name="t_flipped%d" % i)
            for kpass in range(2):
                for u in range(2):
                    nc.tensor.transpose(
                        flipped[:, kpass, u, :], pairs[:, 256 * kpass + u : 256 * (kpass + 1) : 2], ident_f[:]
                    )
            t_flipped[i] = flipped

        def empty_t(i):
            nc.scalar.copy(out=t_grouped[i][:], in_=t_flipped[i][:].rearrange("p c u b -> p c b u"))

        def quantise_t(i):
            nc.vector.quantize_mx(
                out=t_words[i][:].bitcast(FP8X4),
                scales=t_scales[i][:],
                in_=t_grouped[i][:].rearrange("p c b u -> p (c b u)").bitcast(BF16),
            )

        o_ps = {}
        grouped = {}
        core_words = {}
        core_scales = {}

        def loaded(kpass, lo, hi):
            for i, (load_pass, first, width) in enumerate(LOADS):
                if load_pass == kpass and first <= lo and hi <= first + width:
                    return core_raw[i][:, :, lo - first : hi - first]

        def regroup(j):
            kpass, col, width, cut = PIECES[j]
            tile_j = grouped_pool.tile([P, width, PACK], BF16, tag="grouped", name="grouped%d" % j, align_bytes=64)
            for copy, lo, hi in ((nc.vector.tensor_copy, 0, cut), (nc.scalar.copy, cut, width)):
                if lo < hi:
                    copy(
                        out=tile_j[:, lo:hi, :].rearrange("p (c i) t -> p c t i", i=RUN),
                        in_=loaded(kpass, col + lo, col + hi).rearrange("p t (c i) -> p c t i", i=RUN),
                    )
            grouped[j] = tile_j

        def quantise(j, lo=0, hi=None):
            width = PIECES[j][2]
            hi = hi or width
            if lo == 0:
                core_words[j] = keep.tile([P, width], U32, name="core_words%d" % j, align_bytes=64)
                core_scales[j] = keep.tile([P, width], U8, name="core_scales%d" % j, align_bytes=64)
            nc.vector.quantize_mx(
                out=core_words[j][:, lo:hi].bitcast(FP8X4),
                scales=core_scales[j][:, lo:hi],
                in_=grouped[j][:, lo:hi, :].rearrange("p w j -> p (w j)"),
            )

        def multiply(j, lo=0, hi=None):
            kpass, col, width, cut = PIECES[j]
            t_cols = slice(P * (kpass % 2), P * (kpass % 2 + 1))
            for n, (first, columns) in enumerate(SUMS):
                if col + lo <= first < col + (hi or width):
                    if kpass == 0:
                        o_ps[n] = o_banks.tile([P, BANK], F32, name="o_ps%d" % n, tag="o%d" % n)
                    here = slice(first - col, first - col + columns)
                    nc.tensor.matmul_mx(
                        out=o_ps[n][:, 0:columns],
                        lhsT=t_words[kpass // 2][:, t_cols].bitcast(FP8X4),
                        lhsT_scale=t_scales[kpass // 2][:, t_cols],
                        rhs=core_words[j][:, here].bitcast(FP8X4),
                        rhs_scale=core_scales[j][:, here],
                        start=(kpass == 0),
                        stop=(kpass == 3),
                    )

        order1 = keep.tile([P, N_BANKS, PACK, P], F32, name="order1")
        o_sb = keep.tile([P, N_BANKS, PACK, P], F32, name="o_sb")
        z_sb = keep.tile([P, N_BANKS, PACK, P], F32, name="z_sb")
        sums = keep.tile([P, 3], F32, name="sums")
        squares = keep.tile([P, 3], F32, name="squares")
        products = keep.tile([P, 3], F32, name="products")
        stats = keep.tile([P, 21], F32, name="stats")
        nc.vector.memset(stats[:, 0:9:3], float(BANK))
        x_t = keep.tile([P, P], BF16, name="x_t")
        order1_ps = {}
        x_flipped = []

        def transpose_x():
            x_flipped.append(work_banks.tile([P, P], BF16, tag="work2", name="x_flipped"))
            nc.tensor.transpose(x_flipped[0][:], x_raw[:], ident_b[:])

        def empty_x():
            nc.vector.tensor_copy(out=x_t[:], in_=x_flipped[0][:])

        def multiply_order1(n):
            pool, tag = (work_banks, "work%d" % n) if n < 3 else (o_banks, "o4")
            acc = pool.tile([P, BANK], F32, tag=tag, name="order1_ps%d" % n)
            cols = slice(BANK * n, BANK * (n + 1))
            nc.tensor.matmul(out=acc[:], lhsT=x_t[:], rhs=km_raw[:, cols], start=True, stop=False)
            nc.tensor.matmul(out=acc[:], lhsT=first_row[:], rhs=b1_row[:, cols], start=False, stop=True)
            order1_ps[n] = acc

        def by_parity(bank):
            return bank.rearrange("b (x e) -> b e x", e=2)

        def runs(tile, n):
            return tile[:, n].rearrange("b (e u) q -> b e (u q)", e=2)

        def empty_order1(n):
            if n < 3:
                nc.scalar.copy(out=runs(order1, n), in_=by_parity(order1_ps[n][:]))
            else:
                nc.scalar.copy(
                    out=order1[:, n].rearrange("b (u e) q -> b u e q", e=2),
                    in_=order1_ps[n][:].rearrange("b (u q e) -> b u e q", u=2, e=2),
                )

        def add_bank(n):
            nc.vector.scalar_tensor_tensor(
                out=runs(o_sb, n),
                in0=by_parity(o_ps[n][:]),
                scalar=1.0,
                in1=runs(order1, n),
                op0=ALU.mult,
                op1=ALU.add,
                accum_out=sums[:, n : n + 1],
            )

        def add_last(u):
            mine = slice(2 * u, 2 * u + 2)
            nc.vector.tensor_tensor(
                out=o_sb[:, 3, mine, :], in0=by_parity(o_ps[3 + u][:, 0 : BANK // 2]), in1=order1[:, 3, mine, :], op=ALU.add
            )

        def square_bank(n):
            nc.scalar.activation(out=z_sb[:, n], in_=o_sb[:, n], func=ACT.Square, accum_out=squares[:, n : n + 1])

        def means():
            nc.vector.tensor_scalar_mul(out=stats[:, 1:9:3], in0=sums[:], scalar1=1.0 / BANK)

        def mean_products():
            nc.vector.scalar_tensor_tensor(out=products[:], in0=sums[:], scalar=1.0 / BANK, in1=sums[:], op0=ALU.mult, op1=ALU.mult)

        def deviations():
            nc.vector.tensor_tensor(out=stats[:, 2:9:3], in0=squares[:], in1=products[:], op=ALU.subtract)

        def last_stats(u):
            nc.vector.bn_stats(
                out=stats[:, 9 + 6 * u : 15 + 6 * u],
                in_=o_sb[:, 3, 2 * u : 2 * u + 2, :].rearrange("b t q -> b (t q)"),
            )

        w_words = keep.tile([P, 2, 4, OUT // 2], U32, name="w_words", align_bytes=64)
        w_scales = keep.tile([P, 2, 4, OUT // 2], U8, name="w_scales", align_bytes=64)
        w_grouped = keep.tile([P, 2, 4, 2, P, 2], F32, name="w_grouped", align_bytes=64)
        w_flipped = {}

        def transpose_w(g, half):
            pool, tag = (work_banks, "work%d" % g) if g < 3 else (o_banks, "o1")
            flipped = pool.tile([P, 2, 2, P], F32, tag=tag, name="w_flipped%d%d" % (g, half))
            for r in range(2):
                pairs = w_raw[2 * half + r][:].bitcast(F32)
                for u in range(2):
                    first = 256 * g + P * u
                    nc.tensor.transpose(flipped[:, r, u, :], pairs[:, first : first + P], ident_f[:])
            w_flipped[g, half] = flipped

        def keep_clock(bank, passes):
            spare = o_banks.tile([P, BANK], F32, name="spare%d" % bank, tag="o%d" % bank)
            for i in range(passes):
                nc.tensor.matmul_mx(
                    out=spare[:],
                    lhsT=t_words[1][:, 0:P].bitcast(FP8X4),
                    lhsT_scale=t_scales[1][:, 0:P],
                    rhs=core_words[0][:].bitcast(FP8X4),
                    rhs_scale=core_scales[0][:],
                    start=True,
                    stop=True,
                )

        def empty_w(g, half):
            nc.scalar.copy(out=w_grouped[:, half, g], in_=w_flipped[g, half][:].rearrange("p r u n -> p r n u"))

        def empty_w_vector(g, half):
            nc.vector.tensor_copy(out=w_grouped[:, half, g], in_=w_flipped[g, half][:].rearrange("p r u n -> p r n u"))

        def quantise_w(half, lo, hi):
            nc.vector.quantize_mx(
                out=w_words[:, half, lo:hi].rearrange("p g n -> p (g n)").bitcast(FP8X4),
                scales=w_scales[:, half, lo:hi].rearrange("p g n -> p (g n)"),
                in_=w_grouped[:, half, lo:hi].rearrange("p g r n u -> p (g r n u)").bitcast(BF16),
            )

        mean_var = keep.tile([P, 2], F32, name="mean_var")
        rstd = keep.tile([P, 1], F32, name="rstd")
        vec_pairs = keep.tile([P, 16], F32, name="vec_pairs")
        vec_cols = keep.tile([P, 32], F32, name="vec_cols")
        y_planes = keep.tile([P, 4, PACK, P], BF16, name="y_planes")
        y_grouped = keep.tile([P, 4, P, PACK], BF16, name="y_grouped", align_bytes=64)
        y_words = keep.tile([P, 4 * P], U32, name="y_words", align_bytes=64)
        y_scales = keep.tile([P, 4 * P], U8, name="y_scales", align_bytes=64)
        z_flipped = {}
        vec_flipped = []

        def transpose_vectors():
            vec_flipped.append(work_banks.tile([P, P], F32, tag="work2", name="vec_flipped"))
            nc.tensor.transpose(vec_flipped[0][:], vec_rows[:], ident_f[:])

        def empty_vectors():
            nc.scalar.copy(out=vec_pairs[:], in_=vec_flipped[0][:, 0:16])

        def widen_vectors():
            nc.scalar.copy(out=vec_cols[:], in_=vec_pairs[:].bitcast(BF16))

        def aggregate():
            nc.vector.bn_aggr(out=mean_var[:], in_=stats[:])

        def inverse_deviation():
            nc.scalar.activation(
                out=rstd[:], in_=mean_var[:, 1:2], func=ACT.Abs_reciprocal_sqrt, bias=eps[:], scale=1.0
            )

        def normalise(g, lo=0, hi=PACK):
            nc.vector.tensor_scalar(
                out=z_sb[:, g, lo:hi],
                in0=o_sb[:, g, lo:hi],
                scalar1=mean_var[:, 0:1],
                scalar2=rstd[:],
                op0=ALU.subtract,
                op1=ALU.mult,
            )

        def transpose_z(g, bank, lo=0, hi=PACK):
            flipped = o_banks.tile([P, hi - lo, P], F32, name="z_flipped%d_%d" % (g, lo), tag="o%d" % bank)
            for t in range(lo, hi):
                nc.tensor.transpose(flipped[:, t - lo, :], z_sb[:, g, t, :], ident_f[:])
                z_flipped[g, t] = flipped[:, t - lo, :]

        def affine(g, halves=(0, 1)):
            for e in halves:
                for u in range(2):
                    k = PACK * g + 2 * u + e
                    nc.scalar.activation(
                        out=y_planes[:, g, 2 * u + e, :],
                        in_=z_flipped[g, 2 * e + u if g < 3 else 2 * u + e],
                        func=ACT.Identity,
                        bias=vec_cols[:, 16 + k : 17 + k],
                        scale=vec_cols[:, k : k + 1],
                    )

        def regroup_y(g):
            nc.vector.tensor_copy(
                out=y_grouped[:, g].rearrange("p (c i) t -> p c t i", i=RUN),
                in_=y_planes[:, g].rearrange("p t (c i) -> p c t i", i=RUN),
            )

        def quantise_y(lo, hi):
            nc.vector.quantize_mx(
                out=y_words[:, P * lo : P * hi].bitcast(FP8X4),
                scales=y_scales[:, P * lo : P * hi],
                in_=y_grouped[:, lo:hi].rearrange("p g b t -> p (g b t)"),
            )

        out_ps = {}
        result = keep.tile([P, OUT], F32, name="result")
        out_rows = out.rearrange("b o n -> b (o n)")

        def multiply_y(half, g):
            if g == 0:
                out_ps[half] = work_banks.tile([P, OUT // 2], F32, tag="work%d" % half, name="out_ps%d" % half)
            nc.tensor.matmul_mx(
                out=out_ps[half][:],
                lhsT=y_words[:, P * g : P * (g + 1)].bitcast(FP8X4),
                lhsT_scale=y_scales[:, P * g : P * (g + 1)],
                rhs=w_words[:, half, g].bitcast(FP8X4),
                rhs_scale=w_scales[:, half, g],
                start=(g == 0),
                stop=(g == 3),
            )

        def finish(half):
            cols = slice(OUT // 2 * half, OUT // 2 * (half + 1))
            nc.vector.tensor_tensor(out=result[:, cols], in0=out_ps[half][:], in1=fcb[:, cols], op=ALU.add)
            nc.sync.dma_start(out=out_rows[:, cols], in_=result[:, cols])

        ctx.enter_context(tc.manual_schedule())
        transpose_t(0)
        empty_t(0)
        quantise_t(0)
        regroup(0)
        regroup(1)
        quantise(0)
        multiply(0)
        regroup(2)
        quantise(1)
        multiply(1)
        transpose_t(1)
        transpose_x()
        regroup(3)
        quantise(2)
        multiply(2)
        empty_t(1)
        empty_x()
        quantise(3)
        quantise_t(1)
        regroup(4)
        multiply_order1(0)
        multiply_order1(1)
        multiply_order1(2)
        multiply_order1(3)
        multiply(3)
        empty_order1(0)
        empty_order1(1)
        empty_order1(2)
        quantise(4)
        multiply(4)
        regroup(5)
        add_bank(0)
        add_bank(1)
        empty_order1(3)
        regroup(6)
        quantise(5)
        multiply(5)
        regroup(7)
        quantise(6)
        multiply(6)
        regroup(8)
        transpose_vectors()
        quantise(7)
        multiply(7)
        regroup(9)
        transpose_w(0, 0)
        quantise(8)
        multiply(8)
        quantise(9, 0, 256)
        quantise(9, 256, 512)
        multiply(9, 0, 256)
        multiply(9, 256, 512)
        transpose_w(1, 0)
        empty_vectors()
        square_bank(0)
        empty_w(0, 0)
        widen_vectors()
        square_bank(1)
        transpose_w(2, 0)
        transpose_w(3, 0)
        transpose_w(0, 1)
        add_bank(2)
        keep_clock(0, 2)
        add_last(0)
        add_last(1)
        square_bank(2)
        empty_w(1, 0)
        means()
        mean_products()
        transpose_w(1, 1)
        empty_w(2, 0)
        last_stats(0)
        last_stats(1)
        deviations()
        aggregate()
        inverse_deviation()
        empty_w_vector(0, 1)
        empty_w(3, 0)
        normalise(0, 0, 2)
        transpose_z(0, 0, 0, 2)
        normalise(0, 2, 4)
        transpose_z(0, 2, 2, 4)
        empty_w(1, 1)
        normalise(1)
        transpose_z(1, 3)
        normalise(2)
        normalise(3)
        transpose_z(2, 4)
        affine(0, (0,))
        transpose_z(3, 0)
        transpose_w(2, 1)
        transpose_w(3, 1)
        quantise_w(0, 0, 2)
        affine(0, (1,))
        keep_clock(2, 2)
        quantise_w(0, 2, 4)
        affine(1)
        regroup_y(0)
        quantise_w(1, 0, 2)
        affine(2)
        affine(3)
        empty_w(2, 1)
        empty_w(3, 1)
        regroup_y(1)
        regroup_y(2)
        quantise_y(0, 2)
        regroup_y(3)
        quantise_y(2, 3)
        quantise_y(3, 4)
        quantise_w(1, 2, 3)
        multiply_y(0, 0)
        multiply_y(0, 1)
        multiply_y(1, 0)
        multiply_y(1, 1)
        multiply_y(0, 2)
        multiply_y(0, 3)
        quantise_w(1, 3, 4)
        finish(0)
        multiply_y(1, 2)
        multiply_y(1, 3)
        finish(1)
